import numpy as np
import ml_dtypes


def mxq(x, axis, fmt="e4m3"):
    dtype, down = {"e4m3": (ml_dtypes.float8_e4m3fn, 7), "e5m2": (ml_dtypes.float8_e5m2, 14)}[fmt]
    v = np.moveaxis(np.asarray(x, np.float32).astype(ml_dtypes.bfloat16).astype(np.float64), axis, -1)
    blocks = v.reshape(v.shape[:-1] + (-1, 32))
    amax = np.abs(blocks).max(-1, keepdims=True)
    byte = np.maximum(np.where(amax > 0, np.frexp(amax)[1] - 1 + 127, 0) - down, 1)
    scale = np.exp2(byte - 127.0)
    codes = (blocks / scale).astype(np.float32).astype(dtype).astype(np.float64)
    return np.moveaxis((codes * scale).reshape(v.shape), -1, axis)


WIDE = False


def mx_kscale(k):
    if not WIDE:
        return np.ones(k)
    levels = np.array([10, -10, 5, -5, 0])
    if k % 512:
        return np.exp2(np.random.permutation(np.resize(levels, k // 32))).repeat(32)
    a = np.empty((k // 512, 16))
    for p in range(k // 512):
        a[p, :8] = np.random.permutation(np.resize(levels, 8))
        for g in range(8):
            far = levels[np.abs(levels - a[p, g]) >= 10]
            a[p, g + 8] = far[np.random.randint(len(far))]
    return np.exp2(a.ravel()).repeat(32)


BF16 = ml_dtypes.bfloat16


def bf(x):
    return np.asarray(x, np.float32).astype(BF16)


def f64(x):
    return np.asarray(x).astype(np.float64)


B, T, C, NH, G, HS, K, WIN = 1, 1024, 1024, 16, 4, 128, 4, 512
QPK = NH // G


def silu(v):
    return v / (1.0 + np.exp(-v))


def causal_conv1d_silu(u, w):
    up = np.pad(u, ((0, 0), (K - 1, 0), (0, 0)))
    out = sum(w[None, None, :, j] * up[:, j:j + T, :] for j in range(K))
    return silu(out)


def apply_rope(u, cos, sin):
    d = cos.shape[-1]
    u1, u2 = u[..., :d], u[..., d:]
    c = cos[None, :, None, :]
    s = sin[None, :, None, :]
    return np.concatenate([u1 * c - u2 * s, u1 * s + u2 * c], axis=-1)


def draw0():
    s = mx_kscale(C)
    theta = 1.0 / (10000.0 ** (np.arange(0, HS, 2) / HS))
    idx = np.outer(np.arange(T), theta)
    return {"x": bf(np.random.standard_normal((B, T, C)) * s),
            "Wqkv": bf(np.random.standard_normal((C, (NH + 2 * G) * HS)) * 2.0 / np.sqrt(C) / s[:, None]),
            "q_conv_w": bf(np.random.standard_normal((NH * HS, K)) * 0.5),
            "k_conv_w": bf(np.random.standard_normal((G * HS, K)) * 0.5),
            "v_conv_w": bf(np.random.standard_normal((G * HS, K)) * 0.5),
            "cos": bf(np.cos(idx)), "sin": bf(np.sin(idx))}


def core(x, Wqkv, q_conv_w, k_conv_w, v_conv_w, cos, sin):
    qkv = (mxq(f64(x).reshape(B * T, C), 1, "e4m3") @ mxq(f64(Wqkv), 0, "e4m3")).reshape(B, T, G, QPK + 2, HS)
    q = qkv[..., :QPK, :].reshape(B, T, NH * HS)
    k = qkv[..., QPK:QPK + 1, :].reshape(B, T, G * HS)
    v = qkv[..., QPK + 1:, :].reshape(B, T, G * HS)
    q = causal_conv1d_silu(q, f64(q_conv_w)).reshape(B, T, NH, HS)
    k = causal_conv1d_silu(k, f64(k_conv_w)).reshape(B, T, G, HS)
    v = causal_conv1d_silu(v, f64(v_conv_w)).reshape(B, T, G, HS)
    q = apply_rope(q, f64(cos), f64(sin))
    k = apply_rope(k, f64(cos), f64(sin))
    return q, k, v


def e4m3fn_bytes(y):
    return np.clip(np.asarray(y, np.float64), -448.0, 448.0).astype(np.float32).astype(ml_dtypes.float8_e4m3fn).view(np.uint8)


def e4m3fn_values(b):
    return np.asarray(b, np.uint8).view(ml_dtypes.float8_e4m3fn).astype(np.float64)


def setup_inputs():
    d = draw0()
    x0 = np.asarray(d['Wqkv']).astype(np.float64)
    s = (np.max(np.abs(x0), axis=(1,), keepdims=True) / 448.0).astype(np.float32)
    out = {}
    for k, v in d.items():
        if k == 'Wqkv':
            out['Wqkv_bytes'] = e4m3fn_bytes(x0 / s.astype(np.float64))
            out['Wqkv_scale'] = s
        else:
            out[k] = v
    return out


def reference(x, Wqkv_bytes, Wqkv_scale, q_conv_w, k_conv_w, v_conv_w, cos, sin):
    return core(x, e4m3fn_values(Wqkv_bytes) * Wqkv_scale.astype(np.float64), q_conv_w, k_conv_w, v_conv_w, cos, sin)

@@ -1,0 +1,327 @@
+from contextlib import ExitStack
+
+import concourse.mybir as mybir
+from concourse.masks import make_identity
+
+F32 = mybir.dt.float32
+BF16 = mybir.dt.bfloat16
+U32 = mybir.dt.uint32
+U8 = mybir.dt.uint8
+FP8 = mybir.dt.float8_e4m3fn
+FP8X4 = mybir.dt.float8_e4m3fn_x4
+ACT = mybir.ActivationFunctionType
+ALU = mybir.AluOpType
+
+P = 128
+T = 1024
+C = 1024
+NCOL = 3072
+HS = 128
+TAPS = 4
+NHEADS = NCOL // HS
+PASSES = C // 512
+TT = T // P
+
+FLOPS = 2 * T * C * NCOL
+
+LOADS = [(0, 128), (128, 384), (512, 512), (1024, 512), (1536, 512), (2048, 512), (2560, 512)]
+UNITS = [(0, 128), (128, 128), (256, 256), (512, 512), (1024, 512), (1536, 512), (2048, 512), (2560, 512)]
+NSETS = 3
+S_TAP2_ROLES = (0, 2)
+
+
+def tile_gpt_pa_kernel(tc, x, Wqkv_bytes, Wqkv_scale, q_conv_w, k_conv_w, v_conv_w, cos, sin, out_0, out_1, out_2):
+    nc = tc.nc
+    with ExitStack() as ctx:
+        keep = ctx.enter_context(tc.tile_pool(name="keep", bufs=1))
+        wstage = ctx.enter_context(tc.tile_pool(name="wstage", bufs=3))
+        work = ctx.enter_context(tc.tile_pool(name="work", bufs=2))
+        outp = ctx.enter_context(tc.tile_pool(name="outp", bufs=3))
+        psum_p = ctx.enter_context(tc.psum_pool(name="psum_p", bufs=4))
+        psum_c = ctx.enter_context(tc.psum_pool(name="psum_c", bufs=4))
+        ctx.enter_context(tc.manual_schedule())
+
+        wbytes = []
+        for li, (c0, w) in enumerate(LOADS):
+            wbytes.append(keep.tile([P, PASSES, 4, w], U8, name="wbytes%d" % li, tag="wbytes%d" % li))
+        xraw = []
+        for tt in range(TT):
+            xraw.append(keep.tile([P, C], BF16, name="xraw%d" % tt, tag="xraw%d" % tt))
+        wscale = keep.tile([P, PASSES, 4], F32, name="wscale", tag="wscale")
+        qw = keep.tile([P, 16, TAPS], BF16, name="qw", tag="qw")
+        kw = keep.tile([P, 4, TAPS], BF16, name="kw", tag="kw")
+        vw = keep.tile([P, 4, TAPS], BF16, name="vw", tag="vw")
+        wf = keep.tile([P, NHEADS, TAPS], F32, name="wf", tag="wf")
+        cc = keep.tile([P, TT, HS], BF16, name="cc", tag="cc")
+        ss = keep.tile([P, TT, HS], BF16, name="ss", tag="ss")
+        ident = keep.tile([P, P], F32, name="ident", tag="ident")
+        warm = keep.tile([P, 1], F32, name="warm", tag="warm")
+        taps = []
+        for s in range(NSETS):
+            row = []
+            for j in range(TAPS):
+                row.append(keep.tile([P, T], F32, name="tap%d_%d" % (s, j), tag="tap%d_%d" % (s, j)))
+            taps.append(row)
+        xg = []
+        xc = []
+        xs = []
+        for hf in range(2):
+            xg.append(keep.tile([P, PASSES, 512, 4], BF16, name="xg%d" % hf, tag="xg%d" % hf, align_bytes=64))
+            xc.append(keep.tile([P, PASSES, 512], U32, name="xc%d" % hf, tag="xc%d" % hf, align_bytes=64))
+            xs.append(keep.tile([P, PASSES, 512], U8, name="xs%d" % hf, tag="xs%d" % hf, align_bytes=64))
+        wc = []
+        ws = []
+        for ui, (c0, w) in enumerate(UNITS):
+            wc.append(keep.tile([P, PASSES, w], U32, name="wc%d" % ui, tag="wc%d" % ui, align_bytes=64))
+            ws.append(keep.tile([P, PASSES, w], U8, name="ws%d" % ui, tag="ws%d" % ui, align_bytes=64))
+
+        w_view = Wqkv_bytes.rearrange("(g p t) n -> g p t n", p=P, t=4)
+        x_view = x.rearrange("b (tt p) k -> (b tt) p k", p=P)
+
+        def load_w(li):
+            c0, w = LOADS[li]
+            for g in range(PASSES):
+                nc.sync.dma_start(out=wbytes[li][:, g, :, :], in_=w_view[g][:, :, c0:c0 + w])
+
+        nc.sync.dma_start(out=wscale[:], in_=Wqkv_scale.rearrange("(g p t) o -> p g (t o)", p=P, t=4))
+        load_w(0)
+        for tt in range(4):
+            nc.sync.dma_start(out=xraw[tt][:], in_=x_view[tt])
+        load_w(1)
+        for tt in range(4, TT):
+            nc.sync.dma_start(out=xraw[tt][:], in_=x_view[tt])
+        for li in range(2, len(LOADS)):
+            load_w(li)
+
+        nc.vector.memset(warm[:], 0.0)
+        nc.gpsimd.dma_start(out=qw[:], in_=q_conv_w.rearrange("(h d) j -> d h j", d=P))
+        make_identity(nc, ident[:])
+        nc.gpsimd.dma_start(out=kw[:], in_=k_conv_w.rearrange("(h d) j -> d h j", d=P))
+        nc.gpsimd.dma_start(out=vw[:], in_=v_conv_w.rearrange("(h d) j -> d h j", d=P))
+        for s in range(NSETS):
+            for j in range(TAPS - 1):
+                nc.gpsimd.memset(taps[s][j][:, 0:8], 0.0)
+        wf_g = wf[:].rearrange("p (g r) j -> p g r j", r=6)
+        nc.gpsimd.tensor_copy(out=wf_g[:, :, 0:4, :], in_=qw[:].rearrange("p (g r) j -> p g r j", r=4))
+        nc.gpsimd.tensor_copy(out=wf_g[:, :, 4, :], in_=kw[:])
+        nc.gpsimd.tensor_copy(out=wf_g[:, :, 5, :], in_=vw[:])
+        nc.gpsimd.dma_start(out=cc[:, :, 0:64], in_=cos.rearrange("(tt p) i -> p tt i", p=P))
+        nc.gpsimd.dma_start(out=ss[:, :, 64:128], in_=sin.rearrange("(tt p) i -> p tt i", p=P))
+        nc.gpsimd.tensor_copy(out=cc[:, :, 64:128], in_=cc[:, :, 0:64])
+        nc.gpsimd.tensor_scalar(out=ss[:, :, 0:64], in0=ss[:, :, 64:128], scalar1=-1.0, scalar2=0.0, op0=ALU.mult, op1=ALU.add)
+
+        nc.scalar.activation(out=warm[:], in_=warm[:], func=ACT.Silu)
+
+        def x_turn(hf):
+            words_out = xg[hf][:].rearrange("p g t j -> p (g t j)").bitcast(F32).rearrange("p (g t u) -> p g t u", g=PASSES, u=2)
+            for q in range(4):
+                words = xraw[hf * 4 + q][:].bitcast(F32)
+                xt = psum_c.tile([P, PASSES, 2, P], F32, name="xt", tag="cbank")
+                for g in range(PASSES):
+                    for u in range(2):
+                        nc.tensor.transpose(xt[:, g, u, :], words[:, 256 * g + u:256 * (g + 1):2], ident[:])
+                dst = words_out[:, :, q * P:(q + 1) * P, :]
+                src = xt[:].rearrange("p g u r -> p g r u")
+                if q % 2 == 0:
+                    nc.vector.tensor_copy(out=dst, in_=src)
+                else:
+                    nc.scalar.copy(out=dst, in_=src)
+
+        def x_quant(hf):
+            for g in range(PASSES):
+                nc.vector.quantize_mx(
+                    out=xc[hf][:, g, :].bitcast(FP8X4),
+                    scales=xs[hf][:, g, :],
+                    in_=xg[hf][:, g, :, :].rearrange("p t j -> p (t j)"),
+                )
+
+        wplanes = {}
+        wgroup = {}
+
+        def w_widen(ui, g, planes):
+            c0, w = UNITS[ui]
+            li = max(i for i in range(len(LOADS)) if LOADS[i][0] <= c0)
+            off = c0 - LOADS[li][0]
+            if (ui, g) not in wplanes:
+                wplanes[(ui, g)] = wstage.tile([P, 4, w], BF16, name="wp", tag="wp")
+            for t in planes:
+                nc.scalar.activation(
+                    out=wplanes[(ui, g)][:, t, :],
+                    in_=wbytes[li][:, g, t, off:off + w].bitcast(FP8),
+                    func=ACT.Copy,
+                    scale=wscale[:, g, t:t + 1],
+                )
+
+        def w_interleave(ui, g):
+            w = UNITS[ui][1]
+            wgroup[(ui, g)] = wstage.tile([P, w, 4], BF16, name="wg", tag="wg", align_bytes=64)
+            nc.vector.tensor_copy(out=wgroup[(ui, g)][:], in_=wplanes[(ui, g)][:].rearrange("p t n -> p n t"))
+
+        def w_quant(ui, g):
+            nc.vector.quantize_mx(
+                out=wc[ui][:, g, :].bitcast(FP8X4),
+                scales=ws[ui][:, g, :],
+                in_=wgroup[(ui, g)][:].rearrange("p n t -> p (n t)"),
+            )
+
+        q_view = out_0.rearrange("b (tt p) h d -> p (b tt) h d", p=P)
+        k_view = out_1.rearrange("b (tt p) h d -> p (b tt) h d", p=P)
+        v_view = out_2.rearrange("b (tt p) h d -> p (b tt) h d", p=P)
+        accs = {}
+        us = {}
+        cvs = {}
+        sil = {}
+
+        def s_tap2(hw):
+            return (hw % 6) in S_TAP2_ROLES
+
+        def st_mx(hw):
+            ui = max(i for i in range(len(UNITS)) if UNITS[i][0] <= hw * HS)
+            off = hw * HS - UNITS[ui][0]
+            cols = slice(off, off + HS)
+            accs[hw] = []
+            for hf in range(2):
+                acc = psum_p.tile([P, 512], F32, name="acc", tag="pbank")
+                accs[hw].append(acc)
+                for g in range(PASSES):
+                    nc.tensor.matmul_mx(
+                        out=acc[:],
+                        lhsT=wc[ui][:, g, cols].bitcast(FP8X4),
+                        lhsT_scale=ws[ui][:, g, cols],
+                        rhs=xc[hf][:, g, :].bitcast(FP8X4),
+                        rhs_scale=xs[hf][:, g, :],
+                        start=(g == 0),
+                        stop=(g == PASSES - 1),
+                    )
+
+        def st_su(hw):
+            tp = taps[hw % NSETS]
+            us[hw] = work.tile([P, T], F32, name="u", tag="u")
+            for hf in range(2):
+                acc = accs[hw][hf]
+                nc.scalar.copy(out=us[hw][:, hf * 512:(hf + 1) * 512], in_=acc[:])
+                nc.scalar.activation(out=tp[3][:, hf * 512:(hf + 1) * 512], in_=acc[:], func=ACT.Copy, scale=wf[:, hw, 3:4])
+                if s_tap2(hw):
+                    lo = 1 + hf * 512
+                    hi = min(lo + 512, T)
+                    nc.scalar.activation(out=tp[2][:, lo:hi], in_=acc[:, 0:hi - lo], func=ACT.Copy, scale=wf[:, hw, 2:3])
+
+        def st_vp(hw):
+            tp = taps[hw % NSETS]
+            for j in range(2 if s_tap2(hw) else 3):
+                sh = TAPS - 1 - j
+                nc.vector.tensor_scalar(out=tp[j][:, sh:T], in0=us[hw][:, 0:T - sh], scalar1=wf[:, hw, j:j + 1], scalar2=None, op0=ALU.mult)
+
+        def st_tr(hw):
+            tp = taps[hw % NSETS]
+            cvs[hw] = []
+            for b in range(2):
+                cv = psum_c.tile([P, 4, HS], F32, name="cv", tag="cbank")
+                cvs[hw].append(cv)
+                for q in range(4):
+                    tt = b * 4 + q
+                    for j in range(TAPS):
+                        nc.tensor.matmul(
+                            out=cv[:, q, :],
+                            lhsT=tp[j][:, tt * P:(tt + 1) * P],
+                            rhs=ident[:],
+                            is_transpose=True,
+                            start=(j == 0),
+                            stop=(j == TAPS - 1),
+                        )
+
+        def st_ss(hw):
+            grp, r = divmod(hw, 6)
+            sil[hw] = outp.tile([P, TT, HS], F32, name="s", tag="s")
+            for b in range(2):
+                nc.scalar.activation(out=sil[hw][:, b * 4:(b + 1) * 4, :], in_=cvs[hw][b][:], func=ACT.Silu)
+            if r == 5:
+                nc.sync.dma_start(out=v_view[:, :, grp, :], in_=sil[hw][:])
+
+        def st_vr(hw):
+            grp, r = divmod(hw, 6)
+            if r == 5:
+                return
+            s = sil[hw]
+            o = outp.tile([P, TT, HS], F32, name="o", tag="o")
+            rot = work.tile([P, TT, HS], F32, name="rot", tag="rot")
+            nc.vector.tensor_tensor(out=o[:], in0=s[:], in1=cc[:], op=ALU.mult)
+            nc.vector.tensor_tensor(out=rot[:, :, 0:64], in0=s[:, :, 64:128], in1=ss[:, :, 0:64], op=ALU.mult)
+            nc.vector.tensor_tensor(out=rot[:, :, 64:128], in0=s[:, :, 0:64], in1=ss[:, :, 64:128], op=ALU.mult)
+            nc.vector.tensor_tensor(out=o[:], in0=o[:], in1=rot[:], op=ALU.add)
+            if r == 4:
+                nc.sync.dma_start(out=k_view[:, :, grp, :], in_=o[:])
+            else:
+                nc.sync.dma_start(out=q_view[:, :, grp * 4 + r, :], in_=o[:])
+
+        s_work = {}
+        v_pre = {}
+        v_mid = {}
+        v_post = {}
+
+        def put(table, slot, item):
+            table.setdefault(slot, []).append(item)
+
+        put(s_work, 0, (2, 0, (0, 1, 2, 3)))
+        put(s_work, 0, (2, 1, (0, 1, 2, 3)))
+        put(v_pre, 1, ("i", 2, 0))
+        put(v_pre, 1, ("i", 2, 1))
+        put(v_post, 1, ("q", 2, 0))
+        put(v_post, 1, ("q", 2, 1))
+        put(s_work, 1, (3, 0, (0, 1, 2, 3)))
+        put(s_work, 2, (3, 1, (0, 1, 2, 3)))
+        put(v_post, 2, ("i", 3, 0))
+        put(v_pre, 3, ("i", 3, 1))
+        put(v_mid, 3, ("q", 3, 0))
+        put(v_post, 3, ("q", 3, 1))
+        for ui in range(4, len(UNITS)):
+            h0 = UNITS[ui][0] // HS
+            put(s_work, h0 - 5, (ui, 0, (0, 1)))
+            put(s_work, h0 - 4, (ui, 0, (2, 3)))
+            put(s_work, h0 - 3, (ui, 1, (0, 1)))
+            put(s_work, h0 - 2, (ui, 1, (2, 3)))
+            put(v_post, h0 - 3, ("i", ui, 0))
+            put(v_mid, h0 - 2, ("q", ui, 0))
+            put(v_pre, h0 - 1, ("i", ui, 1))
+            put(v_post, h0 - 1, ("q", ui, 1))
+
+        def v_do(items):
+            for kind, ui, g in items:
+                if kind == "i":
+                    w_interleave(ui, g)
+                else:
+                    w_quant(ui, g)
+
+        for g in range(PASSES):
+            w_widen(0, g, (0, 1, 2, 3))
+        x_turn(0)
+        for g in range(PASSES):
+            w_interleave(0, g)
+        x_quant(0)
+        for g in range(PASSES):
+            w_quant(0, g)
+        for g in range(PASSES):
+            w_widen(1, g, (0, 1, 2, 3))
+        x_turn(1)
+        for g in range(PASSES):
+            w_interleave(1, g)
+        x_quant(1)
+        for g in range(PASSES):
+            w_quant(1, g)
+
+        for i in range(NHEADS + 3):
+            v_do(v_pre.get(i, []))
+            if i < NHEADS:
+                st_mx(i)
+                st_su(i)
+            for ui, g, planes in s_work.get(i, []):
+                w_widen(ui, g, planes)
+            if 0 <= i - 1 < NHEADS:
+                st_vp(i - 1)
+            v_do(v_mid.get(i, []))
+            if 0 <= i - 2 < NHEADS:
+                st_tr(i - 2)
+                st_ss(i - 2)
+            if 0 <= i - 3 < NHEADS:
+                st_vr(i - 3)
+            v_do(v_post.get(i, []))

@@ -122,10 +122,7 @@ def tile_gpt_pa_kernel(tc, x, Wqkv_bytes, Wqkv_scale, q_conv_w, k_conv_w, v_conv
                         nc.tensor.transpose(xt[:, g, u, :], words[:, 256 * g + u:256 * (g + 1):2], ident[:])
                 dst = words_out[:, :, q * P:(q + 1) * P, :]
                 src = xt[:].rearrange("p g u r -> p g r u")
-                if q % 2 == 0:
-                    nc.vector.tensor_copy(out=dst, in_=src)
-                else:
-                    nc.scalar.copy(out=dst, in_=src)
+                nc.scalar.copy(out=dst, in_=src)
 
         def x_quant(hf):
             for g in range(PASSES):
@@ -156,6 +153,20 @@ def tile_gpt_pa_kernel(tc, x, Wqkv_bytes, Wqkv_scale, q_conv_w, k_conv_w, v_conv
             w = UNITS[ui][1]
             wgroup[(ui, g)] = wstage.tile([P, w, 4], BF16, name="wg", tag="wg", align_bytes=64)
             nc.vector.tensor_copy(out=wgroup[(ui, g)][:], in_=wplanes[(ui, g)][:].rearrange("p t n -> p n t"))
+
+        def w_direct(ui, g):
+            c0, w = UNITS[ui]
+            li = max(i for i in range(len(LOADS)) if LOADS[i][0] <= c0)
+            off = c0 - LOADS[li][0]
+            wgroup[(ui, g)] = wstage.tile([P, w, 4], BF16, name="wg", tag="wg", align_bytes=64)
+            for t in range(4):
+                nc.vector.tensor_scalar(
+                    out=wgroup[(ui, g)][:, :, t],
+                    in0=wbytes[li][:, g, t, off:off + w].bitcast(FP8),
+                    scalar1=wscale[:, g, t:t + 1],
+                    scalar2=None,
+                    op0=ALU.mult,
+                )
 
         def w_quant(ui, g):
             nc.vector.quantize_mx(
@@ -196,7 +207,7 @@ def tile_gpt_pa_kernel(tc, x, Wqkv_bytes, Wqkv_scale, q_conv_w, k_conv_w, v_conv
 
         def st_su(hw):
             tp = taps[hw % NSETS]
-            us[hw] = work.tile([P, T], F32, name="u", tag="u")
+            us[hw] = work.tile([P, T], F32, name="u", tag="u", bufs=3)
             for hf in range(2):
                 acc = accs[hw][hf]
                 nc.scalar.copy(out=us[hw][:, hf * 512:(hf + 1) * 512], in_=acc[:])
@@ -238,16 +249,24 @@ def tile_gpt_pa_kernel(tc, x, Wqkv_bytes, Wqkv_scale, q_conv_w, k_conv_w, v_conv
             if r == 5:
                 nc.sync.dma_start(out=v_view[:, :, grp, :], in_=sil[hw][:])
 
-        def st_vr(hw):
-            grp, r = divmod(hw, 6)
-            if r == 5:
+        ropes = {}
+
+        def st_vr_products(hw):
+            if hw % 6 == 5:
                 return
             s = sil[hw]
             o = outp.tile([P, TT, HS], F32, name="o", tag="o")
             rot = work.tile([P, TT, HS], F32, name="rot", tag="rot")
+            ropes[hw] = (o, rot)
             nc.vector.tensor_tensor(out=o[:], in0=s[:], in1=cc[:], op=ALU.mult)
             nc.vector.tensor_tensor(out=rot[:, :, 0:64], in0=s[:, :, 64:128], in1=ss[:, :, 0:64], op=ALU.mult)
             nc.vector.tensor_tensor(out=rot[:, :, 64:128], in0=s[:, :, 0:64], in1=ss[:, :, 64:128], op=ALU.mult)
+
+        def st_vr_add(hw):
+            grp, r = divmod(hw, 6)
+            if r == 5:
+                return
+            o, rot = ropes[hw]
             nc.vector.tensor_tensor(out=o[:], in0=o[:], in1=rot[:], op=ALU.add)
             if r == 4:
                 nc.sync.dma_start(out=k_view[:, :, grp, :], in_=o[:])
@@ -262,20 +281,9 @@ def tile_gpt_pa_kernel(tc, x, Wqkv_bytes, Wqkv_scale, q_conv_w, k_conv_w, v_conv
         def put(table, slot, item):
             table.setdefault(slot, []).append(item)
 
-        put(s_work, 0, (2, 0, (0, 1, 2, 3)))
-        put(s_work, 0, (2, 1, (0, 1, 2, 3)))
-        put(v_pre, 1, ("i", 2, 0))
-        put(v_pre, 1, ("i", 2, 1))
-        put(v_post, 1, ("q", 2, 0))
-        put(v_post, 1, ("q", 2, 1))
-        put(s_work, 1, (3, 0, (0, 1, 2, 3)))
-        put(s_work, 2, (3, 1, (0, 1, 2, 3)))
-        put(v_post, 2, ("i", 3, 0))
-        put(v_pre, 3, ("i", 3, 1))
-        put(v_mid, 3, ("q", 3, 0))
-        put(v_post, 3, ("q", 3, 1))
+        LEAD = 1
         for ui in range(4, len(UNITS)):
-            h0 = UNITS[ui][0] // HS
+            h0 = UNITS[ui][0] // HS - LEAD
             put(s_work, h0 - 5, (ui, 0, (0, 1)))
             put(s_work, h0 - 4, (ui, 0, (2, 3)))
             put(s_work, h0 - 3, (ui, 1, (0, 1)))
@@ -284,6 +292,7 @@ def tile_gpt_pa_kernel(tc, x, Wqkv_bytes, Wqkv_scale, q_conv_w, k_conv_w, v_conv
             put(v_mid, h0 - 2, ("q", ui, 0))
             put(v_pre, h0 - 1, ("i", ui, 1))
             put(v_post, h0 - 1, ("q", ui, 1))
+        direct_at = {0: 2, 1: 3}
 
         def v_do(items):
             for kind, ui, g in items:
@@ -292,22 +301,22 @@ def tile_gpt_pa_kernel(tc, x, Wqkv_bytes, Wqkv_scale, q_conv_w, k_conv_w, v_conv
                 else:
                     w_quant(ui, g)
 
-        for g in range(PASSES):
-            w_widen(0, g, (0, 1, 2, 3))
+        def direct_unit(ui):
+            for g in range(PASSES):
+                w_direct(ui, g)
+
+        def quant_unit(ui):
+            for g in range(PASSES):
+                w_quant(ui, g)
+
+        direct_unit(0)
         x_turn(0)
-        for g in range(PASSES):
-            w_interleave(0, g)
+        quant_unit(0)
         x_quant(0)
-        for g in range(PASSES):
-            w_quant(0, g)
-        for g in range(PASSES):
-            w_widen(1, g, (0, 1, 2, 3))
+        direct_unit(1)
         x_turn(1)
-        for g in range(PASSES):
-            w_interleave(1, g)
+        quant_unit(1)
         x_quant(1)
-        for g in range(PASSES):
-            w_quant(1, g)
 
         for i in range(NHEADS + 3):
             v_do(v_pre.get(i, []))
@@ -316,6 +325,8 @@ def tile_gpt_pa_kernel(tc, x, Wqkv_bytes, Wqkv_scale, q_conv_w, k_conv_w, v_conv
                 st_su(i)
             for ui, g, planes in s_work.get(i, []):
                 w_widen(ui, g, planes)
+            if 0 <= i - 3 < NHEADS:
+                st_vr_products(i - 3)
             if 0 <= i - 1 < NHEADS:
                 st_vp(i - 1)
             v_do(v_mid.get(i, []))
@@ -323,5 +334,8 @@ def tile_gpt_pa_kernel(tc, x, Wqkv_bytes, Wqkv_scale, q_conv_w, k_conv_w, v_conv
                 st_tr(i - 2)
                 st_ss(i - 2)
             if 0 <= i - 3 < NHEADS:
-                st_vr(i - 3)
+                st_vr_add(i - 3)
+            if i in direct_at:
+                direct_unit(direct_at[i])
+                quant_unit(direct_at[i])
             v_do(v_post.get(i, []))

@@ -24,10 +24,14 @@ TT = T // P
 
 FLOPS = 2 * T * C * NCOL
 
-LOADS = [(0, 128), (128, 384), (512, 512), (1024, 512), (1536, 512), (2048, 512), (2560, 512)]
-UNITS = [(0, 128), (128, 128), (256, 256), (512, 512), (1024, 512), (1536, 512), (2048, 512), (2560, 512)]
+LOADS = [(0, 256), (256, 256), (512, 512), (1024, 512), (1536, 512), (2048, 512), (2560, 512)]
+SUB = 256
+NSUB = (NCOL // SUB) * PASSES
 NSETS = 3
-S_TAP2_ROLES = (0, 2)
+LEAD_Q = 3
+LEAD_I = 4
+LEAD_W = 5
+V_ADD_FROM = 22
 
 
 def tile_gpt_pa_kernel(tc, x, Wqkv_bytes, Wqkv_scale, q_conv_w, k_conv_w, v_conv_w, cos, sin, out_0, out_1, out_2):
@@ -35,10 +39,10 @@ def tile_gpt_pa_kernel(tc, x, Wqkv_bytes, Wqkv_scale, q_conv_w, k_conv_w, v_conv
     with ExitStack() as ctx:
         keep = ctx.enter_context(tc.tile_pool(name="keep", bufs=1))
         wstage = ctx.enter_context(tc.tile_pool(name="wstage", bufs=3))
-        work = ctx.enter_context(tc.tile_pool(name="work", bufs=2))
         outp = ctx.enter_context(tc.tile_pool(name="outp", bufs=3))
-        psum_p = ctx.enter_context(tc.psum_pool(name="psum_p", bufs=4))
-        psum_c = ctx.enter_context(tc.psum_pool(name="psum_c", bufs=4))
+        psum_t = ctx.enter_context(tc.psum_pool(name="psum_t", bufs=1))
+        psum_p = ctx.enter_context(tc.psum_pool(name="psum_p", bufs=3))
+        psum_c = ctx.enter_context(tc.psum_pool(name="psum_c", bufs=3))
         ctx.enter_context(tc.manual_schedule())
 
         wbytes = []
@@ -55,13 +59,13 @@ def tile_gpt_pa_kernel(tc, x, Wqkv_bytes, Wqkv_scale, q_conv_w, k_conv_w, v_conv
         cc = keep.tile([P, TT, HS], BF16, name="cc", tag="cc")
         ss = keep.tile([P, TT, HS], BF16, name="ss", tag="ss")
         ident = keep.tile([P, P], F32, name="ident", tag="ident")
+        identb = keep.tile([P, P], BF16, name="identb", tag="identb")
         warm = keep.tile([P, 1], F32, name="warm", tag="warm")
-        taps = []
+        pair_a = []
+        pair_b = []
         for s in range(NSETS):
-            row = []
-            for j in range(TAPS):
-                row.append(keep.tile([P, T], F32, name="tap%d_%d" % (s, j), tag="tap%d_%d" % (s, j)))
-            taps.append(row)
+            pair_a.append(keep.tile([P, T], F32, name="pair_a%d" % s, tag="pair_a%d" % s))
+            pair_b.append(keep.tile([P, T], F32, name="pair_b%d" % s, tag="pair_b%d" % s))
         xg = []
         xc = []
         xs = []
@@ -71,18 +75,25 @@ def tile_gpt_pa_kernel(tc, x, Wqkv_bytes, Wqkv_scale, q_conv_w, k_conv_w, v_conv
             xs.append(keep.tile([P, PASSES, 512], U8, name="xs%d" % hf, tag="xs%d" % hf, align_bytes=64))
         wc = []
         ws = []
-        for ui, (c0, w) in enumerate(UNITS):
-            wc.append(keep.tile([P, PASSES, w], U32, name="wc%d" % ui, tag="wc%d" % ui, align_bytes=64))
-            ws.append(keep.tile([P, PASSES, w], U8, name="ws%d" % ui, tag="ws%d" % ui, align_bytes=64))
+        for k in range(NSUB):
+            wc.append(keep.tile([P, SUB], U32, name="wc%d" % k, tag="wc%d" % k, align_bytes=64))
+            ws.append(keep.tile([P, SUB], U8, name="ws%d" % k, tag="ws%d" % k, align_bytes=64))
+        ccp = psum_t.tile([P, TT, HS], BF16, name="ccp", tag="ccp")
+        ssp = psum_t.tile([P, TT, HS], BF16, name="ssp", tag="ssp")
 
         w_view = Wqkv_bytes.rearrange("(g p t) n -> g p t n", p=P, t=4)
         x_view = x.rearrange("b (tt p) k -> (b tt) p k", p=P)
+        cos_v = cos.rearrange("(tt p) i -> p tt i", p=P)
+        sin_v = sin.rearrange("(tt p) i -> p tt i", p=P)
 
         def load_w(li):
             c0, w = LOADS[li]
             for g in range(PASSES):
                 nc.sync.dma_start(out=wbytes[li][:, g, :, :], in_=w_view[g][:, :, c0:c0 + w])
 
+        nc.scalar.dma_start(out=qw[:], in_=q_conv_w.rearrange("(h d) j -> d h j", d=P))
+        nc.scalar.dma_start(out=kw[:], in_=k_conv_w.rearrange("(h d) j -> d h j", d=P))
+        nc.scalar.dma_start(out=vw[:], in_=v_conv_w.rearrange("(h d) j -> d h j", d=P))
         nc.sync.dma_start(out=wscale[:], in_=Wqkv_scale.rearrange("(g p t) o -> p g (t o)", p=P, t=4))
         load_w(0)
         for tt in range(4):
@@ -90,29 +101,34 @@ def tile_gpt_pa_kernel(tc, x, Wqkv_bytes, Wqkv_scale, q_conv_w, k_conv_w, v_conv
         load_w(1)
         for tt in range(4, TT):
             nc.sync.dma_start(out=xraw[tt][:], in_=x_view[tt])
+        nc.sync.dma_start(out=cc[:, :, 0:64], in_=cos_v)
+        nc.sync.dma_start(out=cc[:, :, 64:128], in_=cos_v)
+        nc.sync.dma_start(out=ss[:, :, 64:128], in_=sin_v)
         for li in range(2, len(LOADS)):
             load_w(li)
 
         nc.vector.memset(warm[:], 0.0)
-        nc.gpsimd.dma_start(out=qw[:], in_=q_conv_w.rearrange("(h d) j -> d h j", d=P))
+        nc.scalar.activation(out=warm[:], in_=warm[:], func=ACT.Silu)
         make_identity(nc, ident[:])
-        nc.gpsimd.dma_start(out=kw[:], in_=k_conv_w.rearrange("(h d) j -> d h j", d=P))
-        nc.gpsimd.dma_start(out=vw[:], in_=v_conv_w.rearrange("(h d) j -> d h j", d=P))
         for s in range(NSETS):
-            for j in range(TAPS - 1):
-                nc.gpsimd.memset(taps[s][j][:, 0:8], 0.0)
+            nc.gpsimd.memset(pair_a[s][:, 0:8], 0.0)
         wf_g = wf[:].rearrange("p (g r) j -> p g r j", r=6)
         nc.gpsimd.tensor_copy(out=wf_g[:, :, 0:4, :], in_=qw[:].rearrange("p (g r) j -> p g r j", r=4))
         nc.gpsimd.tensor_copy(out=wf_g[:, :, 4, :], in_=kw[:])
         nc.gpsimd.tensor_copy(out=wf_g[:, :, 5, :], in_=vw[:])
-        nc.gpsimd.dma_start(out=cc[:, :, 0:64], in_=cos.rearrange("(tt p) i -> p tt i", p=P))
-        nc.gpsimd.dma_start(out=ss[:, :, 64:128], in_=sin.rearrange("(tt p) i -> p tt i", p=P))
-        nc.gpsimd.tensor_copy(out=cc[:, :, 64:128], in_=cc[:, :, 0:64])
-        nc.gpsimd.tensor_scalar(out=ss[:, :, 0:64], in0=ss[:, :, 64:128], scalar1=-1.0, scalar2=0.0, op0=ALU.mult, op1=ALU.add)
 
-        nc.scalar.activation(out=warm[:], in_=warm[:], func=ACT.Silu)
+        def tables_gpsimd():
+            make_identity(nc, identb[:])
+            nc.gpsimd.tensor_scalar(out=ss[:, :, 0:64], in0=ss[:, :, 64:128], scalar1=-1.0, scalar2=0.0, op0=ALU.mult, op1=ALU.add)
 
-        def x_turn(hf):
+        def tables_tensor():
+            for dst, src in ((ccp, cc), (ssp, ss)):
+                dst_flat = dst[:].rearrange("p t d -> p (t d)")
+                src_flat = src[:].rearrange("p t d -> p (t d)")
+                for b in range(2):
+                    nc.tensor.matmul(out=dst_flat[:, b * 512:(b + 1) * 512], lhsT=identb[:], rhs=src_flat[:, b * 512:(b + 1) * 512], start=True, stop=True)
+
+        def x_turn(hf, engines):
             words_out = xg[hf][:].rearrange("p g t j -> p (g t j)").bitcast(F32).rearrange("p (g t u) -> p g t u", g=PASSES, u=2)
             for q in range(4):
                 words = xraw[hf * 4 + q][:].bitcast(F32)
@@ -122,7 +138,10 @@ def tile_gpt_pa_kernel(tc, x, Wqkv_bytes, Wqkv_scale, q_conv_w, k_conv_w, v_conv
                         nc.tensor.transpose(xt[:, g, u, :], words[:, 256 * g + u:256 * (g + 1):2], ident[:])
                 dst = words_out[:, :, q * P:(q + 1) * P, :]
                 src = xt[:].rearrange("p g u r -> p g r u")
-                nc.scalar.copy(out=dst, in_=src)
+                if engines[q] == "V":
+                    nc.vector.tensor_copy(out=dst, in_=src)
+                else:
+                    nc.scalar.copy(out=dst, in_=src)
 
         def x_quant(hf):
             for g in range(PASSES):
@@ -135,111 +154,90 @@ def tile_gpt_pa_kernel(tc, x, Wqkv_bytes, Wqkv_scale, q_conv_w, k_conv_w, v_conv
         wplanes = {}
         wgroup = {}
 
-        def w_widen(ui, g, planes):
-            c0, w = UNITS[ui]
+        def w_widen(k):
+            if not 0 <= k < NSUB:
+                return
+            c0 = (k // 2) * SUB
+            g = k % 2
             li = max(i for i in range(len(LOADS)) if LOADS[i][0] <= c0)
             off = c0 - LOADS[li][0]
-            if (ui, g) not in wplanes:
-                wplanes[(ui, g)] = wstage.tile([P, 4, w], BF16, name="wp", tag="wp")
-            for t in planes:
+            wplanes[k] = wstage.tile([P, 4, SUB], BF16, name="wp", tag="wp")
+            for t in range(4):
                 nc.scalar.activation(
-                    out=wplanes[(ui, g)][:, t, :],
-                    in_=wbytes[li][:, g, t, off:off + w].bitcast(FP8),
+                    out=wplanes[k][:, t, :],
+                    in_=wbytes[li][:, g, t, off:off + SUB].bitcast(FP8),
                     func=ACT.Copy,
                     scale=wscale[:, g, t:t + 1],
                 )
 
-        def w_interleave(ui, g):
-            w = UNITS[ui][1]
-            wgroup[(ui, g)] = wstage.tile([P, w, 4], BF16, name="wg", tag="wg", align_bytes=64)
-            nc.vector.tensor_copy(out=wgroup[(ui, g)][:], in_=wplanes[(ui, g)][:].rearrange("p t n -> p n t"))
+        def w_interleave(k):
+            if not 0 <= k < NSUB:
+                return
+            wgroup[k] = wstage.tile([P, SUB, 4], BF16, name="wg", tag="wg", bufs=1, align_bytes=64)
+            nc.gpsimd.tensor_scalar(out=wgroup[k][:], in0=wplanes[k][:].rearrange("p t n -> p n t"), scalar1=1.0, scalar2=0.0, op0=ALU.mult, op1=ALU.add)
 
-        def w_direct(ui, g):
-            c0, w = UNITS[ui]
-            li = max(i for i in range(len(LOADS)) if LOADS[i][0] <= c0)
-            off = c0 - LOADS[li][0]
-            wgroup[(ui, g)] = wstage.tile([P, w, 4], BF16, name="wg", tag="wg", align_bytes=64)
-            for t in range(4):
-                nc.vector.tensor_scalar(
-                    out=wgroup[(ui, g)][:, :, t],
-                    in0=wbytes[li][:, g, t, off:off + w].bitcast(FP8),
-                    scalar1=wscale[:, g, t:t + 1],
-                    scalar2=None,
-                    op0=ALU.mult,
-                )
-
-        def w_quant(ui, g):
-            nc.vector.quantize_mx(
-                out=wc[ui][:, g, :].bitcast(FP8X4),
-                scales=ws[ui][:, g, :],
-                in_=wgroup[(ui, g)][:].rearrange("p n t -> p (n t)"),
-            )
+        def w_quant(k):
+            if not 0 <= k < NSUB:
+                return
+            nc.vector.quantize_mx(out=wc[k][:].bitcast(FP8X4), scales=ws[k][:], in_=wgroup[k][:].rearrange("p n t -> p (n t)"))
 
         q_view = out_0.rearrange("b (tt p) h d -> p (b tt) h d", p=P)
         k_view = out_1.rearrange("b (tt p) h d -> p (b tt) h d", p=P)
         v_view = out_2.rearrange("b (tt p) h d -> p (b tt) h d", p=P)
         accs = {}
-        us = {}
         cvs = {}
         sil = {}
-
-        def s_tap2(hw):
-            return (hw % 6) in S_TAP2_ROLES
+        ropes = {}
 
         def st_mx(hw):
-            ui = max(i for i in range(len(UNITS)) if UNITS[i][0] <= hw * HS)
-            off = hw * HS - UNITS[ui][0]
+            unit = (hw * HS) // SUB
+            off = hw * HS - unit * SUB
             cols = slice(off, off + HS)
             accs[hw] = []
             for hf in range(2):
                 acc = psum_p.tile([P, 512], F32, name="acc", tag="pbank")
                 accs[hw].append(acc)
                 for g in range(PASSES):
+                    k = unit * 2 + g
                     nc.tensor.matmul_mx(
                         out=acc[:],
-                        lhsT=wc[ui][:, g, cols].bitcast(FP8X4),
-                        lhsT_scale=ws[ui][:, g, cols],
+                        lhsT=wc[k][:, cols].bitcast(FP8X4),
+                        lhsT_scale=ws[k][:, cols],
                         rhs=xc[hf][:, g, :].bitcast(FP8X4),
                         rhs_scale=xs[hf][:, g, :],
                         start=(g == 0),
                         stop=(g == PASSES - 1),
                     )
 
-        def st_su(hw):
-            tp = taps[hw % NSETS]
-            us[hw] = work.tile([P, T], F32, name="u", tag="u", bufs=3)
+        def span(hf, shift):
+            lo = shift + hf * 512
+            return lo, min(lo + 512, T)
+
+        def st_s_taps(hw):
             for hf in range(2):
                 acc = accs[hw][hf]
-                nc.scalar.copy(out=us[hw][:, hf * 512:(hf + 1) * 512], in_=acc[:])
-                nc.scalar.activation(out=tp[3][:, hf * 512:(hf + 1) * 512], in_=acc[:], func=ACT.Copy, scale=wf[:, hw, 3:4])
-                if s_tap2(hw):
-                    lo = 1 + hf * 512
-                    hi = min(lo + 512, T)
-                    nc.scalar.activation(out=tp[2][:, lo:hi], in_=acc[:, 0:hi - lo], func=ACT.Copy, scale=wf[:, hw, 2:3])
+                for dst, j in ((pair_a[hw % NSETS], 1), (pair_b[hw % NSETS], 3)):
+                    lo, hi = span(hf, TAPS - 1 - j)
+                    nc.scalar.activation(out=dst[:, lo:hi], in_=acc[:, 0:hi - lo], func=ACT.Copy, scale=wf[:, hw, j:j + 1])
 
-        def st_vp(hw):
-            tp = taps[hw % NSETS]
-            for j in range(2 if s_tap2(hw) else 3):
-                sh = TAPS - 1 - j
-                nc.vector.tensor_scalar(out=tp[j][:, sh:T], in0=us[hw][:, 0:T - sh], scalar1=wf[:, hw, j:j + 1], scalar2=None, op0=ALU.mult)
+        def st_v_taps(hw):
+            for hf in range(2):
+                acc = accs[hw][hf]
+                for dst, j in ((pair_a[hw % NSETS], 0), (pair_b[hw % NSETS], 2)):
+                    lo, hi = span(hf, TAPS - 1 - j)
+                    nc.vector.scalar_tensor_tensor(
+                        out=dst[:, lo:hi], in0=acc[:, 0:hi - lo], scalar=wf[:, hw, j:j + 1], in1=dst[:, lo:hi], op0=ALU.mult, op1=ALU.add
+                    )
 
         def st_tr(hw):
-            tp = taps[hw % NSETS]
             cvs[hw] = []
             for b in range(2):
                 cv = psum_c.tile([P, 4, HS], F32, name="cv", tag="cbank")
                 cvs[hw].append(cv)
                 for q in range(4):
                     tt = b * 4 + q
-                    for j in range(TAPS):
-                        nc.tensor.matmul(
-                            out=cv[:, q, :],
-                            lhsT=tp[j][:, tt * P:(tt + 1) * P],
-                            rhs=ident[:],
-                            is_transpose=True,
-                            start=(j == 0),
-                            stop=(j == TAPS - 1),
-                        )
+                    nc.tensor.matmul(out=cv[:, q, :], lhsT=pair_a[hw % NSETS][:, tt * P:(tt + 1) * P], rhs=ident[:], is_transpose=True, start=True, stop=False)
+                    nc.tensor.matmul(out=cv[:, q, :], lhsT=pair_b[hw % NSETS][:, tt * P:(tt + 1) * P], rhs=ident[:], is_transpose=True, start=False, stop=True)
 
         def st_ss(hw):
             grp, r = divmod(hw, 6)
@@ -249,93 +247,67 @@ def tile_gpt_pa_kernel(tc, x, Wqkv_bytes, Wqkv_scale, q_conv_w, k_conv_w, v_conv
             if r == 5:
                 nc.sync.dma_start(out=v_view[:, :, grp, :], in_=sil[hw][:])
 
-        ropes = {}
-
-        def st_vr_products(hw):
+        def st_rope_products(hw):
             if hw % 6 == 5:
                 return
             s = sil[hw]
             o = outp.tile([P, TT, HS], F32, name="o", tag="o")
-            rot = work.tile([P, TT, HS], F32, name="rot", tag="rot")
+            rot = outp.tile([P, TT, HS], F32, name="rot", tag="rot")
             ropes[hw] = (o, rot)
-            nc.vector.tensor_tensor(out=o[:], in0=s[:], in1=cc[:], op=ALU.mult)
-            nc.vector.tensor_tensor(out=rot[:, :, 0:64], in0=s[:, :, 64:128], in1=ss[:, :, 0:64], op=ALU.mult)
-            nc.vector.tensor_tensor(out=rot[:, :, 64:128], in0=s[:, :, 0:64], in1=ss[:, :, 64:128], op=ALU.mult)
+            nc.vector.tensor_tensor(out=o[:], in0=s[:], in1=ccp[:], op=ALU.mult)
+            nc.vector.tensor_tensor(out=rot[:, :, 0:64], in0=s[:, :, 64:128], in1=ssp[:, :, 0:64], op=ALU.mult)
+            nc.vector.tensor_tensor(out=rot[:, :, 64:128], in0=s[:, :, 0:64], in1=ssp[:, :, 64:128], op=ALU.mult)
 
-        def st_vr_add(hw):
+        def st_rope_add(hw):
             grp, r = divmod(hw, 6)
             if r == 5:
                 return
             o, rot = ropes[hw]
-            nc.vector.tensor_tensor(out=o[:], in0=o[:], in1=rot[:], op=ALU.add)
-            if r == 4:
-                nc.sync.dma_start(out=k_view[:, :, grp, :], in_=o[:])
+            fin = outp.tile([P, TT, HS], F32, name="fin", tag="fin")
+            if hw >= V_ADD_FROM:
+                nc.vector.tensor_tensor(out=fin[:], in0=o[:], in1=rot[:], op=ALU.add)
             else:
-                nc.sync.dma_start(out=q_view[:, :, grp * 4 + r, :], in_=o[:])
+                nc.gpsimd.tensor_tensor(out=fin[:], in0=o[:], in1=rot[:], op=ALU.add)
+            if r == 4:
+                nc.sync.dma_start(out=k_view[:, :, grp, :], in_=fin[:])
+            else:
+                nc.sync.dma_start(out=q_view[:, :, grp * 4 + r, :], in_=fin[:])
 
-        s_work = {}
-        v_pre = {}
-        v_mid = {}
-        v_post = {}
-
-        def put(table, slot, item):
-            table.setdefault(slot, []).append(item)
-
-        LEAD = 1
-        for ui in range(4, len(UNITS)):
-            h0 = UNITS[ui][0] // HS - LEAD
-            put(s_work, h0 - 5, (ui, 0, (0, 1)))
-            put(s_work, h0 - 4, (ui, 0, (2, 3)))
-            put(s_work, h0 - 3, (ui, 1, (0, 1)))
-            put(s_work, h0 - 2, (ui, 1, (2, 3)))
-            put(v_post, h0 - 3, ("i", ui, 0))
-            put(v_mid, h0 - 2, ("q", ui, 0))
-            put(v_pre, h0 - 1, ("i", ui, 1))
-            put(v_post, h0 - 1, ("q", ui, 1))
-        direct_at = {0: 2, 1: 3}
-
-        def v_do(items):
-            for kind, ui, g in items:
-                if kind == "i":
-                    w_interleave(ui, g)
-                else:
-                    w_quant(ui, g)
-
-        def direct_unit(ui):
-            for g in range(PASSES):
-                w_direct(ui, g)
-
-        def quant_unit(ui):
-            for g in range(PASSES):
-                w_quant(ui, g)
-
-        direct_unit(0)
-        x_turn(0)
-        quant_unit(0)
+        w_widen(0)
+        w_widen(1)
+        x_turn(0, "VVVV")
+        w_interleave(0)
         x_quant(0)
-        direct_unit(1)
-        x_turn(1)
-        quant_unit(1)
+        w_quant(0)
+        w_interleave(1)
+        for k in range(2, LEAD_W - 1):
+            w_widen(k)
+        x_turn(1, "SVSV")
+        w_quant(1)
         x_quant(1)
+        for k in range(2, LEAD_I):
+            w_interleave(k)
+            if k < LEAD_Q:
+                w_quant(k)
+        tables_gpsimd()
 
-        for i in range(NHEADS + 3):
-            v_do(v_pre.get(i, []))
+        for i in range(NHEADS + 2):
             if i < NHEADS:
                 st_mx(i)
-                st_su(i)
-            for ui, g, planes in s_work.get(i, []):
-                w_widen(ui, g, planes)
-            if 0 <= i - 3 < NHEADS:
-                st_vr_products(i - 3)
-            if 0 <= i - 1 < NHEADS:
-                st_vp(i - 1)
-            v_do(v_mid.get(i, []))
+                st_s_taps(i)
+            if i == 2:
+                tables_tensor()
+            if i == 0:
+                w_widen(LEAD_W - 1)
+            w_widen(i + LEAD_W)
             if 0 <= i - 2 < NHEADS:
-                st_tr(i - 2)
-                st_ss(i - 2)
-            if 0 <= i - 3 < NHEADS:
-                st_vr_add(i - 3)
-            if i in direct_at:
-                direct_unit(direct_at[i])
-                quant_unit(direct_at[i])
-            v_do(v_post.get(i, []))
+                st_rope_products(i - 2)
+            if i < NHEADS:
+                st_v_taps(i)
+            if 0 <= i - 2 < NHEADS:
+                st_rope_add(i - 2)
+            w_quant(i + LEAD_Q)
+            w_interleave(i + LEAD_I)
+            if 0 <= i - 1 < NHEADS:
+                st_tr(i - 1)
+                st_ss(i - 1)

@@ -220,7 +220,7 @@ def tile_gpt_pa_kernel(tc, x, Wqkv_bytes, Wqkv_scale, q_conv_w, k_conv_w, v_conv
                     lo, hi = span(hf, TAPS - 1 - j)
                     nc.scalar.activation(out=dst[:, lo:hi], in_=acc[:, 0:hi - lo], func=ACT.Copy, scale=wf[:, hw, j:j + 1])
 
-        def st_v_taps(hw):
+        def st_v_taps(hw, between):
             for hf in range(2):
                 acc = accs[hw][hf]
                 for dst, j in ((pair_a[hw % NSETS], 0), (pair_b[hw % NSETS], 2)):
@@ -228,6 +228,8 @@ def tile_gpt_pa_kernel(tc, x, Wqkv_bytes, Wqkv_scale, q_conv_w, k_conv_w, v_conv
                     nc.vector.scalar_tensor_tensor(
                         out=dst[:, lo:hi], in0=acc[:, 0:hi - lo], scalar=wf[:, hw, j:j + 1], in1=dst[:, lo:hi], op0=ALU.mult, op1=ALU.add
                     )
+                if hf == 0:
+                    between()
 
         def st_tr(hw):
             cvs[hw] = []
@@ -247,14 +249,13 @@ def tile_gpt_pa_kernel(tc, x, Wqkv_bytes, Wqkv_scale, q_conv_w, k_conv_w, v_conv
             if r == 5:
                 nc.sync.dma_start(out=v_view[:, :, grp, :], in_=sil[hw][:])
 
-        def st_rope_products(hw):
-            if hw % 6 == 5:
-                return
+        def st_rope_products(hw, between):
             s = sil[hw]
             o = outp.tile([P, TT, HS], F32, name="o", tag="o")
             rot = outp.tile([P, TT, HS], F32, name="rot", tag="rot")
             ropes[hw] = (o, rot)
             nc.vector.tensor_tensor(out=o[:], in0=s[:], in1=ccp[:], op=ALU.mult)
+            between()
             nc.vector.tensor_tensor(out=rot[:, :, 0:64], in0=s[:, :, 64:128], in1=ssp[:, :, 0:64], op=ALU.mult)
             nc.vector.tensor_tensor(out=rot[:, :, 64:128], in0=s[:, :, 0:64], in1=ssp[:, :, 64:128], op=ALU.mult)
 
@@ -285,11 +286,14 @@ def tile_gpt_pa_kernel(tc, x, Wqkv_bytes, Wqkv_scale, q_conv_w, k_conv_w, v_conv
         x_turn(1, "SVSV")
         w_quant(1)
         x_quant(1)
-        for k in range(2, LEAD_I):
+        for k in range(2, LEAD_I - 1):
             w_interleave(k)
-            if k < LEAD_Q:
+            if k < LEAD_Q - 1:
                 w_quant(k)
         tables_gpsimd()
+
+        def nothing():
+            return None
 
         for i in range(NHEADS + 2):
             if i < NHEADS:
@@ -300,14 +304,19 @@ def tile_gpt_pa_kernel(tc, x, Wqkv_bytes, Wqkv_scale, q_conv_w, k_conv_w, v_conv
             if i == 0:
                 w_widen(LEAD_W - 1)
             w_widen(i + LEAD_W)
-            if 0 <= i - 2 < NHEADS:
-                st_rope_products(i - 2)
-            if i < NHEADS:
-                st_v_taps(i)
+
+            def w_step():
+                w_quant(i - 1 + LEAD_Q)
+                w_interleave(i - 1 + LEAD_I)
+
+            if 0 <= i - 2 < NHEADS and (i - 2) % 6 != 5:
+                st_rope_products(i - 2, w_step)
+                if i < NHEADS:
+                    st_v_taps(i, nothing)
+            elif i < NHEADS:
+                st_v_taps(i, w_step)
             if 0 <= i - 2 < NHEADS:
                 st_rope_add(i - 2)
-            w_quant(i + LEAD_Q)
-            w_interleave(i + LEAD_I)
             if 0 <= i - 1 < NHEADS:
                 st_tr(i - 1)
                 st_ss(i - 1)

@@ -17,6 +17,7 @@ T = 1024
 C = 1024
 NCOL = 3072
 HS = 128
+HALF = HS // 2
 TAPS = 4
 NHEADS = NCOL // HS
 PASSES = C // 512
@@ -32,17 +33,34 @@ LEAD_Q = 3
 LEAD_I = 4
 LEAD_W = 5
 V_ADD_FROM = 22
+ACC_BANKS = 4
+CV_BANKS = 3
+WP_BUFS = 3
+WG_BUFS = 1
+OUT_BUFS = 3
+LR = 2
+LA = 2
+DIAG = ()
+CHAIN = (0, 1)
+POOL_O = ()
+S3 = (21, 22, 23)
+PAD = TAPS - 1
+HEAD = 0
+X1ENG = "SVSV"
+X1A = (0, 1, 2, 3)
+X1B = ()
 
 
 def tile_gpt_pa_kernel(tc, x, Wqkv_bytes, Wqkv_scale, q_conv_w, k_conv_w, v_conv_w, cos, sin, out_0, out_1, out_2):
     nc = tc.nc
     with ExitStack() as ctx:
         keep = ctx.enter_context(tc.tile_pool(name="keep", bufs=1))
-        wstage = ctx.enter_context(tc.tile_pool(name="wstage", bufs=3))
-        outp = ctx.enter_context(tc.tile_pool(name="outp", bufs=3))
+        wstage = ctx.enter_context(tc.tile_pool(name="wstage", bufs=WP_BUFS))
+        outp = ctx.enter_context(tc.tile_pool(name="outp", bufs=OUT_BUFS))
         psum_t = ctx.enter_context(tc.psum_pool(name="psum_t", bufs=1))
-        psum_p = ctx.enter_context(tc.psum_pool(name="psum_p", bufs=3))
-        psum_c = ctx.enter_context(tc.psum_pool(name="psum_c", bufs=3))
+        psum_p = ctx.enter_context(tc.psum_pool(name="psum_p", bufs=ACC_BANKS))
+        psum_c = ctx.enter_context(tc.psum_pool(name="psum_c", bufs=CV_BANKS))
+        psum_b = ctx.enter_context(tc.psum_pool(name="psum_b", bufs=1)) if DIAG else None
         ctx.enter_context(tc.manual_schedule())
 
         wbytes = []
@@ -56,8 +74,7 @@ def tile_gpt_pa_kernel(tc, x, Wqkv_bytes, Wqkv_scale, q_conv_w, k_conv_w, v_conv
         kw = keep.tile([P, 4, TAPS], BF16, name="kw", tag="kw")
         vw = keep.tile([P, 4, TAPS], BF16, name="vw", tag="vw")
         wf = keep.tile([P, NHEADS, TAPS], F32, name="wf", tag="wf")
-        cc = keep.tile([P, TT, HS], BF16, name="cc", tag="cc")
-        ss = keep.tile([P, TT, HS], BF16, name="ss", tag="ss")
+        tabs = keep.tile([P, 2, TT, HALF], BF16, name="tabs", tag="tabs")
         ident = keep.tile([P, P], F32, name="ident", tag="ident")
         identb = keep.tile([P, P], BF16, name="identb", tag="identb")
         warm = keep.tile([P, 1], F32, name="warm", tag="warm")
@@ -66,6 +83,14 @@ def tile_gpt_pa_kernel(tc, x, Wqkv_bytes, Wqkv_scale, q_conv_w, k_conv_w, v_conv
         for s in range(NSETS):
             pair_a.append(keep.tile([P, T], F32, name="pair_a%d" % s, tag="pair_a%d" % s))
             pair_b.append(keep.tile([P, T], F32, name="pair_b%d" % s, tag="pair_b%d" % s))
+        pair_c = []
+        for s in range(NSETS if S3 else 0):
+            pair_c.append(keep.tile([P, T], F32, name="pair_c%d" % s, tag="pair_c%d" % s))
+        upad = {}
+        dmat = {}
+        for n, hw in enumerate(DIAG):
+            upad[hw] = keep.tile([P, PAD + T], F32, name="upad%d" % (n % 2), tag="upad%d" % (n % 2))
+            dmat[hw] = keep.tile([P, TAPS, P], F32, name="dmat%d" % n, tag="dmat%d" % n)
         xg = []
         xc = []
         xs = []
@@ -78,8 +103,7 @@ def tile_gpt_pa_kernel(tc, x, Wqkv_bytes, Wqkv_scale, q_conv_w, k_conv_w, v_conv
         for k in range(NSUB):
             wc.append(keep.tile([P, SUB], U32, name="wc%d" % k, tag="wc%d" % k, align_bytes=64))
             ws.append(keep.tile([P, SUB], U8, name="ws%d" % k, tag="ws%d" % k, align_bytes=64))
-        ccp = psum_t.tile([P, TT, HS], BF16, name="ccp", tag="ccp")
-        ssp = psum_t.tile([P, TT, HS], BF16, name="ssp", tag="ssp")
+        tab = psum_t.tile([P, 2, TT, HALF], BF16, name="tab", tag="tab")
 
         w_view = Wqkv_bytes.rearrange("(g p t) n -> g p t n", p=P, t=4)
         x_view = x.rearrange("b (tt p) k -> (b tt) p k", p=P)
@@ -101,9 +125,8 @@ def tile_gpt_pa_kernel(tc, x, Wqkv_bytes, Wqkv_scale, q_conv_w, k_conv_w, v_conv
         load_w(1)
         for tt in range(4, TT):
             nc.sync.dma_start(out=xraw[tt][:], in_=x_view[tt])
-        nc.sync.dma_start(out=cc[:, :, 0:64], in_=cos_v)
-        nc.sync.dma_start(out=cc[:, :, 64:128], in_=cos_v)
-        nc.sync.dma_start(out=ss[:, :, 64:128], in_=sin_v)
+        nc.sync.dma_start(out=tabs[:, 0, :, :], in_=cos_v)
+        nc.sync.dma_start(out=tabs[:, 1, :, :], in_=sin_v)
         for li in range(2, len(LOADS)):
             load_w(li)
 
@@ -112,6 +135,10 @@ def tile_gpt_pa_kernel(tc, x, Wqkv_bytes, Wqkv_scale, q_conv_w, k_conv_w, v_conv
         make_identity(nc, ident[:])
         for s in range(NSETS):
             nc.gpsimd.memset(pair_a[s][:, 0:8], 0.0)
+            if S3:
+                nc.gpsimd.memset(pair_c[s][:, 0:8], 0.0)
+        for hw in DIAG[0:2]:
+            nc.gpsimd.memset(upad[hw][:, 0:PAD], 0.0)
         wf_g = wf[:].rearrange("p (g r) j -> p g r j", r=6)
         nc.gpsimd.tensor_copy(out=wf_g[:, :, 0:4, :], in_=qw[:].rearrange("p (g r) j -> p g r j", r=4))
         nc.gpsimd.tensor_copy(out=wf_g[:, :, 4, :], in_=kw[:])
@@ -119,18 +146,20 @@ def tile_gpt_pa_kernel(tc, x, Wqkv_bytes, Wqkv_scale, q_conv_w, k_conv_w, v_conv
 
         def tables_gpsimd():
             make_identity(nc, identb[:])
-            nc.gpsimd.tensor_scalar(out=ss[:, :, 0:64], in0=ss[:, :, 64:128], scalar1=-1.0, scalar2=0.0, op0=ALU.mult, op1=ALU.add)
+
+        def diag_matrices(hw):
+            for j in range(TAPS):
+                nc.gpsimd.tensor_scalar(out=dmat[hw][:, j, :], in0=ident[:], scalar1=wf[:, hw, j:j + 1], scalar2=0.0, op0=ALU.mult, op1=ALU.add)
 
         def tables_tensor():
-            for dst, src in ((ccp, cc), (ssp, ss)):
-                dst_flat = dst[:].rearrange("p t d -> p (t d)")
-                src_flat = src[:].rearrange("p t d -> p (t d)")
-                for b in range(2):
-                    nc.tensor.matmul(out=dst_flat[:, b * 512:(b + 1) * 512], lhsT=identb[:], rhs=src_flat[:, b * 512:(b + 1) * 512], start=True, stop=True)
+            for b in range(2):
+                nc.tensor.matmul(
+                    out=tab[:, b, :, :].rearrange("p t i -> p (t i)"), lhsT=identb[:], rhs=tabs[:, b, :, :].rearrange("p t i -> p (t i)"), start=True, stop=True
+                )
 
-        def x_turn(hf, engines):
+        def x_turn(hf, engines, qs=(0, 1, 2, 3)):
             words_out = xg[hf][:].rearrange("p g t j -> p (g t j)").bitcast(F32).rearrange("p (g t u) -> p g t u", g=PASSES, u=2)
-            for q in range(4):
+            for q in qs:
                 words = xraw[hf * 4 + q][:].bitcast(F32)
                 xt = psum_c.tile([P, PASSES, 2, P], F32, name="xt", tag="cbank")
                 for g in range(PASSES):
@@ -173,7 +202,7 @@ def tile_gpt_pa_kernel(tc, x, Wqkv_bytes, Wqkv_scale, q_conv_w, k_conv_w, v_conv
         def w_interleave(k):
             if not 0 <= k < NSUB:
                 return
-            wgroup[k] = wstage.tile([P, SUB, 4], BF16, name="wg", tag="wg", bufs=1, align_bytes=64)
+            wgroup[k] = wstage.tile([P, SUB, 4], BF16, name="wg", tag="wg", bufs=WG_BUFS, align_bytes=64)
             nc.gpsimd.tensor_scalar(out=wgroup[k][:], in0=wplanes[k][:].rearrange("p t n -> p n t"), scalar1=1.0, scalar2=0.0, op0=ALU.mult, op1=ALU.add)
 
         def w_quant(k):
@@ -189,14 +218,13 @@ def tile_gpt_pa_kernel(tc, x, Wqkv_bytes, Wqkv_scale, q_conv_w, k_conv_w, v_conv
         sil = {}
         ropes = {}
 
-        def st_mx(hw):
+        def st_mx(hw, hfs=(0, 1)):
             unit = (hw * HS) // SUB
             off = hw * HS - unit * SUB
             cols = slice(off, off + HS)
-            accs[hw] = []
-            for hf in range(2):
+            for hf in hfs:
                 acc = psum_p.tile([P, 512], F32, name="acc", tag="pbank")
-                accs[hw].append(acc)
+                accs[(hw, hf)] = acc
                 for g in range(PASSES):
                     k = unit * 2 + g
                     nc.tensor.matmul_mx(
@@ -213,51 +241,99 @@ def tile_gpt_pa_kernel(tc, x, Wqkv_bytes, Wqkv_scale, q_conv_w, k_conv_w, v_conv
             lo = shift + hf * 512
             return lo, min(lo + 512, T)
 
-        def st_s_taps(hw):
-            for hf in range(2):
-                acc = accs[hw][hf]
-                for dst, j in ((pair_a[hw % NSETS], 1), (pair_b[hw % NSETS], 3)):
-                    lo, hi = span(hf, TAPS - 1 - j)
-                    nc.scalar.activation(out=dst[:, lo:hi], in_=acc[:, 0:hi - lo], func=ACT.Copy, scale=wf[:, hw, j:j + 1])
+        def s_product(hw, hf, dst, j):
+            lo, hi = span(hf, TAPS - 1 - j)
+            nc.scalar.activation(out=dst[:, lo:hi], in_=accs[(hw, hf)][:, 0:hi - lo], func=ACT.Copy, scale=wf[:, hw, j:j + 1])
 
-        def st_v_taps(hw, between):
-            for hf in range(2):
-                acc = accs[hw][hf]
-                for dst, j in ((pair_a[hw % NSETS], 0), (pair_b[hw % NSETS], 2)):
-                    lo, hi = span(hf, TAPS - 1 - j)
-                    nc.vector.scalar_tensor_tensor(
-                        out=dst[:, lo:hi], in0=acc[:, 0:hi - lo], scalar=wf[:, hw, j:j + 1], in1=dst[:, lo:hi], op0=ALU.mult, op1=ALU.add
-                    )
-                if hf == 0:
-                    between()
+        def v_madd(hw, hf, dst, j):
+            lo, hi = span(hf, TAPS - 1 - j)
+            nc.vector.scalar_tensor_tensor(
+                out=dst[:, lo:hi], in0=accs[(hw, hf)][:, 0:hi - lo], scalar=wf[:, hw, j:j + 1], in1=dst[:, lo:hi], op0=ALU.mult, op1=ALU.add
+            )
+
+        def st_s_taps(hw, hfs=(0, 1)):
+            a, b = pair_a[hw % NSETS], pair_b[hw % NSETS]
+            for hf in hfs:
+                if hw in DIAG:
+                    nc.scalar.copy(out=upad[hw][:, PAD + hf * 512:PAD + (hf + 1) * 512], in_=accs[(hw, hf)][:])
+                elif hw in CHAIN:
+                    s_product(hw, hf, b, 3)
+                else:
+                    s_product(hw, hf, a, 1)
+                    s_product(hw, hf, b, 3)
+                    if hw in S3:
+                        s_product(hw, hf, pair_c[hw % NSETS], 2)
+
+        def st_v_taps(hw, between, hfs=(0, 1)):
+            a, b = pair_a[hw % NSETS], pair_b[hw % NSETS]
+            if hw in DIAG:
+                between()
+            elif hw in CHAIN:
+                for j in (2, 1, 0):
+                    for hf in range(2):
+                        v_madd(hw, hf, b, j)
+                    if j == 2:
+                        between()
+            else:
+                for hf in hfs:
+                    v_madd(hw, hf, a, 0)
+                    if hw not in S3:
+                        v_madd(hw, hf, b, 2)
+                    if hf == 0:
+                        between()
 
         def st_tr(hw):
+            a, b = pair_a[hw % NSETS], pair_b[hw % NSETS]
             cvs[hw] = []
-            for b in range(2):
+            for bk in range(2):
                 cv = psum_c.tile([P, 4, HS], F32, name="cv", tag="cbank")
                 cvs[hw].append(cv)
                 for q in range(4):
-                    tt = b * 4 + q
-                    nc.tensor.matmul(out=cv[:, q, :], lhsT=pair_a[hw % NSETS][:, tt * P:(tt + 1) * P], rhs=ident[:], is_transpose=True, start=True, stop=False)
-                    nc.tensor.matmul(out=cv[:, q, :], lhsT=pair_b[hw % NSETS][:, tt * P:(tt + 1) * P], rhs=ident[:], is_transpose=True, start=False, stop=True)
+                    tt = bk * 4 + q
+                    if hw not in CHAIN:
+                        nc.tensor.matmul(out=cv[:, q, :], lhsT=a[:, tt * P:(tt + 1) * P], rhs=ident[:], is_transpose=True, start=True, stop=False)
+                    if hw in S3:
+                        nc.tensor.matmul(out=cv[:, q, :], lhsT=pair_c[hw % NSETS][:, tt * P:(tt + 1) * P], rhs=ident[:], is_transpose=True, start=False, stop=False)
+                    nc.tensor.matmul(out=cv[:, q, :], lhsT=b[:, tt * P:(tt + 1) * P], rhs=ident[:], is_transpose=True, start=(hw in CHAIN), stop=True)
 
-        def st_ss(hw):
+        def st_diag_tile(hw, tt):
+            bk, q = divmod(tt, 4)
+            if q == 0:
+                if bk == 0:
+                    cvs[hw] = []
+                cvs[hw].append(psum_b.tile([P, 4, HS], F32, name="bg", tag="bgbank"))
+            for j in range(TAPS):
+                nc.tensor.matmul(
+                    out=cvs[hw][bk][:, q, :], lhsT=upad[hw][:, tt * P + j:(tt + 1) * P + j], rhs=dmat[hw][:, j, :], start=(j == 0), stop=(j == TAPS - 1)
+                )
+
+        def st_ss_bank(hw, bk):
+            if bk == 0:
+                sil[hw] = outp.tile([P, TT, HS], F32, name="s", tag="s")
+            nc.scalar.activation(out=sil[hw][:, bk * 4:(bk + 1) * 4, :], in_=cvs[hw][bk][:], func=ACT.Silu)
             grp, r = divmod(hw, 6)
-            sil[hw] = outp.tile([P, TT, HS], F32, name="s", tag="s")
-            for b in range(2):
-                nc.scalar.activation(out=sil[hw][:, b * 4:(b + 1) * 4, :], in_=cvs[hw][b][:], func=ACT.Silu)
-            if r == 5:
+            if r == 5 and bk == 1:
                 nc.sync.dma_start(out=v_view[:, :, grp, :], in_=sil[hw][:])
+
+        def halves(t):
+            return t[:].rearrange("p t (h i) -> p t h i", h=2)
+
+        def both_halves(table):
+            return table.unsqueeze(2).to_broadcast([P, TT, 2, HALF])
 
         def st_rope_products(hw, between):
             s = sil[hw]
             o = outp.tile([P, TT, HS], F32, name="o", tag="o")
             rot = outp.tile([P, TT, HS], F32, name="rot", tag="rot")
             ropes[hw] = (o, rot)
-            nc.vector.tensor_tensor(out=o[:], in0=s[:], in1=ccp[:], op=ALU.mult)
-            between()
-            nc.vector.tensor_tensor(out=rot[:, :, 0:64], in0=s[:, :, 64:128], in1=ssp[:, :, 0:64], op=ALU.mult)
-            nc.vector.tensor_tensor(out=rot[:, :, 64:128], in0=s[:, :, 0:64], in1=ssp[:, :, 64:128], op=ALU.mult)
+            if hw in POOL_O:
+                nc.gpsimd.tensor_tensor(out=halves(o), in0=halves(s), in1=both_halves(tabs[:, 0, :, :]), op=ALU.mult)
+                nc.vector.tensor_tensor(out=halves(rot), in0=halves(s), in1=both_halves(tab[:, 1, :, :]), op=ALU.mult)
+                between()
+            else:
+                nc.vector.tensor_tensor(out=halves(o), in0=halves(s), in1=both_halves(tab[:, 0, :, :]), op=ALU.mult)
+                between()
+                nc.vector.tensor_tensor(out=halves(rot), in0=halves(s), in1=both_halves(tab[:, 1, :, :]), op=ALU.mult)
 
         def st_rope_add(hw):
             grp, r = divmod(hw, 6)
@@ -265,40 +341,72 @@ def tile_gpt_pa_kernel(tc, x, Wqkv_bytes, Wqkv_scale, q_conv_w, k_conv_w, v_conv
                 return
             o, rot = ropes[hw]
             fin = outp.tile([P, TT, HS], F32, name="fin", tag="fin")
-            if hw >= V_ADD_FROM:
-                nc.vector.tensor_tensor(out=fin[:], in0=o[:], in1=rot[:], op=ALU.add)
-            else:
-                nc.gpsimd.tensor_tensor(out=fin[:], in0=o[:], in1=rot[:], op=ALU.add)
+            eng = nc.vector if hw >= V_ADD_FROM else nc.gpsimd
+            eng.tensor_tensor(out=fin[:, :, 0:HALF], in0=o[:, :, 0:HALF], in1=rot[:, :, HALF:HS], op=ALU.subtract)
+            eng.tensor_tensor(out=fin[:, :, HALF:HS], in0=o[:, :, HALF:HS], in1=rot[:, :, 0:HALF], op=ALU.add)
             if r == 4:
                 nc.sync.dma_start(out=k_view[:, :, grp, :], in_=fin[:])
             else:
                 nc.sync.dma_start(out=q_view[:, :, grp * 4 + r, :], in_=fin[:])
 
-        w_widen(0)
-        w_widen(1)
-        x_turn(0, "VVVV")
-        w_interleave(0)
-        x_quant(0)
-        w_quant(0)
-        w_interleave(1)
-        for k in range(2, LEAD_W - 1):
-            w_widen(k)
-        x_turn(1, "SVSV")
-        w_quant(1)
-        x_quant(1)
-        for k in range(2, LEAD_I - 1):
-            w_interleave(k)
-            if k < LEAD_Q - 1:
-                w_quant(k)
-        tables_gpsimd()
-
         def nothing():
             return None
 
-        for i in range(NHEADS + 2):
-            if i < NHEADS:
+        if HEAD == 0:
+            w_widen(0)
+            w_widen(1)
+            x_turn(0, "VVVV")
+            w_interleave(0)
+            x_quant(0)
+            w_quant(0)
+            w_interleave(1)
+            for k in range(2, LEAD_W - 1):
+                w_widen(k)
+            x_turn(1, "SVSV")
+            w_quant(1)
+            x_quant(1)
+            for k in range(2, LEAD_I - 1):
+                w_interleave(k)
+                if k < LEAD_Q - 1:
+                    w_quant(k)
+            tables_gpsimd()
+        else:
+            w_widen(0)
+            w_widen(1)
+            x_turn(0, "VVVV")
+            w_interleave(0)
+            w_interleave(1)
+            x_quant(0)
+            w_quant(0)
+            w_quant(1)
+            for k in range(2, LEAD_W - 1):
+                w_widen(k)
+            x_turn(1, X1ENG, X1A)
+            st_mx(0, (0,))
+            st_mx(1, (0,))
+            x_turn(1, X1ENG, X1B)
+            st_s_taps(0, (0,))
+            st_s_taps(1, (0,))
+            for k in range(2, LEAD_I - 1):
+                w_interleave(k)
+            st_v_taps(0, nothing, (0,))
+            x_quant(1)
+            st_v_taps(1, nothing, (0,))
+            for k in range(2, LEAD_Q - 1):
+                w_quant(k)
+            tables_gpsimd()
+
+        for i in range(NHEADS + max(LR, LA) + 1):
+            if i < NHEADS and HEAD == 1 and i < 2:
+                st_mx(i, (1,))
+                st_s_taps(i, (1,))
+            elif i < NHEADS:
                 st_mx(i)
                 st_s_taps(i)
+            for hw in DIAG:
+                for tt in range(TT):
+                    if i == hw + 1 + (3 * tt) // 4:
+                        st_diag_tile(hw, tt)
             if i == 2:
                 tables_tensor()
             if i == 0:
@@ -309,14 +417,25 @@ def tile_gpt_pa_kernel(tc, x, Wqkv_bytes, Wqkv_scale, q_conv_w, k_conv_w, v_conv
                 w_quant(i - 1 + LEAD_Q)
                 w_interleave(i - 1 + LEAD_I)
 
-            if 0 <= i - 2 < NHEADS and (i - 2) % 6 != 5:
-                st_rope_products(i - 2, w_step)
+            if 0 <= i - LR < NHEADS and (i - LR) % 6 != 5:
+                st_rope_products(i - LR, w_step)
                 if i < NHEADS:
                     st_v_taps(i, nothing)
+            elif i < NHEADS and HEAD == 1 and i < 2:
+                w_step()
+                st_v_taps(i, nothing, (1,))
             elif i < NHEADS:
                 st_v_taps(i, w_step)
-            if 0 <= i - 2 < NHEADS:
-                st_rope_add(i - 2)
-            if 0 <= i - 1 < NHEADS:
+            if i + 2 in DIAG:
+                diag_matrices(i + 2)
+            if 0 <= i - LA < NHEADS:
+                st_rope_add(i - LA)
+            if 0 <= i - 1 < NHEADS and i - 1 not in DIAG:
                 st_tr(i - 1)
-                st_ss(i - 1)
+                st_ss_bank(i - 1, 0)
+                st_ss_bank(i - 1, 1)
+            for hw in DIAG:
+                if i == hw + 3:
+                    st_ss_bank(hw, 0)
+                if i == hw + 6:
+                    st_ss_bank(hw, 1)

@@ -29,14 +29,14 @@ LOADS = [(0, 256), (256, 256), (512, 512), (1024, 512), (1536, 512), (2048, 512)
 SUB = 256
 NSUB = (NCOL // SUB) * PASSES
 NSETS = 3
-LEAD_Q = 3
-LEAD_I = 4
-LEAD_W = 5
+LEAD_Q = 4
+LEAD_I = 5
+LEAD_W = 6
 V_ADD_FROM = 22
 ACC_BANKS = 4
 CV_BANKS = 3
 WP_BUFS = 3
-WG_BUFS = 1
+WG_BUFS = 2
 OUT_BUFS = 3
 LR = 2
 LA = 2
@@ -45,7 +45,11 @@ CHAIN = (0, 1)
 POOL_O = ()
 S3 = (21, 22, 23)
 PAD = TAPS - 1
-HEAD = 0
+HEAD = 2
+HW_A = 4
+QSIZES = (2,) * 12
+W_BEFORE_X = (0, 4)
+TAB_BEFORE_W = 2
 X1ENG = "SVSV"
 X1A = (0, 1, 2, 3)
 X1B = ()
@@ -100,9 +104,17 @@ def tile_gpt_pa_kernel(tc, x, Wqkv_bytes, Wqkv_scale, q_conv_w, k_conv_w, v_conv
             xs.append(keep.tile([P, PASSES, 512], U8, name="xs%d" % hf, tag="xs%d" % hf, align_bytes=64))
         wc = []
         ws = []
-        for k in range(NSUB):
-            wc.append(keep.tile([P, SUB], U32, name="wc%d" % k, tag="wc%d" % k, align_bytes=64))
-            ws.append(keep.tile([P, SUB], U8, name="ws%d" % k, tag="ws%d" % k, align_bytes=64))
+        place = {}
+        last_of = {}
+        k = 0
+        for gi, n in enumerate(QSIZES):
+            wc.append(keep.tile([P, n, SUB], U32, name="wc%d" % gi, tag="wc%d" % gi, align_bytes=64))
+            ws.append(keep.tile([P, n, SUB], U8, name="ws%d" % gi, tag="ws%d" % gi, align_bytes=64))
+            for pos in range(n):
+                place[k] = (gi, pos)
+                k += 1
+            last_of[k - 1] = gi
+        assert k == NSUB
         tab = psum_t.tile([P, 2, TT, HALF], BF16, name="tab", tag="tab")
 
         w_view = Wqkv_bytes.rearrange("(g p t) n -> g p t n", p=P, t=4)
@@ -119,15 +131,16 @@ def tile_gpt_pa_kernel(tc, x, Wqkv_bytes, Wqkv_scale, q_conv_w, k_conv_w, v_conv
         nc.scalar.dma_start(out=kw[:], in_=k_conv_w.rearrange("(h d) j -> d h j", d=P))
         nc.scalar.dma_start(out=vw[:], in_=v_conv_w.rearrange("(h d) j -> d h j", d=P))
         nc.sync.dma_start(out=wscale[:], in_=Wqkv_scale.rearrange("(g p t) o -> p g (t o)", p=P, t=4))
-        load_w(0)
-        for tt in range(4):
+        wl = 0
+        for tt in range(TT):
+            while wl < len(W_BEFORE_X) and W_BEFORE_X[wl] <= tt:
+                load_w(wl)
+                wl += 1
             nc.sync.dma_start(out=xraw[tt][:], in_=x_view[tt])
-        load_w(1)
-        for tt in range(4, TT):
-            nc.sync.dma_start(out=xraw[tt][:], in_=x_view[tt])
-        nc.sync.dma_start(out=tabs[:, 0, :, :], in_=cos_v)
-        nc.sync.dma_start(out=tabs[:, 1, :, :], in_=sin_v)
-        for li in range(2, len(LOADS)):
+        for li in range(wl, len(LOADS)):
+            if li == TAB_BEFORE_W:
+                nc.sync.dma_start(out=tabs[:, 0, :, :], in_=cos_v)
+                nc.sync.dma_start(out=tabs[:, 1, :, :], in_=sin_v)
             load_w(li)
 
         nc.vector.memset(warm[:], 0.0)
@@ -202,13 +215,20 @@ def tile_gpt_pa_kernel(tc, x, Wqkv_bytes, Wqkv_scale, q_conv_w, k_conv_w, v_conv
         def w_interleave(k):
             if not 0 <= k < NSUB:
                 return
-            wgroup[k] = wstage.tile([P, SUB, 4], BF16, name="wg", tag="wg", bufs=WG_BUFS, align_bytes=64)
-            nc.gpsimd.tensor_scalar(out=wgroup[k][:], in0=wplanes[k][:].rearrange("p t n -> p n t"), scalar1=1.0, scalar2=0.0, op0=ALU.mult, op1=ALU.add)
+            gi, pos = place[k]
+            if pos == 0:
+                wgroup[gi] = wstage.tile([P, QSIZES[gi], SUB, 4], BF16, name="wg", tag="wg", bufs=WG_BUFS, align_bytes=64)
+            nc.gpsimd.tensor_scalar(out=wgroup[gi][:, pos, :, :], in0=wplanes[k][:].rearrange("p t n -> p n t"), scalar1=1.0, scalar2=0.0, op0=ALU.mult, op1=ALU.add)
 
         def w_quant(k):
-            if not 0 <= k < NSUB:
+            if k not in last_of:
                 return
-            nc.vector.quantize_mx(out=wc[k][:].bitcast(FP8X4), scales=ws[k][:], in_=wgroup[k][:].rearrange("p n t -> p (n t)"))
+            gi = last_of[k]
+            nc.vector.quantize_mx(
+                out=wc[gi][:].rearrange("p s n -> p (s n)").bitcast(FP8X4),
+                scales=ws[gi][:].rearrange("p s n -> p (s n)"),
+                in_=wgroup[gi][:].rearrange("p s n t -> p (s n t)"),
+            )
 
         q_view = out_0.rearrange("b (tt p) h d -> p (b tt) h d", p=P)
         k_view = out_1.rearrange("b (tt p) h d -> p (b tt) h d", p=P)
@@ -226,11 +246,11 @@ def tile_gpt_pa_kernel(tc, x, Wqkv_bytes, Wqkv_scale, q_conv_w, k_conv_w, v_conv
                 acc = psum_p.tile([P, 512], F32, name="acc", tag="pbank")
                 accs[(hw, hf)] = acc
                 for g in range(PASSES):
-                    k = unit * 2 + g
+                    gi, pos = place[unit * 2 + g]
                     nc.tensor.matmul_mx(
                         out=acc[:],
-                        lhsT=wc[k][:, cols].bitcast(FP8X4),
-                        lhsT_scale=ws[k][:, cols],
+                        lhsT=wc[gi][:, pos, cols].bitcast(FP8X4),
+                        lhsT_scale=ws[gi][:, pos, cols],
                         rhs=xc[hf][:, g, :].bitcast(FP8X4),
                         rhs_scale=xs[hf][:, g, :],
                         start=(g == 0),
@@ -369,6 +389,30 @@ def tile_gpt_pa_kernel(tc, x, Wqkv_bytes, Wqkv_scale, q_conv_w, k_conv_w, v_conv
                 w_interleave(k)
                 if k < LEAD_Q - 1:
                     w_quant(k)
+            tables_gpsimd()
+        elif HEAD == 2:
+            w_widen(0)
+            w_widen(1)
+            x_turn(0, "VVVV")
+            w_interleave(0)
+            w_interleave(1)
+            x_quant(0)
+            w_quant(0)
+            w_quant(1)
+            for k in range(2, HW_A):
+                w_widen(k)
+            x_turn(1, X1ENG)
+            for k in range(HW_A, LEAD_W - 1):
+                w_widen(k)
+            w_interleave(2)
+            w_interleave(3)
+            x_quant(1)
+            w_quant(2)
+            w_quant(3)
+            for k in range(4, LEAD_I - 1):
+                w_interleave(k)
+            for k in range(4, LEAD_Q - 1):
+                w_quant(k)
             tables_gpsimd()
         else:
             w_widen(0)

@@ -36,7 +36,7 @@ V_ADD_FROM = 22
 ACC_BANKS = 4
 CV_BANKS = 3
 WP_BUFS = 3
-WG_BUFS = 2
+WG_BUFS = 1
 OUT_BUFS = 3
 LR = 2
 LA = 2
@@ -46,6 +46,12 @@ POOL_O = ()
 S3 = (21, 22, 23)
 PAD = TAPS - 1
 HEAD = 2
+BG_LATE = False
+BG_START = (6, 12, 18)
+BG_NUM = 3
+BG_DEN = 4
+BG_SS = 0
+WIDE = False
 HW_A = 4
 QSIZES = (2,) * 12
 W_BEFORE_X = (0, 4)
@@ -203,11 +209,18 @@ def tile_gpt_pa_kernel(tc, x, Wqkv_bytes, Wqkv_scale, q_conv_w, k_conv_w, v_conv
             g = k % 2
             li = max(i for i in range(len(LOADS)) if LOADS[i][0] <= c0)
             off = c0 - LOADS[li][0]
-            wplanes[k] = wstage.tile([P, 4, SUB], BF16, name="wp", tag="wp")
+            if WIDE:
+                if off != 0:
+                    wplanes[k] = wplanes[k - 2]
+                    return
+                width = LOADS[li][1]
+            else:
+                width = SUB
+            wplanes[k] = wstage.tile([P, 4, width], BF16, name="wp", tag="wp")
             for t in range(4):
                 nc.scalar.activation(
                     out=wplanes[k][:, t, :],
-                    in_=wbytes[li][:, g, t, off:off + SUB].bitcast(FP8),
+                    in_=wbytes[li][:, g, t, off:off + width].bitcast(FP8),
                     func=ACT.Copy,
                     scale=wscale[:, g, t:t + 1],
                 )
@@ -218,7 +231,11 @@ def tile_gpt_pa_kernel(tc, x, Wqkv_bytes, Wqkv_scale, q_conv_w, k_conv_w, v_conv
             gi, pos = place[k]
             if pos == 0:
                 wgroup[gi] = wstage.tile([P, QSIZES[gi], SUB, 4], BF16, name="wg", tag="wg", bufs=WG_BUFS, align_bytes=64)
-            nc.gpsimd.tensor_scalar(out=wgroup[gi][:, pos, :, :], in0=wplanes[k][:].rearrange("p t n -> p n t"), scalar1=1.0, scalar2=0.0, op0=ALU.mult, op1=ALU.add)
+            c0 = (k // 2) * SUB
+            off = (c0 - max(c for c, w in LOADS if c <= c0)) if WIDE else 0
+            nc.gpsimd.tensor_scalar(
+                out=wgroup[gi][:, pos, :, :], in0=wplanes[k][:, :, off:off + SUB].rearrange("p t n -> p n t"), scalar1=1.0, scalar2=0.0, op0=ALU.mult, op1=ALU.add
+            )
 
         def w_quant(k):
             if k not in last_of:
@@ -328,7 +345,9 @@ def tile_gpt_pa_kernel(tc, x, Wqkv_bytes, Wqkv_scale, q_conv_w, k_conv_w, v_conv
                 )
 
         def st_ss_bank(hw, bk):
-            if bk == 0:
+            if bk == 0 and hw in DIAG:
+                sil[hw] = outp.tile([P, TT, HS], F32, name="sbg", tag="sbg", bufs=1)
+            elif bk == 0:
                 sil[hw] = outp.tile([P, TT, HS], F32, name="s", tag="s")
             nc.scalar.activation(out=sil[hw][:, bk * 4:(bk + 1) * 4, :], in_=cvs[hw][bk][:], func=ACT.Silu)
             grp, r = divmod(hw, 6)
@@ -447,10 +466,11 @@ def tile_gpt_pa_kernel(tc, x, Wqkv_bytes, Wqkv_scale, q_conv_w, k_conv_w, v_conv
             elif i < NHEADS:
                 st_mx(i)
                 st_s_taps(i)
-            for hw in DIAG:
-                for tt in range(TT):
-                    if i == hw + 1 + (3 * tt) // 4:
-                        st_diag_tile(hw, tt)
+            if not BG_LATE:
+                for n, hw in enumerate(DIAG):
+                    for tt in range(TT):
+                        if i == BG_START[n] + (BG_NUM * tt) // BG_DEN:
+                            st_diag_tile(hw, tt)
             if i == 2:
                 tables_tensor()
             if i == 0:
@@ -478,8 +498,13 @@ def tile_gpt_pa_kernel(tc, x, Wqkv_bytes, Wqkv_scale, q_conv_w, k_conv_w, v_conv
                 st_tr(i - 1)
                 st_ss_bank(i - 1, 0)
                 st_ss_bank(i - 1, 1)
-            for hw in DIAG:
-                if i == hw + 3:
+            if BG_LATE:
+                for n, hw in enumerate(DIAG):
+                    for tt in range(TT):
+                        if i == BG_START[n] + (BG_NUM * tt) // BG_DEN:
+                            st_diag_tile(hw, tt)
+            for n, hw in enumerate(DIAG):
+                if i == BG_START[n] + (BG_NUM * 3) // BG_DEN + BG_SS:
                     st_ss_bank(hw, 0)
-                if i == hw + 6:
+                if i == BG_START[n] + (BG_NUM * 7) // BG_DEN + BG_SS:
                     st_ss_bank(hw, 1)

@@ -44,8 +44,18 @@ DIAG = ()
 CHAIN = (0, 1)
 POOL_O = ()
 S3 = (21, 22, 23)
+P2 = ()
 PAD = TAPS - 1
 HEAD = 2
+VW = ()
+TAIL = 2
+WIDE2 = False
+WB_LEAD = 7
+XQ_FIRST = True
+RA1 = False
+WG_OWN = 0
+DIAG_ON_V = False
+WI_MERGE = False
 BG_LATE = False
 BG_START = (6, 12, 18)
 BG_NUM = 3
@@ -96,6 +106,17 @@ def tile_gpt_pa_kernel(tc, x, Wqkv_bytes, Wqkv_scale, q_conv_w, k_conv_w, v_conv
         pair_c = []
         for s in range(NSETS if S3 else 0):
             pair_c.append(keep.tile([P, T], F32, name="pair_c%d" % s, tag="pair_c%d" % s))
+        p2t = []
+        for s in range(2 if P2 else 0):
+            p2t.append(
+                (
+                    keep.tile([P, PAD + T], F32, name="usb%d" % s, tag="usb%d" % s),
+                    keep.tile([P, PAD + T], F32, name="pp1%d" % s, tag="pp1%d" % s),
+                    keep.tile([P, PAD + T], F32, name="pp3%d" % s, tag="pp3%d" % s),
+                    keep.tile([P, T], F32, name="va%d" % s, tag="va%d" % s),
+                    keep.tile([P, T], F32, name="vb%d" % s, tag="vb%d" % s),
+                )
+            )
         upad = {}
         dmat = {}
         for n, hw in enumerate(DIAG):
@@ -122,6 +143,9 @@ def tile_gpt_pa_kernel(tc, x, Wqkv_bytes, Wqkv_scale, q_conv_w, k_conv_w, v_conv
             last_of[k - 1] = gi
         assert k == NSUB
         tab = psum_t.tile([P, 2, TT, HALF], BF16, name="tab", tag="tab")
+        if RA1:
+            sgn_s = keep.tile([P, TT, 2, HALF], BF16, name="sgn_s", tag="sgn_s")
+            sgn = psum_t.tile([P, TT, 2, HALF], BF16, name="sgn", tag="sgn")
 
         w_view = Wqkv_bytes.rearrange("(g p t) n -> g p t n", p=P, t=4)
         x_view = x.rearrange("b (tt p) k -> (b tt) p k", p=P)
@@ -156,6 +180,10 @@ def tile_gpt_pa_kernel(tc, x, Wqkv_bytes, Wqkv_scale, q_conv_w, k_conv_w, v_conv
             nc.gpsimd.memset(pair_a[s][:, 0:8], 0.0)
             if S3:
                 nc.gpsimd.memset(pair_c[s][:, 0:8], 0.0)
+        for tiles in p2t:
+            nc.gpsimd.memset(tiles[0][:, 0:PAD], 0.0)
+            nc.gpsimd.memset(tiles[3][:, 0:8], 0.0)
+            nc.gpsimd.memset(tiles[4][:, 0:8], 0.0)
         for hw in DIAG[0:2]:
             nc.gpsimd.memset(upad[hw][:, 0:PAD], 0.0)
         wf_g = wf[:].rearrange("p (g r) j -> p g r j", r=6)
@@ -165,16 +193,31 @@ def tile_gpt_pa_kernel(tc, x, Wqkv_bytes, Wqkv_scale, q_conv_w, k_conv_w, v_conv
 
         def tables_gpsimd():
             make_identity(nc, identb[:])
+            if RA1:
+                nc.gpsimd.tensor_scalar(out=sgn_s[:, :, 0, :], in0=tabs[:, 1, :, :], scalar1=-1.0, scalar2=0.0, op0=ALU.mult, op1=ALU.add)
+                nc.gpsimd.tensor_scalar(out=sgn_s[:, :, 1, :], in0=tabs[:, 1, :, :], scalar1=1.0, scalar2=0.0, op0=ALU.mult, op1=ALU.add)
 
         def diag_matrices(hw):
             for j in range(TAPS):
                 nc.gpsimd.tensor_scalar(out=dmat[hw][:, j, :], in0=ident[:], scalar1=wf[:, hw, j:j + 1], scalar2=0.0, op0=ALU.mult, op1=ALU.add)
+
+        if DIAG_ON_V:
+            for hw in DIAG:
+                nc.vector.tensor_tensor(
+                    out=dmat[hw][:], in0=ident[:].unsqueeze(1).to_broadcast([P, TAPS, P]), in1=wf[:, hw, :].unsqueeze(2).to_broadcast([P, TAPS, P]), op=ALU.mult
+                )
 
         def tables_tensor():
             for b in range(2):
                 nc.tensor.matmul(
                     out=tab[:, b, :, :].rearrange("p t i -> p (t i)"), lhsT=identb[:], rhs=tabs[:, b, :, :].rearrange("p t i -> p (t i)"), start=True, stop=True
                 )
+
+        def tables_tensor2():
+            flat_d = sgn[:].rearrange("p t h i -> p (t h i)")
+            flat_s = sgn_s[:].rearrange("p t h i -> p (t h i)")
+            for b in range(2):
+                nc.tensor.matmul(out=flat_d[:, b * 512:(b + 1) * 512], lhsT=identb[:], rhs=flat_s[:, b * 512:(b + 1) * 512], start=True, stop=True)
 
         def x_turn(hf, engines, qs=(0, 1, 2, 3)):
             words_out = xg[hf][:].rearrange("p g t j -> p (g t j)").bitcast(F32).rearrange("p (g t u) -> p g t u", g=PASSES, u=2)
@@ -200,10 +243,25 @@ def tile_gpt_pa_kernel(tc, x, Wqkv_bytes, Wqkv_scale, q_conv_w, k_conv_w, v_conv
                 )
 
         wplanes = {}
+        wpair = {}
         wgroup = {}
+
+        wblock = {}
+
+        def w_widen_block(slot):
+            for m in range(1, NCOL // 512):
+                for e in range(8):
+                    at = 4 * m - WB_LEAD + e // 2
+                    if at == slot or (slot is None and at < 0):
+                        g, t = divmod(e, 4)
+                        if e == 0:
+                            wblock[m] = wstage.tile([P, PASSES, 4, 512], BF16, name="wpb", tag="wpb", bufs=2)
+                        nc.scalar.activation(out=wblock[m][:, g, t, :], in_=wbytes[m + 1][:, g, t, :].bitcast(FP8), func=ACT.Copy, scale=wscale[:, g, t:t + 1])
 
         def w_widen(k):
             if not 0 <= k < NSUB:
+                return
+            if WIDE2 and k >= 4:
                 return
             c0 = (k // 2) * SUB
             g = k % 2
@@ -216,8 +274,16 @@ def tile_gpt_pa_kernel(tc, x, Wqkv_bytes, Wqkv_scale, q_conv_w, k_conv_w, v_conv
                 width = LOADS[li][1]
             else:
                 width = SUB
-            wplanes[k] = wstage.tile([P, 4, width], BF16, name="wp", tag="wp")
+            if WI_MERGE:
+                if g == 0:
+                    wpair[k // 2] = wstage.tile([P, PASSES, 4, SUB], BF16, name="wp", tag="wp")
+                wplanes[k] = wpair[k // 2][:, g, :, :]
+            else:
+                wplanes[k] = wstage.tile([P, 4, width], BF16, name="wp", tag="wp")[:]
             for t in range(4):
+                if k in VW:
+                    nc.vector.tensor_scalar(out=wplanes[k][:, t, :], in0=wbytes[li][:, g, t, off:off + width].bitcast(FP8), scalar1=wscale[:, g, t:t + 1], scalar2=None, op0=ALU.mult)
+                    continue
                 nc.scalar.activation(
                     out=wplanes[k][:, t, :],
                     in_=wbytes[li][:, g, t, off:off + width].bitcast(FP8),
@@ -229,12 +295,20 @@ def tile_gpt_pa_kernel(tc, x, Wqkv_bytes, Wqkv_scale, q_conv_w, k_conv_w, v_conv
             if not 0 <= k < NSUB:
                 return
             gi, pos = place[k]
-            if pos == 0:
+            if WI_MERGE:
+                if pos == 1:
+                    wgroup[gi] = wstage.tile([P, QSIZES[gi], SUB, 4], BF16, name="wg", tag="wg", bufs=WG_BUFS, align_bytes=64)
+                    nc.gpsimd.tensor_scalar(out=wgroup[gi][:], in0=wpair[k // 2][:].rearrange("p g t n -> p g n t"), scalar1=1.0, scalar2=0.0, op0=ALU.mult, op1=ALU.add)
+                return
+            if pos == 0 and gi < WG_OWN:
+                wgroup[gi] = wstage.tile([P, QSIZES[gi], SUB, 4], BF16, name="wgo%d" % gi, tag="wgo%d" % gi, bufs=1, align_bytes=64)
+            elif pos == 0:
                 wgroup[gi] = wstage.tile([P, QSIZES[gi], SUB, 4], BF16, name="wg", tag="wg", bufs=WG_BUFS, align_bytes=64)
             c0 = (k // 2) * SUB
-            off = (c0 - max(c for c, w in LOADS if c <= c0)) if WIDE else 0
+            off = (c0 - max(c for c, w in LOADS if c <= c0)) if (WIDE or WIDE2) else 0
+            planes = wblock[k // 4][:, k % 2, :, :] if (WIDE2 and k >= 4) else wplanes[k]
             nc.gpsimd.tensor_scalar(
-                out=wgroup[gi][:, pos, :, :], in0=wplanes[k][:, :, off:off + SUB].rearrange("p t n -> p n t"), scalar1=1.0, scalar2=0.0, op0=ALU.mult, op1=ALU.add
+                out=wgroup[gi][:, pos, :, :], in0=planes[:, :, off:off + SUB].rearrange("p t n -> p n t"), scalar1=1.0, scalar2=0.0, op0=ALU.mult, op1=ALU.add
             )
 
         def w_quant(k):
@@ -291,7 +365,9 @@ def tile_gpt_pa_kernel(tc, x, Wqkv_bytes, Wqkv_scale, q_conv_w, k_conv_w, v_conv
         def st_s_taps(hw, hfs=(0, 1)):
             a, b = pair_a[hw % NSETS], pair_b[hw % NSETS]
             for hf in hfs:
-                if hw in DIAG:
+                if hw in P2:
+                    nc.scalar.copy(out=p2t[P2.index(hw) % 2][0][:, PAD + hf * 512:PAD + (hf + 1) * 512], in_=accs[(hw, hf)][:])
+                elif hw in DIAG:
                     nc.scalar.copy(out=upad[hw][:, PAD + hf * 512:PAD + (hf + 1) * 512], in_=accs[(hw, hf)][:])
                 elif hw in CHAIN:
                     s_product(hw, hf, b, 3)
@@ -303,11 +379,19 @@ def tile_gpt_pa_kernel(tc, x, Wqkv_bytes, Wqkv_scale, q_conv_w, k_conv_w, v_conv
 
         def st_v_taps(hw, between, hfs=(0, 1)):
             a, b = pair_a[hw % NSETS], pair_b[hw % NSETS]
-            if hw in DIAG:
+            if hw in P2:
+                tiles = p2t[P2.index(hw) % 2]
+                for hf in hfs:
+                    for dst, j in ((tiles[3], 0), (tiles[4], 2)):
+                        lo, hi = span(hf, TAPS - 1 - j)
+                        nc.vector.tensor_scalar(out=dst[:, lo:hi], in0=accs[(hw, hf)][:, 0:hi - lo], scalar1=wf[:, hw, j:j + 1], scalar2=None, op0=ALU.mult)
+                    if hf == 0:
+                        between()
+            elif hw in DIAG:
                 between()
             elif hw in CHAIN:
                 for j in (2, 1, 0):
-                    for hf in range(2):
+                    for hf in hfs:
                         v_madd(hw, hf, b, j)
                     if j == 2:
                         between()
@@ -319,6 +403,11 @@ def tile_gpt_pa_kernel(tc, x, Wqkv_bytes, Wqkv_scale, q_conv_w, k_conv_w, v_conv
                     if hf == 0:
                         between()
 
+        def st_g_taps(hw):
+            tiles = p2t[P2.index(hw) % 2]
+            for dst, j in ((tiles[1], 1), (tiles[2], 3)):
+                nc.gpsimd.tensor_scalar(out=dst[:], in0=tiles[0][:], scalar1=wf[:, hw, j:j + 1], scalar2=0.0, op0=ALU.mult, op1=ALU.add)
+
         def st_tr(hw):
             a, b = pair_a[hw % NSETS], pair_b[hw % NSETS]
             cvs[hw] = []
@@ -327,6 +416,11 @@ def tile_gpt_pa_kernel(tc, x, Wqkv_bytes, Wqkv_scale, q_conv_w, k_conv_w, v_conv
                 cvs[hw].append(cv)
                 for q in range(4):
                     tt = bk * 4 + q
+                    if hw in P2:
+                        tiles = p2t[P2.index(hw) % 2]
+                        for n, (src, sh) in enumerate(((tiles[3], 0), (tiles[4], 0), (tiles[1], 1), (tiles[2], 3))):
+                            nc.tensor.matmul(out=cv[:, q, :], lhsT=src[:, tt * P + sh:(tt + 1) * P + sh], rhs=ident[:], is_transpose=True, start=(n == 0), stop=(n == 3))
+                        continue
                     if hw not in CHAIN:
                         nc.tensor.matmul(out=cv[:, q, :], lhsT=a[:, tt * P:(tt + 1) * P], rhs=ident[:], is_transpose=True, start=True, stop=False)
                     if hw in S3:
@@ -351,7 +445,9 @@ def tile_gpt_pa_kernel(tc, x, Wqkv_bytes, Wqkv_scale, q_conv_w, k_conv_w, v_conv
                 sil[hw] = outp.tile([P, TT, HS], F32, name="s", tag="s")
             nc.scalar.activation(out=sil[hw][:, bk * 4:(bk + 1) * 4, :], in_=cvs[hw][bk][:], func=ACT.Silu)
             grp, r = divmod(hw, 6)
-            if r == 5 and bk == 1:
+            if r == 5 and TAIL >= 2 and hw == NHEADS - 1:
+                nc.sync.dma_start(out=v_view[:, bk * 4:(bk + 1) * 4, grp, :], in_=sil[hw][:, bk * 4:(bk + 1) * 4, :])
+            elif r == 5 and bk == 1:
                 nc.sync.dma_start(out=v_view[:, :, grp, :], in_=sil[hw][:])
 
         def halves(t):
@@ -365,6 +461,20 @@ def tile_gpt_pa_kernel(tc, x, Wqkv_bytes, Wqkv_scale, q_conv_w, k_conv_w, v_conv
             o = outp.tile([P, TT, HS], F32, name="o", tag="o")
             rot = outp.tile([P, TT, HS], F32, name="rot", tag="rot")
             ropes[hw] = (o, rot)
+            if TAIL >= 4 and hw >= V_ADD_FROM:
+                grp = hw // 6
+                fin = outp.tile([P, TT, HS], F32, name="fin", tag="fin")
+                for b in range(2):
+                    tsl = slice(b * 4, (b + 1) * 4)
+                    for dst, k in ((o, 0), (rot, 1)):
+                        nc.vector.tensor_tensor(
+                            out=halves(dst)[:, tsl, :, :], in0=halves(s)[:, tsl, :, :], in1=tab[:, k, tsl, :].unsqueeze(2).to_broadcast([P, 4, 2, HALF]), op=ALU.mult
+                        )
+                    nc.vector.tensor_tensor(out=fin[:, tsl, 0:HALF], in0=o[:, tsl, 0:HALF], in1=rot[:, tsl, HALF:HS], op=ALU.subtract)
+                    nc.vector.tensor_tensor(out=fin[:, tsl, HALF:HS], in0=o[:, tsl, HALF:HS], in1=rot[:, tsl, 0:HALF], op=ALU.add)
+                    nc.sync.dma_start(out=k_view[:, tsl, grp, :], in_=fin[:, tsl, :])
+                between()
+                return
             if hw in POOL_O:
                 nc.gpsimd.tensor_tensor(out=halves(o), in0=halves(s), in1=both_halves(tabs[:, 0, :, :]), op=ALU.mult)
                 nc.vector.tensor_tensor(out=halves(rot), in0=halves(s), in1=both_halves(tab[:, 1, :, :]), op=ALU.mult)
@@ -372,17 +482,32 @@ def tile_gpt_pa_kernel(tc, x, Wqkv_bytes, Wqkv_scale, q_conv_w, k_conv_w, v_conv
             else:
                 nc.vector.tensor_tensor(out=halves(o), in0=halves(s), in1=both_halves(tab[:, 0, :, :]), op=ALU.mult)
                 between()
-                nc.vector.tensor_tensor(out=halves(rot), in0=halves(s), in1=both_halves(tab[:, 1, :, :]), op=ALU.mult)
+                if RA1:
+                    nc.vector.tensor_tensor(out=halves(rot), in0=halves(s)[:, :, ::-1, :], in1=sgn[:], op=ALU.mult)
+                else:
+                    nc.vector.tensor_tensor(out=halves(rot), in0=halves(s), in1=both_halves(tab[:, 1, :, :]), op=ALU.mult)
 
         def st_rope_add(hw):
             grp, r = divmod(hw, 6)
             if r == 5:
                 return
+            if TAIL >= 4 and hw >= V_ADD_FROM:
+                return
             o, rot = ropes[hw]
             fin = outp.tile([P, TT, HS], F32, name="fin", tag="fin")
             eng = nc.vector if hw >= V_ADD_FROM else nc.gpsimd
-            eng.tensor_tensor(out=fin[:, :, 0:HALF], in0=o[:, :, 0:HALF], in1=rot[:, :, HALF:HS], op=ALU.subtract)
-            eng.tensor_tensor(out=fin[:, :, HALF:HS], in0=o[:, :, HALF:HS], in1=rot[:, :, 0:HALF], op=ALU.add)
+            if TAIL >= 3 and hw >= V_ADD_FROM:
+                for b in range(2):
+                    tsl = slice(b * 4, (b + 1) * 4)
+                    eng.tensor_tensor(out=fin[:, tsl, 0:HALF], in0=o[:, tsl, 0:HALF], in1=rot[:, tsl, HALF:HS], op=ALU.subtract)
+                    eng.tensor_tensor(out=fin[:, tsl, HALF:HS], in0=o[:, tsl, HALF:HS], in1=rot[:, tsl, 0:HALF], op=ALU.add)
+                    nc.sync.dma_start(out=k_view[:, tsl, grp, :], in_=fin[:, tsl, :])
+                return
+            if RA1:
+                eng.tensor_tensor(out=fin[:], in0=o[:], in1=rot[:], op=ALU.add)
+            else:
+                eng.tensor_tensor(out=fin[:, :, 0:HALF], in0=o[:, :, 0:HALF], in1=rot[:, :, HALF:HS], op=ALU.subtract)
+                eng.tensor_tensor(out=fin[:, :, HALF:HS], in0=o[:, :, HALF:HS], in1=rot[:, :, 0:HALF], op=ALU.add)
             if r == 4:
                 nc.sync.dma_start(out=k_view[:, :, grp, :], in_=fin[:])
             else:
@@ -423,6 +548,8 @@ def tile_gpt_pa_kernel(tc, x, Wqkv_bytes, Wqkv_scale, q_conv_w, k_conv_w, v_conv
             x_turn(1, X1ENG)
             for k in range(HW_A, LEAD_W - 1):
                 w_widen(k)
+            if WIDE2:
+                w_widen_block(None)
             w_interleave(2)
             w_interleave(3)
             x_quant(1)
@@ -442,7 +569,7 @@ def tile_gpt_pa_kernel(tc, x, Wqkv_bytes, Wqkv_scale, q_conv_w, k_conv_w, v_conv
             x_quant(0)
             w_quant(0)
             w_quant(1)
-            for k in range(2, LEAD_W - 1):
+            for k in range(2, HW_A):
                 w_widen(k)
             x_turn(1, X1ENG, X1A)
             st_mx(0, (0,))
@@ -450,12 +577,21 @@ def tile_gpt_pa_kernel(tc, x, Wqkv_bytes, Wqkv_scale, q_conv_w, k_conv_w, v_conv
             x_turn(1, X1ENG, X1B)
             st_s_taps(0, (0,))
             st_s_taps(1, (0,))
-            for k in range(2, LEAD_I - 1):
-                w_interleave(k)
+            for k in range(HW_A, LEAD_W - 1):
+                w_widen(k)
+            w_interleave(2)
+            w_interleave(3)
+            if XQ_FIRST:
+                x_quant(1)
             st_v_taps(0, nothing, (0,))
-            x_quant(1)
             st_v_taps(1, nothing, (0,))
-            for k in range(2, LEAD_Q - 1):
+            if not XQ_FIRST:
+                x_quant(1)
+            w_quant(2)
+            w_quant(3)
+            for k in range(4, LEAD_I - 1):
+                w_interleave(k)
+            for k in range(4, LEAD_Q - 1):
                 w_quant(k)
             tables_gpsimd()
 
@@ -473,9 +609,13 @@ def tile_gpt_pa_kernel(tc, x, Wqkv_bytes, Wqkv_scale, q_conv_w, k_conv_w, v_conv
                             st_diag_tile(hw, tt)
             if i == 2:
                 tables_tensor()
+                if RA1:
+                    tables_tensor2()
             if i == 0:
                 w_widen(LEAD_W - 1)
             w_widen(i + LEAD_W)
+            if WIDE2:
+                w_widen_block(i)
 
             def w_step():
                 w_quant(i - 1 + LEAD_Q)
@@ -490,14 +630,19 @@ def tile_gpt_pa_kernel(tc, x, Wqkv_bytes, Wqkv_scale, q_conv_w, k_conv_w, v_conv
                 st_v_taps(i, nothing, (1,))
             elif i < NHEADS:
                 st_v_taps(i, w_step)
-            if i + 2 in DIAG:
+            if i in P2:
+                st_g_taps(i)
+            if i + 2 in DIAG and not DIAG_ON_V:
                 diag_matrices(i + 2)
-            if 0 <= i - LA < NHEADS:
+            late_add = TAIL >= 1 and i >= NHEADS
+            if 0 <= i - LA < NHEADS and not late_add:
                 st_rope_add(i - LA)
             if 0 <= i - 1 < NHEADS and i - 1 not in DIAG:
                 st_tr(i - 1)
                 st_ss_bank(i - 1, 0)
                 st_ss_bank(i - 1, 1)
+            if 0 <= i - LA < NHEADS and late_add:
+                st_rope_add(i - LA)
             if BG_LATE:
                 for n, hw in enumerate(DIAG):
                     for tt in range(TT):

@@ -44,9 +44,13 @@ DIAG = ()
 CHAIN = (0, 1)
 POOL_O = ()
 S3 = (21, 22, 23)
+S4 = ()
 P2 = ()
 PAD = TAPS - 1
 HEAD = 2
+WLOAD = True
+WW_LAST = False
+WQ0_LATE = False
 VW = ()
 TAIL = 2
 WIDE2 = False
@@ -65,7 +69,7 @@ WIDE = False
 HW_A = 4
 QSIZES = (2,) * 12
 W_BEFORE_X = (0, 4)
-TAB_BEFORE_W = 2
+TAB_BEFORE_W = 3
 X1ENG = "SVSV"
 X1A = (0, 1, 2, 3)
 X1B = ()
@@ -106,6 +110,9 @@ def tile_gpt_pa_kernel(tc, x, Wqkv_bytes, Wqkv_scale, q_conv_w, k_conv_w, v_conv
         pair_c = []
         for s in range(NSETS if S3 else 0):
             pair_c.append(keep.tile([P, T], F32, name="pair_c%d" % s, tag="pair_c%d" % s))
+        pair_d = []
+        for s in range(NSETS if S4 else 0):
+            pair_d.append(keep.tile([P, T], F32, name="pair_d%d" % s, tag="pair_d%d" % s))
         p2t = []
         for s in range(2 if P2 else 0):
             p2t.append(
@@ -157,9 +164,19 @@ def tile_gpt_pa_kernel(tc, x, Wqkv_bytes, Wqkv_scale, q_conv_w, k_conv_w, v_conv
             for g in range(PASSES):
                 nc.sync.dma_start(out=wbytes[li][:, g, :, :], in_=w_view[g][:, :, c0:c0 + w])
 
-        nc.scalar.dma_start(out=qw[:], in_=q_conv_w.rearrange("(h d) j -> d h j", d=P))
-        nc.scalar.dma_start(out=kw[:], in_=k_conv_w.rearrange("(h d) j -> d h j", d=P))
-        nc.scalar.dma_start(out=vw[:], in_=v_conv_w.rearrange("(h d) j -> d h j", d=P))
+        if WLOAD:
+            wrow = keep.tile([P, HS * TAPS], BF16, name="wrow", tag="wrow")
+            wrj = keep.tile([P, TAPS, HS], BF16, name="wrj", tag="wrj")
+            nc.scalar.dma_start(out=wrow[0:16, :], in_=q_conv_w.rearrange("(h d) j -> h (d j)", d=P))
+            nc.scalar.dma_start(out=wrow[16:20, :], in_=k_conv_w.rearrange("(h d) j -> h (d j)", d=P))
+            nc.scalar.dma_start(out=wrow[20:24, :], in_=v_conv_w.rearrange("(h d) j -> h (d j)", d=P))
+            nc.scalar.dma_start(out=wrow[24:32, :], in_=q_conv_w.rearrange("(h d) j -> h (d j)", d=P)[0:8, :])
+            nc.vector.memset(wrow[32:64, :], 0.0)
+            nc.vector.memset(wrow[64:128, :], 0.0)
+        else:
+            nc.scalar.dma_start(out=qw[:], in_=q_conv_w.rearrange("(h d) j -> d h j", d=P))
+            nc.scalar.dma_start(out=kw[:], in_=k_conv_w.rearrange("(h d) j -> d h j", d=P))
+            nc.scalar.dma_start(out=vw[:], in_=v_conv_w.rearrange("(h d) j -> d h j", d=P))
         nc.sync.dma_start(out=wscale[:], in_=Wqkv_scale.rearrange("(g p t) o -> p g (t o)", p=P, t=4))
         wl = 0
         for tt in range(TT):
@@ -175,11 +192,15 @@ def tile_gpt_pa_kernel(tc, x, Wqkv_bytes, Wqkv_scale, q_conv_w, k_conv_w, v_conv
 
         nc.vector.memset(warm[:], 0.0)
         nc.scalar.activation(out=warm[:], in_=warm[:], func=ACT.Silu)
+        if WLOAD:
+            make_identity(nc, identb[:])
         make_identity(nc, ident[:])
         for s in range(NSETS):
             nc.gpsimd.memset(pair_a[s][:, 0:8], 0.0)
             if S3:
                 nc.gpsimd.memset(pair_c[s][:, 0:8], 0.0)
+            if S4:
+                nc.gpsimd.memset(pair_d[s][:, 0:8], 0.0)
         for tiles in p2t:
             nc.gpsimd.memset(tiles[0][:, 0:PAD], 0.0)
             nc.gpsimd.memset(tiles[3][:, 0:8], 0.0)
@@ -187,12 +208,25 @@ def tile_gpt_pa_kernel(tc, x, Wqkv_bytes, Wqkv_scale, q_conv_w, k_conv_w, v_conv
         for hw in DIAG[0:2]:
             nc.gpsimd.memset(upad[hw][:, 0:PAD], 0.0)
         wf_g = wf[:].rearrange("p (g r) j -> p g r j", r=6)
-        nc.gpsimd.tensor_copy(out=wf_g[:, :, 0:4, :], in_=qw[:].rearrange("p (g r) j -> p g r j", r=4))
-        nc.gpsimd.tensor_copy(out=wf_g[:, :, 4, :], in_=kw[:])
-        nc.gpsimd.tensor_copy(out=wf_g[:, :, 5, :], in_=vw[:])
+        def conv_weights():
+            nc.vector.tensor_copy(out=wrj[:], in_=wrow[:].rearrange("p (d j) -> p j d", j=TAPS))
+            w_t = psum_c.tile([P, TAPS, HS], BF16, name="w_t", tag="cbank")
+            for j in range(TAPS):
+                nc.tensor.transpose(w_t[:, j, :], wrj[:, j, :], identb[:])
+            nc.vector.tensor_copy(out=wf_g[:, :, 0:4, :], in_=w_t[:, :, 0:16].rearrange("p j (g r) -> p g r j", r=4))
+            nc.vector.tensor_copy(out=wf_g[:, :, 4, :], in_=w_t[:, :, 16:20].rearrange("p j g -> p g j"))
+            nc.vector.tensor_copy(out=wf_g[:, :, 5, :], in_=w_t[:, :, 20:24].rearrange("p j g -> p g j"))
+
+        if WLOAD:
+            conv_weights()
+        else:
+            nc.gpsimd.tensor_copy(out=wf_g[:, :, 0:4, :], in_=qw[:].rearrange("p (g r) j -> p g r j", r=4))
+            nc.gpsimd.tensor_copy(out=wf_g[:, :, 4, :], in_=kw[:])
+            nc.gpsimd.tensor_copy(out=wf_g[:, :, 5, :], in_=vw[:])
 
         def tables_gpsimd():
-            make_identity(nc, identb[:])
+            if not WLOAD:
+                make_identity(nc, identb[:])
             if RA1:
                 nc.gpsimd.tensor_scalar(out=sgn_s[:, :, 0, :], in0=tabs[:, 1, :, :], scalar1=-1.0, scalar2=0.0, op0=ALU.mult, op1=ALU.add)
                 nc.gpsimd.tensor_scalar(out=sgn_s[:, :, 1, :], in0=tabs[:, 1, :, :], scalar1=1.0, scalar2=0.0, op0=ALU.mult, op1=ALU.add)
@@ -376,6 +410,8 @@ def tile_gpt_pa_kernel(tc, x, Wqkv_bytes, Wqkv_scale, q_conv_w, k_conv_w, v_conv
                     s_product(hw, hf, b, 3)
                     if hw in S3:
                         s_product(hw, hf, pair_c[hw % NSETS], 2)
+                    if hw in S4:
+                        s_product(hw, hf, pair_d[hw % NSETS], 0)
 
         def st_v_taps(hw, between, hfs=(0, 1)):
             a, b = pair_a[hw % NSETS], pair_b[hw % NSETS]
@@ -397,7 +433,8 @@ def tile_gpt_pa_kernel(tc, x, Wqkv_bytes, Wqkv_scale, q_conv_w, k_conv_w, v_conv
                         between()
             else:
                 for hf in hfs:
-                    v_madd(hw, hf, a, 0)
+                    if hw not in S4:
+                        v_madd(hw, hf, a, 0)
                     if hw not in S3:
                         v_madd(hw, hf, b, 2)
                     if hf == 0:
@@ -425,6 +462,8 @@ def tile_gpt_pa_kernel(tc, x, Wqkv_bytes, Wqkv_scale, q_conv_w, k_conv_w, v_conv
                         nc.tensor.matmul(out=cv[:, q, :], lhsT=a[:, tt * P:(tt + 1) * P], rhs=ident[:], is_transpose=True, start=True, stop=False)
                     if hw in S3:
                         nc.tensor.matmul(out=cv[:, q, :], lhsT=pair_c[hw % NSETS][:, tt * P:(tt + 1) * P], rhs=ident[:], is_transpose=True, start=False, stop=False)
+                    if hw in S4:
+                        nc.tensor.matmul(out=cv[:, q, :], lhsT=pair_d[hw % NSETS][:, tt * P:(tt + 1) * P], rhs=ident[:], is_transpose=True, start=False, stop=False)
                     nc.tensor.matmul(out=cv[:, q, :], lhsT=b[:, tt * P:(tt + 1) * P], rhs=ident[:], is_transpose=True, start=(hw in CHAIN), stop=True)
 
         def st_diag_tile(hw, tt):
@@ -541,8 +580,9 @@ def tile_gpt_pa_kernel(tc, x, Wqkv_bytes, Wqkv_scale, q_conv_w, k_conv_w, v_conv
             w_interleave(0)
             w_interleave(1)
             x_quant(0)
-            w_quant(0)
-            w_quant(1)
+            if not WQ0_LATE:
+                w_quant(0)
+                w_quant(1)
             for k in range(2, HW_A):
                 w_widen(k)
             x_turn(1, X1ENG)
@@ -550,9 +590,14 @@ def tile_gpt_pa_kernel(tc, x, Wqkv_bytes, Wqkv_scale, q_conv_w, k_conv_w, v_conv
                 w_widen(k)
             if WIDE2:
                 w_widen_block(None)
+            if WQ0_LATE:
+                x_quant(1)
+                w_quant(0)
+                w_quant(1)
             w_interleave(2)
             w_interleave(3)
-            x_quant(1)
+            if not WQ0_LATE:
+                x_quant(1)
             w_quant(2)
             w_quant(3)
             for k in range(4, LEAD_I - 1):
@@ -611,11 +656,15 @@ def tile_gpt_pa_kernel(tc, x, Wqkv_bytes, Wqkv_scale, q_conv_w, k_conv_w, v_conv
                 tables_tensor()
                 if RA1:
                     tables_tensor2()
-            if i == 0:
-                w_widen(LEAD_W - 1)
-            w_widen(i + LEAD_W)
-            if WIDE2:
-                w_widen_block(i)
+            def widen_now():
+                if i == 0:
+                    w_widen(LEAD_W - 1)
+                w_widen(i + LEAD_W)
+                if WIDE2:
+                    w_widen_block(i)
+
+            if not WW_LAST:
+                widen_now()
 
             def w_step():
                 w_quant(i - 1 + LEAD_Q)
@@ -643,6 +692,8 @@ def tile_gpt_pa_kernel(tc, x, Wqkv_bytes, Wqkv_scale, q_conv_w, k_conv_w, v_conv
                 st_ss_bank(i - 1, 1)
             if 0 <= i - LA < NHEADS and late_add:
                 st_rope_add(i - LA)
+            if WW_LAST:
+                widen_now()
             if BG_LATE:
                 for n, hw in enumerate(DIAG):
                     for tt in range(TT):

@@ -19,688 +19,368 @@ NCOL = 3072
 HS = 128
 HALF = HS // 2
 TAPS = 4
+PACK = 4
 NHEADS = NCOL // HS
-PASSES = C // 512
+GROUP = 6
+QUERIES = 4
+PASSES = C // (P * PACK)
+WORDS = P * PACK // 2
+BANK = 512
+HALVES = T // BANK
 TT = T // P
+TILES = TT // HALVES
 
 FLOPS = 2 * T * C * NCOL
 
-LOADS = [(0, 256), (256, 256), (512, 512), (1024, 512), (1536, 512), (2048, 512), (2560, 512)]
-SUB = 256
-NSUB = (NCOL // SUB) * PASSES
-NSETS = 3
-LEAD_Q = 4
-LEAD_I = 5
-LEAD_W = 6
-V_ADD_FROM = 22
-ACC_BANKS = 4
-CV_BANKS = 3
-WP_BUFS = 3
-WG_BUFS = 1
-OUT_BUFS = 3
-LR = 2
-LA = 2
-DIAG = ()
-CHAIN = (0, 1)
-POOL_O = ()
-S3 = (21, 22, 23)
-S4 = ()
-P2 = ()
-PAD = TAPS - 1
-HEAD = 2
-WLOAD = True
-WW_LAST = False
-WQ0_LATE = False
-VW = ()
-TAIL = 2
-WIDE2 = False
-WB_LEAD = 7
-XQ_FIRST = True
-RA1 = False
-WG_OWN = 0
-DIAG_ON_V = False
-WI_MERGE = False
-BG_LATE = False
-BG_START = (6, 12, 18)
-BG_NUM = 3
-BG_DEN = 4
-BG_SS = 0
-WIDE = False
-HW_A = 4
-QSIZES = (2,) * 12
-W_BEFORE_X = (0, 4)
-TAB_BEFORE_W = 3
-X1ENG = "SVSV"
-X1A = (0, 1, 2, 3)
-X1B = ()
+W_LOADS = [(0, 256), (256, 256), (512, 512), (1024, 512), (1536, 512), (2048, 512), (2560, 512)]
+PIECE = 256
+NPIECES = (NCOL // PIECE) * PASSES
+WIDEN_AHEAD = 6
+INTERLEAVE_AHEAD = 4
+QUANTIZE_AHEAD = 3
+TAP_SETS = 3
+VECTOR_HEAVY = (0, 1)
+SCALAR_HEAVY = (21, 22, 23)
+LAST_ROPE_HEAD = 22
 
 
 def tile_gpt_pa_kernel(tc, x, Wqkv_bytes, Wqkv_scale, q_conv_w, k_conv_w, v_conv_w, cos, sin, out_0, out_1, out_2):
     nc = tc.nc
     with ExitStack() as ctx:
         keep = ctx.enter_context(tc.tile_pool(name="keep", bufs=1))
-        wstage = ctx.enter_context(tc.tile_pool(name="wstage", bufs=WP_BUFS))
-        outp = ctx.enter_context(tc.tile_pool(name="outp", bufs=OUT_BUFS))
+        wstage = ctx.enter_context(tc.tile_pool(name="wstage", bufs=3))
+        outp = ctx.enter_context(tc.tile_pool(name="outp", bufs=3))
         psum_t = ctx.enter_context(tc.psum_pool(name="psum_t", bufs=1))
-        psum_p = ctx.enter_context(tc.psum_pool(name="psum_p", bufs=ACC_BANKS))
-        psum_c = ctx.enter_context(tc.psum_pool(name="psum_c", bufs=CV_BANKS))
-        psum_b = ctx.enter_context(tc.psum_pool(name="psum_b", bufs=1)) if DIAG else None
+        psum_p = ctx.enter_context(tc.psum_pool(name="psum_p", bufs=4))
+        psum_c = ctx.enter_context(tc.psum_pool(name="psum_c", bufs=3))
         ctx.enter_context(tc.manual_schedule())
 
         wbytes = []
-        for li, (c0, w) in enumerate(LOADS):
-            wbytes.append(keep.tile([P, PASSES, 4, w], U8, name="wbytes%d" % li, tag="wbytes%d" % li))
+        for li, (c0, width) in enumerate(W_LOADS):
+            wbytes.append(keep.tile([P, PASSES, PACK, width], U8, name="wbytes%d" % li, tag="wbytes%d" % li))
         xraw = []
         for tt in range(TT):
             xraw.append(keep.tile([P, C], BF16, name="xraw%d" % tt, tag="xraw%d" % tt))
-        wscale = keep.tile([P, PASSES, 4], F32, name="wscale", tag="wscale")
-        qw = keep.tile([P, 16, TAPS], BF16, name="qw", tag="qw")
-        kw = keep.tile([P, 4, TAPS], BF16, name="kw", tag="kw")
-        vw = keep.tile([P, 4, TAPS], BF16, name="vw", tag="vw")
-        wf = keep.tile([P, NHEADS, TAPS], F32, name="wf", tag="wf")
-        tabs = keep.tile([P, 2, TT, HALF], BF16, name="tabs", tag="tabs")
+        wscale = keep.tile([P, PASSES, PACK], F32, name="wscale", tag="wscale")
+        conv_w = keep.tile([P, NHEADS, TAPS], F32, name="conv_w", tag="conv_w")
+        tables_sb = keep.tile([P, 2, TT, HALF], BF16, name="tables_sb", tag="tables_sb")
         ident = keep.tile([P, P], F32, name="ident", tag="ident")
         identb = keep.tile([P, P], BF16, name="identb", tag="identb")
         warm = keep.tile([P, 1], F32, name="warm", tag="warm")
-        pair_a = []
-        pair_b = []
-        for s in range(NSETS):
-            pair_a.append(keep.tile([P, T], F32, name="pair_a%d" % s, tag="pair_a%d" % s))
-            pair_b.append(keep.tile([P, T], F32, name="pair_b%d" % s, tag="pair_b%d" % s))
-        pair_c = []
-        for s in range(NSETS if S3 else 0):
-            pair_c.append(keep.tile([P, T], F32, name="pair_c%d" % s, tag="pair_c%d" % s))
-        pair_d = []
-        for s in range(NSETS if S4 else 0):
-            pair_d.append(keep.tile([P, T], F32, name="pair_d%d" % s, tag="pair_d%d" % s))
-        p2t = []
-        for s in range(2 if P2 else 0):
-            p2t.append(
-                (
-                    keep.tile([P, PAD + T], F32, name="usb%d" % s, tag="usb%d" % s),
-                    keep.tile([P, PAD + T], F32, name="pp1%d" % s, tag="pp1%d" % s),
-                    keep.tile([P, PAD + T], F32, name="pp3%d" % s, tag="pp3%d" % s),
-                    keep.tile([P, T], F32, name="va%d" % s, tag="va%d" % s),
-                    keep.tile([P, T], F32, name="vb%d" % s, tag="vb%d" % s),
-                )
-            )
-        upad = {}
-        dmat = {}
-        for n, hw in enumerate(DIAG):
-            upad[hw] = keep.tile([P, PAD + T], F32, name="upad%d" % (n % 2), tag="upad%d" % (n % 2))
-            dmat[hw] = keep.tile([P, TAPS, P], F32, name="dmat%d" % n, tag="dmat%d" % n)
-        xg = []
-        xc = []
-        xs = []
-        for hf in range(2):
-            xg.append(keep.tile([P, PASSES, 512, 4], BF16, name="xg%d" % hf, tag="xg%d" % hf, align_bytes=64))
-            xc.append(keep.tile([P, PASSES, 512], U32, name="xc%d" % hf, tag="xc%d" % hf, align_bytes=64))
-            xs.append(keep.tile([P, PASSES, 512], U8, name="xs%d" % hf, tag="xs%d" % hf, align_bytes=64))
-        wc = []
-        ws = []
-        place = {}
-        last_of = {}
-        k = 0
-        for gi, n in enumerate(QSIZES):
-            wc.append(keep.tile([P, n, SUB], U32, name="wc%d" % gi, tag="wc%d" % gi, align_bytes=64))
-            ws.append(keep.tile([P, n, SUB], U8, name="ws%d" % gi, tag="ws%d" % gi, align_bytes=64))
-            for pos in range(n):
-                place[k] = (gi, pos)
-                k += 1
-            last_of[k - 1] = gi
-        assert k == NSUB
-        tab = psum_t.tile([P, 2, TT, HALF], BF16, name="tab", tag="tab")
-        if RA1:
-            sgn_s = keep.tile([P, TT, 2, HALF], BF16, name="sgn_s", tag="sgn_s")
-            sgn = psum_t.tile([P, TT, 2, HALF], BF16, name="sgn", tag="sgn")
+        sum_a = []
+        sum_b = []
+        for st in range(TAP_SETS):
+            sum_a.append(keep.tile([P, T], F32, name="sum_a%d" % st, tag="sum_a%d" % st))
+            sum_b.append(keep.tile([P, T], F32, name="sum_b%d" % st, tag="sum_b%d" % st))
+        sum_c = []
+        for st in range(TAP_SETS):
+            sum_c.append(keep.tile([P, T], F32, name="sum_c%d" % st, tag="sum_c%d" % st))
+        x_grouped = []
+        x_codes = []
+        x_scales = []
+        for hf in range(HALVES):
+            x_grouped.append(keep.tile([P, PASSES, BANK, PACK], BF16, name="x_grouped%d" % hf, tag="x_grouped%d" % hf, align_bytes=64))
+            x_codes.append(keep.tile([P, PASSES, BANK], U32, name="x_codes%d" % hf, tag="x_codes%d" % hf, align_bytes=64))
+            x_scales.append(keep.tile([P, PASSES, BANK], U8, name="x_scales%d" % hf, tag="x_scales%d" % hf, align_bytes=64))
+        w_codes = []
+        w_scales = []
+        for pair in range(NPIECES // PASSES):
+            w_codes.append(keep.tile([P, PASSES, PIECE], U32, name="w_codes%d" % pair, tag="w_codes%d" % pair, align_bytes=64))
+            w_scales.append(keep.tile([P, PASSES, PIECE], U8, name="w_scales%d" % pair, tag="w_scales%d" % pair, align_bytes=64))
+        tables = psum_t.tile([P, 2, TT, HALF], BF16, name="tables", tag="tables")
+        conv_rows = keep.tile([P, HS * TAPS], BF16, name="conv_rows", tag="conv_rows")
+        conv_by_tap = keep.tile([P, TAPS, HS], BF16, name="conv_by_tap", tag="conv_by_tap")
 
-        w_view = Wqkv_bytes.rearrange("(g p t) n -> g p t n", p=P, t=4)
+        w_view = Wqkv_bytes.rearrange("(g p t) n -> g p t n", p=P, t=PACK)
         x_view = x.rearrange("b (tt p) k -> (b tt) p k", p=P)
-        cos_v = cos.rearrange("(tt p) i -> p tt i", p=P)
-        sin_v = sin.rearrange("(tt p) i -> p tt i", p=P)
 
         def load_w(li):
-            c0, w = LOADS[li]
+            c0, width = W_LOADS[li]
             for g in range(PASSES):
-                nc.sync.dma_start(out=wbytes[li][:, g, :, :], in_=w_view[g][:, :, c0:c0 + w])
+                nc.sync.dma_start(out=wbytes[li][:, g, :, :], in_=w_view[g][:, :, c0:c0 + width])
 
-        if WLOAD:
-            wrow = keep.tile([P, HS * TAPS], BF16, name="wrow", tag="wrow")
-            wrj = keep.tile([P, TAPS, HS], BF16, name="wrj", tag="wrj")
-            nc.scalar.dma_start(out=wrow[0:16, :], in_=q_conv_w.rearrange("(h d) j -> h (d j)", d=P))
-            nc.scalar.dma_start(out=wrow[16:20, :], in_=k_conv_w.rearrange("(h d) j -> h (d j)", d=P))
-            nc.scalar.dma_start(out=wrow[20:24, :], in_=v_conv_w.rearrange("(h d) j -> h (d j)", d=P))
-            nc.scalar.dma_start(out=wrow[24:32, :], in_=q_conv_w.rearrange("(h d) j -> h (d j)", d=P)[0:8, :])
-            nc.vector.memset(wrow[32:64, :], 0.0)
-            nc.vector.memset(wrow[64:128, :], 0.0)
-        else:
-            nc.scalar.dma_start(out=qw[:], in_=q_conv_w.rearrange("(h d) j -> d h j", d=P))
-            nc.scalar.dma_start(out=kw[:], in_=k_conv_w.rearrange("(h d) j -> d h j", d=P))
-            nc.scalar.dma_start(out=vw[:], in_=v_conv_w.rearrange("(h d) j -> d h j", d=P))
-        nc.sync.dma_start(out=wscale[:], in_=Wqkv_scale.rearrange("(g p t) o -> p g (t o)", p=P, t=4))
-        wl = 0
-        for tt in range(TT):
-            while wl < len(W_BEFORE_X) and W_BEFORE_X[wl] <= tt:
-                load_w(wl)
-                wl += 1
+        q_rows = q_conv_w.rearrange("(h d) j -> h (d j)", d=P)
+        nc.scalar.dma_start(out=conv_rows[0:16, :], in_=q_rows)
+        nc.scalar.dma_start(out=conv_rows[16:20, :], in_=k_conv_w.rearrange("(h d) j -> h (d j)", d=P))
+        nc.scalar.dma_start(out=conv_rows[20:24, :], in_=v_conv_w.rearrange("(h d) j -> h (d j)", d=P))
+        nc.scalar.dma_start(out=conv_rows[24:32, :], in_=q_rows[0:8, :])
+        nc.vector.memset(conv_rows[32:64, :], 0.0)
+        nc.vector.memset(conv_rows[64:128, :], 0.0)
+        nc.sync.dma_start(out=wscale[:], in_=Wqkv_scale.rearrange("(g p t) o -> p g (t o)", p=P, t=PACK))
+        load_w(0)
+        for tt in range(TILES):
             nc.sync.dma_start(out=xraw[tt][:], in_=x_view[tt])
-        for li in range(wl, len(LOADS)):
-            if li == TAB_BEFORE_W:
-                nc.sync.dma_start(out=tabs[:, 0, :, :], in_=cos_v)
-                nc.sync.dma_start(out=tabs[:, 1, :, :], in_=sin_v)
+        load_w(1)
+        for tt in range(TILES, TT):
+            nc.sync.dma_start(out=xraw[tt][:], in_=x_view[tt])
+        load_w(2)
+        nc.sync.dma_start(out=tables_sb[:, 0, :, :], in_=cos.rearrange("(tt p) i -> p tt i", p=P))
+        nc.sync.dma_start(out=tables_sb[:, 1, :, :], in_=sin.rearrange("(tt p) i -> p tt i", p=P))
+        for li in range(3, len(W_LOADS)):
             load_w(li)
 
         nc.vector.memset(warm[:], 0.0)
         nc.scalar.activation(out=warm[:], in_=warm[:], func=ACT.Silu)
-        if WLOAD:
-            make_identity(nc, identb[:])
+        make_identity(nc, identb[:])
         make_identity(nc, ident[:])
-        for s in range(NSETS):
-            nc.gpsimd.memset(pair_a[s][:, 0:8], 0.0)
-            if S3:
-                nc.gpsimd.memset(pair_c[s][:, 0:8], 0.0)
-            if S4:
-                nc.gpsimd.memset(pair_d[s][:, 0:8], 0.0)
-        for tiles in p2t:
-            nc.gpsimd.memset(tiles[0][:, 0:PAD], 0.0)
-            nc.gpsimd.memset(tiles[3][:, 0:8], 0.0)
-            nc.gpsimd.memset(tiles[4][:, 0:8], 0.0)
-        for hw in DIAG[0:2]:
-            nc.gpsimd.memset(upad[hw][:, 0:PAD], 0.0)
-        wf_g = wf[:].rearrange("p (g r) j -> p g r j", r=6)
-        def conv_weights():
-            nc.vector.tensor_copy(out=wrj[:], in_=wrow[:].rearrange("p (d j) -> p j d", j=TAPS))
-            w_t = psum_c.tile([P, TAPS, HS], BF16, name="w_t", tag="cbank")
-            for j in range(TAPS):
-                nc.tensor.transpose(w_t[:, j, :], wrj[:, j, :], identb[:])
-            nc.vector.tensor_copy(out=wf_g[:, :, 0:4, :], in_=w_t[:, :, 0:16].rearrange("p j (g r) -> p g r j", r=4))
-            nc.vector.tensor_copy(out=wf_g[:, :, 4, :], in_=w_t[:, :, 16:20].rearrange("p j g -> p g j"))
-            nc.vector.tensor_copy(out=wf_g[:, :, 5, :], in_=w_t[:, :, 20:24].rearrange("p j g -> p g j"))
+        for st in range(TAP_SETS):
+            nc.gpsimd.memset(sum_a[st][:, 0:8], 0.0)
+            nc.gpsimd.memset(sum_c[st][:, 0:8], 0.0)
+        nc.vector.tensor_copy(out=conv_by_tap[:], in_=conv_rows[:].rearrange("p (d j) -> p j d", j=TAPS))
+        conv_t = psum_c.tile([P, TAPS, HS], BF16, name="conv_t", tag="cbank")
+        for j in range(TAPS):
+            nc.tensor.transpose(conv_t[:, j, :], conv_by_tap[:, j, :], identb[:])
+        conv_w_groups = conv_w[:].rearrange("p (grp r) j -> p grp r j", r=GROUP)
+        nc.vector.tensor_copy(out=conv_w_groups[:, :, 0:QUERIES, :], in_=conv_t[:, :, 0:16].rearrange("p j (grp r) -> p grp r j", r=QUERIES))
+        nc.vector.tensor_copy(out=conv_w_groups[:, :, QUERIES, :], in_=conv_t[:, :, 16:20].rearrange("p j grp -> p grp j"))
+        nc.vector.tensor_copy(out=conv_w_groups[:, :, QUERIES + 1, :], in_=conv_t[:, :, 20:24].rearrange("p j grp -> p grp j"))
 
-        if WLOAD:
-            conv_weights()
-        else:
-            nc.gpsimd.tensor_copy(out=wf_g[:, :, 0:4, :], in_=qw[:].rearrange("p (g r) j -> p g r j", r=4))
-            nc.gpsimd.tensor_copy(out=wf_g[:, :, 4, :], in_=kw[:])
-            nc.gpsimd.tensor_copy(out=wf_g[:, :, 5, :], in_=vw[:])
-
-        def tables_gpsimd():
-            if not WLOAD:
-                make_identity(nc, identb[:])
-            if RA1:
-                nc.gpsimd.tensor_scalar(out=sgn_s[:, :, 0, :], in0=tabs[:, 1, :, :], scalar1=-1.0, scalar2=0.0, op0=ALU.mult, op1=ALU.add)
-                nc.gpsimd.tensor_scalar(out=sgn_s[:, :, 1, :], in0=tabs[:, 1, :, :], scalar1=1.0, scalar2=0.0, op0=ALU.mult, op1=ALU.add)
-
-        def diag_matrices(hw):
-            for j in range(TAPS):
-                nc.gpsimd.tensor_scalar(out=dmat[hw][:, j, :], in0=ident[:], scalar1=wf[:, hw, j:j + 1], scalar2=0.0, op0=ALU.mult, op1=ALU.add)
-
-        if DIAG_ON_V:
-            for hw in DIAG:
-                nc.vector.tensor_tensor(
-                    out=dmat[hw][:], in0=ident[:].unsqueeze(1).to_broadcast([P, TAPS, P]), in1=wf[:, hw, :].unsqueeze(2).to_broadcast([P, TAPS, P]), op=ALU.mult
-                )
-
-        def tables_tensor():
-            for b in range(2):
+        def tables_to_psum():
+            for table in range(2):
                 nc.tensor.matmul(
-                    out=tab[:, b, :, :].rearrange("p t i -> p (t i)"), lhsT=identb[:], rhs=tabs[:, b, :, :].rearrange("p t i -> p (t i)"), start=True, stop=True
+                    out=tables[:, table, :, :].rearrange("p tt i -> p (tt i)"),
+                    lhsT=identb[:],
+                    rhs=tables_sb[:, table, :, :].rearrange("p tt i -> p (tt i)"),
+                    start=True,
+                    stop=True,
                 )
 
-        def tables_tensor2():
-            flat_d = sgn[:].rearrange("p t h i -> p (t h i)")
-            flat_s = sgn_s[:].rearrange("p t h i -> p (t h i)")
-            for b in range(2):
-                nc.tensor.matmul(out=flat_d[:, b * 512:(b + 1) * 512], lhsT=identb[:], rhs=flat_s[:, b * 512:(b + 1) * 512], start=True, stop=True)
-
-        def x_turn(hf, engines, qs=(0, 1, 2, 3)):
-            words_out = xg[hf][:].rearrange("p g t j -> p (g t j)").bitcast(F32).rearrange("p (g t u) -> p g t u", g=PASSES, u=2)
-            for q in qs:
-                words = xraw[hf * 4 + q][:].bitcast(F32)
+        def x_turn(hf, engines):
+            words_out = x_grouped[hf][:].rearrange("p g c t -> p (g c t)").bitcast(F32).rearrange("p (g c w) -> p g c w", g=PASSES, w=2)
+            for tq in range(TILES):
+                words = xraw[hf * TILES + tq][:].bitcast(F32)
                 xt = psum_c.tile([P, PASSES, 2, P], F32, name="xt", tag="cbank")
                 for g in range(PASSES):
-                    for u in range(2):
-                        nc.tensor.transpose(xt[:, g, u, :], words[:, 256 * g + u:256 * (g + 1):2], ident[:])
-                dst = words_out[:, :, q * P:(q + 1) * P, :]
-                src = xt[:].rearrange("p g u r -> p g r u")
-                if engines[q] == "V":
+                    for w in range(2):
+                        nc.tensor.transpose(xt[:, g, w, :], words[:, WORDS * g + w:WORDS * (g + 1):2], ident[:])
+                dst = words_out[:, :, tq * P:(tq + 1) * P, :]
+                src = xt[:].rearrange("p g w c -> p g c w")
+                if engines[tq] == "V":
                     nc.vector.tensor_copy(out=dst, in_=src)
                 else:
                     nc.scalar.copy(out=dst, in_=src)
 
-        def x_quant(hf):
+        def x_quantize(hf):
             for g in range(PASSES):
                 nc.vector.quantize_mx(
-                    out=xc[hf][:, g, :].bitcast(FP8X4),
-                    scales=xs[hf][:, g, :],
-                    in_=xg[hf][:, g, :, :].rearrange("p t j -> p (t j)"),
+                    out=x_codes[hf][:, g, :].bitcast(FP8X4),
+                    scales=x_scales[hf][:, g, :],
+                    in_=x_grouped[hf][:, g, :, :].rearrange("p c t -> p (c t)"),
                 )
 
-        wplanes = {}
-        wpair = {}
-        wgroup = {}
+        w_planes = {}
+        w_grouped = {}
 
-        wblock = {}
-
-        def w_widen_block(slot):
-            for m in range(1, NCOL // 512):
-                for e in range(8):
-                    at = 4 * m - WB_LEAD + e // 2
-                    if at == slot or (slot is None and at < 0):
-                        g, t = divmod(e, 4)
-                        if e == 0:
-                            wblock[m] = wstage.tile([P, PASSES, 4, 512], BF16, name="wpb", tag="wpb", bufs=2)
-                        nc.scalar.activation(out=wblock[m][:, g, t, :], in_=wbytes[m + 1][:, g, t, :].bitcast(FP8), func=ACT.Copy, scale=wscale[:, g, t:t + 1])
-
-        def w_widen(k):
-            if not 0 <= k < NSUB:
+        def w_widen(piece):
+            if not 0 <= piece < NPIECES:
                 return
-            if WIDE2 and k >= 4:
-                return
-            c0 = (k // 2) * SUB
-            g = k % 2
-            li = max(i for i in range(len(LOADS)) if LOADS[i][0] <= c0)
-            off = c0 - LOADS[li][0]
-            if WIDE:
-                if off != 0:
-                    wplanes[k] = wplanes[k - 2]
-                    return
-                width = LOADS[li][1]
-            else:
-                width = SUB
-            if WI_MERGE:
-                if g == 0:
-                    wpair[k // 2] = wstage.tile([P, PASSES, 4, SUB], BF16, name="wp", tag="wp")
-                wplanes[k] = wpair[k // 2][:, g, :, :]
-            else:
-                wplanes[k] = wstage.tile([P, 4, width], BF16, name="wp", tag="wp")[:]
-            for t in range(4):
-                if k in VW:
-                    nc.vector.tensor_scalar(out=wplanes[k][:, t, :], in0=wbytes[li][:, g, t, off:off + width].bitcast(FP8), scalar1=wscale[:, g, t:t + 1], scalar2=None, op0=ALU.mult)
-                    continue
+            pair, g = divmod(piece, PASSES)
+            c0 = pair * PIECE
+            li = max(i for i in range(len(W_LOADS)) if W_LOADS[i][0] <= c0)
+            off = c0 - W_LOADS[li][0]
+            w_planes[piece] = wstage.tile([P, PACK, PIECE], BF16, name="wp", tag="wp")
+            for t in range(PACK):
                 nc.scalar.activation(
-                    out=wplanes[k][:, t, :],
-                    in_=wbytes[li][:, g, t, off:off + width].bitcast(FP8),
+                    out=w_planes[piece][:, t, :],
+                    in_=wbytes[li][:, g, t, off:off + PIECE].bitcast(FP8),
                     func=ACT.Copy,
                     scale=wscale[:, g, t:t + 1],
                 )
 
-        def w_interleave(k):
-            if not 0 <= k < NSUB:
+        def w_interleave(piece):
+            if not 0 <= piece < NPIECES:
                 return
-            gi, pos = place[k]
-            if WI_MERGE:
-                if pos == 1:
-                    wgroup[gi] = wstage.tile([P, QSIZES[gi], SUB, 4], BF16, name="wg", tag="wg", bufs=WG_BUFS, align_bytes=64)
-                    nc.gpsimd.tensor_scalar(out=wgroup[gi][:], in0=wpair[k // 2][:].rearrange("p g t n -> p g n t"), scalar1=1.0, scalar2=0.0, op0=ALU.mult, op1=ALU.add)
-                return
-            if pos == 0 and gi < WG_OWN:
-                wgroup[gi] = wstage.tile([P, QSIZES[gi], SUB, 4], BF16, name="wgo%d" % gi, tag="wgo%d" % gi, bufs=1, align_bytes=64)
-            elif pos == 0:
-                wgroup[gi] = wstage.tile([P, QSIZES[gi], SUB, 4], BF16, name="wg", tag="wg", bufs=WG_BUFS, align_bytes=64)
-            c0 = (k // 2) * SUB
-            off = (c0 - max(c for c, w in LOADS if c <= c0)) if (WIDE or WIDE2) else 0
-            planes = wblock[k // 4][:, k % 2, :, :] if (WIDE2 and k >= 4) else wplanes[k]
+            pair, g = divmod(piece, PASSES)
+            if g == 0:
+                w_grouped[pair] = wstage.tile([P, PASSES, PIECE, PACK], BF16, name="wg", tag="wg", bufs=1, align_bytes=64)
             nc.gpsimd.tensor_scalar(
-                out=wgroup[gi][:, pos, :, :], in0=planes[:, :, off:off + SUB].rearrange("p t n -> p n t"), scalar1=1.0, scalar2=0.0, op0=ALU.mult, op1=ALU.add
+                out=w_grouped[pair][:, g, :, :], in0=w_planes[piece][:].rearrange("p t n -> p n t"), scalar1=1.0, scalar2=0.0, op0=ALU.mult, op1=ALU.add
             )
 
-        def w_quant(k):
-            if k not in last_of:
+        def w_quantize(piece):
+            if not 0 <= piece < NPIECES or piece % PASSES != PASSES - 1:
                 return
-            gi = last_of[k]
+            pair = piece // PASSES
             nc.vector.quantize_mx(
-                out=wc[gi][:].rearrange("p s n -> p (s n)").bitcast(FP8X4),
-                scales=ws[gi][:].rearrange("p s n -> p (s n)"),
-                in_=wgroup[gi][:].rearrange("p s n t -> p (s n t)"),
+                out=w_codes[pair][:].rearrange("p g n -> p (g n)").bitcast(FP8X4),
+                scales=w_scales[pair][:].rearrange("p g n -> p (g n)"),
+                in_=w_grouped[pair][:].rearrange("p g n t -> p (g n t)"),
             )
 
         q_view = out_0.rearrange("b (tt p) h d -> p (b tt) h d", p=P)
         k_view = out_1.rearrange("b (tt p) h d -> p (b tt) h d", p=P)
         v_view = out_2.rearrange("b (tt p) h d -> p (b tt) h d", p=P)
-        accs = {}
-        cvs = {}
-        sil = {}
-        ropes = {}
+        proj = {}
+        conv_sum = {}
+        silu_out = {}
+        rope_terms = {}
 
-        def st_mx(hw, hfs=(0, 1)):
-            unit = (hw * HS) // SUB
-            off = hw * HS - unit * SUB
+        def project(hw):
+            pair = (hw * HS) // PIECE
+            off = hw * HS - pair * PIECE
             cols = slice(off, off + HS)
-            for hf in hfs:
-                acc = psum_p.tile([P, 512], F32, name="acc", tag="pbank")
-                accs[(hw, hf)] = acc
+            for hf in range(HALVES):
+                acc = psum_p.tile([P, BANK], F32, name="acc", tag="pbank")
+                proj[(hw, hf)] = acc
                 for g in range(PASSES):
-                    gi, pos = place[unit * 2 + g]
                     nc.tensor.matmul_mx(
                         out=acc[:],
-                        lhsT=wc[gi][:, pos, cols].bitcast(FP8X4),
-                        lhsT_scale=ws[gi][:, pos, cols],
-                        rhs=xc[hf][:, g, :].bitcast(FP8X4),
-                        rhs_scale=xs[hf][:, g, :],
+                        lhsT=w_codes[pair][:, g, cols].bitcast(FP8X4),
+                        lhsT_scale=w_scales[pair][:, g, cols],
+                        rhs=x_codes[hf][:, g, :].bitcast(FP8X4),
+                        rhs_scale=x_scales[hf][:, g, :],
                         start=(g == 0),
                         stop=(g == PASSES - 1),
                     )
 
-        def span(hf, shift):
-            lo = shift + hf * 512
-            return lo, min(lo + 512, T)
+        def shifted(hf, j):
+            lo = TAPS - 1 - j + hf * BANK
+            return lo, min(lo + BANK, T)
 
-        def s_product(hw, hf, dst, j):
-            lo, hi = span(hf, TAPS - 1 - j)
-            nc.scalar.activation(out=dst[:, lo:hi], in_=accs[(hw, hf)][:, 0:hi - lo], func=ACT.Copy, scale=wf[:, hw, j:j + 1])
+        def scalar_product(hw, hf, dst, j):
+            lo, hi = shifted(hf, j)
+            nc.scalar.activation(out=dst[:, lo:hi], in_=proj[(hw, hf)][:, 0:hi - lo], func=ACT.Copy, scale=conv_w[:, hw, j:j + 1])
 
-        def v_madd(hw, hf, dst, j):
-            lo, hi = span(hf, TAPS - 1 - j)
+        def vector_multiply_add(hw, hf, dst, j):
+            lo, hi = shifted(hf, j)
             nc.vector.scalar_tensor_tensor(
-                out=dst[:, lo:hi], in0=accs[(hw, hf)][:, 0:hi - lo], scalar=wf[:, hw, j:j + 1], in1=dst[:, lo:hi], op0=ALU.mult, op1=ALU.add
+                out=dst[:, lo:hi], in0=proj[(hw, hf)][:, 0:hi - lo], scalar=conv_w[:, hw, j:j + 1], in1=dst[:, lo:hi], op0=ALU.mult, op1=ALU.add
             )
 
-        def st_s_taps(hw, hfs=(0, 1)):
-            a, b = pair_a[hw % NSETS], pair_b[hw % NSETS]
-            for hf in hfs:
-                if hw in P2:
-                    nc.scalar.copy(out=p2t[P2.index(hw) % 2][0][:, PAD + hf * 512:PAD + (hf + 1) * 512], in_=accs[(hw, hf)][:])
-                elif hw in DIAG:
-                    nc.scalar.copy(out=upad[hw][:, PAD + hf * 512:PAD + (hf + 1) * 512], in_=accs[(hw, hf)][:])
-                elif hw in CHAIN:
-                    s_product(hw, hf, b, 3)
+        def taps_on_scalar(hw):
+            st = hw % TAP_SETS
+            for hf in range(HALVES):
+                if hw in VECTOR_HEAVY:
+                    scalar_product(hw, hf, sum_b[st], 3)
                 else:
-                    s_product(hw, hf, a, 1)
-                    s_product(hw, hf, b, 3)
-                    if hw in S3:
-                        s_product(hw, hf, pair_c[hw % NSETS], 2)
-                    if hw in S4:
-                        s_product(hw, hf, pair_d[hw % NSETS], 0)
+                    scalar_product(hw, hf, sum_a[st], 1)
+                    scalar_product(hw, hf, sum_b[st], 3)
+                    if hw in SCALAR_HEAVY:
+                        scalar_product(hw, hf, sum_c[st], 2)
 
-        def st_v_taps(hw, between, hfs=(0, 1)):
-            a, b = pair_a[hw % NSETS], pair_b[hw % NSETS]
-            if hw in P2:
-                tiles = p2t[P2.index(hw) % 2]
-                for hf in hfs:
-                    for dst, j in ((tiles[3], 0), (tiles[4], 2)):
-                        lo, hi = span(hf, TAPS - 1 - j)
-                        nc.vector.tensor_scalar(out=dst[:, lo:hi], in0=accs[(hw, hf)][:, 0:hi - lo], scalar1=wf[:, hw, j:j + 1], scalar2=None, op0=ALU.mult)
-                    if hf == 0:
-                        between()
-            elif hw in DIAG:
-                between()
-            elif hw in CHAIN:
+        def taps_on_vector(hw, between):
+            st = hw % TAP_SETS
+            if hw in VECTOR_HEAVY:
                 for j in (2, 1, 0):
-                    for hf in hfs:
-                        v_madd(hw, hf, b, j)
+                    for hf in range(HALVES):
+                        vector_multiply_add(hw, hf, sum_b[st], j)
                     if j == 2:
                         between()
             else:
-                for hf in hfs:
-                    if hw not in S4:
-                        v_madd(hw, hf, a, 0)
-                    if hw not in S3:
-                        v_madd(hw, hf, b, 2)
+                for hf in range(HALVES):
+                    vector_multiply_add(hw, hf, sum_a[st], 0)
+                    if hw not in SCALAR_HEAVY:
+                        vector_multiply_add(hw, hf, sum_b[st], 2)
                     if hf == 0:
                         between()
 
-        def st_g_taps(hw):
-            tiles = p2t[P2.index(hw) % 2]
-            for dst, j in ((tiles[1], 1), (tiles[2], 3)):
-                nc.gpsimd.tensor_scalar(out=dst[:], in0=tiles[0][:], scalar1=wf[:, hw, j:j + 1], scalar2=0.0, op0=ALU.mult, op1=ALU.add)
+        def turn_and_add(hw):
+            st = hw % TAP_SETS
+            parts = [sum_b[st]]
+            if hw not in VECTOR_HEAVY:
+                parts = [sum_a[st]] + ([sum_c[st]] if hw in SCALAR_HEAVY else []) + parts
+            conv_sum[hw] = []
+            for hf in range(HALVES):
+                cv = psum_c.tile([P, TILES, HS], F32, name="cv", tag="cbank")
+                conv_sum[hw].append(cv)
+                for tq in range(TILES):
+                    tt = hf * TILES + tq
+                    for n, part in enumerate(parts):
+                        nc.tensor.matmul(
+                            out=cv[:, tq, :], lhsT=part[:, tt * P:(tt + 1) * P], rhs=ident[:], is_transpose=True, start=(n == 0), stop=(n == len(parts) - 1)
+                        )
 
-        def st_tr(hw):
-            a, b = pair_a[hw % NSETS], pair_b[hw % NSETS]
-            cvs[hw] = []
-            for bk in range(2):
-                cv = psum_c.tile([P, 4, HS], F32, name="cv", tag="cbank")
-                cvs[hw].append(cv)
-                for q in range(4):
-                    tt = bk * 4 + q
-                    if hw in P2:
-                        tiles = p2t[P2.index(hw) % 2]
-                        for n, (src, sh) in enumerate(((tiles[3], 0), (tiles[4], 0), (tiles[1], 1), (tiles[2], 3))):
-                            nc.tensor.matmul(out=cv[:, q, :], lhsT=src[:, tt * P + sh:(tt + 1) * P + sh], rhs=ident[:], is_transpose=True, start=(n == 0), stop=(n == 3))
-                        continue
-                    if hw not in CHAIN:
-                        nc.tensor.matmul(out=cv[:, q, :], lhsT=a[:, tt * P:(tt + 1) * P], rhs=ident[:], is_transpose=True, start=True, stop=False)
-                    if hw in S3:
-                        nc.tensor.matmul(out=cv[:, q, :], lhsT=pair_c[hw % NSETS][:, tt * P:(tt + 1) * P], rhs=ident[:], is_transpose=True, start=False, stop=False)
-                    if hw in S4:
-                        nc.tensor.matmul(out=cv[:, q, :], lhsT=pair_d[hw % NSETS][:, tt * P:(tt + 1) * P], rhs=ident[:], is_transpose=True, start=False, stop=False)
-                    nc.tensor.matmul(out=cv[:, q, :], lhsT=b[:, tt * P:(tt + 1) * P], rhs=ident[:], is_transpose=True, start=(hw in CHAIN), stop=True)
+        def silu(hw, hf):
+            if hf == 0:
+                silu_out[hw] = outp.tile([P, TT, HS], F32, name="s", tag="s")
+            tiles = slice(hf * TILES, (hf + 1) * TILES)
+            nc.scalar.activation(out=silu_out[hw][:, tiles, :], in_=conv_sum[hw][hf][:], func=ACT.Silu)
+            grp, r = divmod(hw, GROUP)
+            if r != GROUP - 1:
+                return
+            if hw == NHEADS - 1:
+                nc.sync.dma_start(out=v_view[:, tiles, grp, :], in_=silu_out[hw][:, tiles, :])
+            elif hf == HALVES - 1:
+                nc.sync.dma_start(out=v_view[:, :, grp, :], in_=silu_out[hw][:])
 
-        def st_diag_tile(hw, tt):
-            bk, q = divmod(tt, 4)
-            if q == 0:
-                if bk == 0:
-                    cvs[hw] = []
-                cvs[hw].append(psum_b.tile([P, 4, HS], F32, name="bg", tag="bgbank"))
-            for j in range(TAPS):
-                nc.tensor.matmul(
-                    out=cvs[hw][bk][:, q, :], lhsT=upad[hw][:, tt * P + j:(tt + 1) * P + j], rhs=dmat[hw][:, j, :], start=(j == 0), stop=(j == TAPS - 1)
-                )
+        def by_halves(tile):
+            return tile[:].rearrange("p tt (h i) -> p tt h i", h=2)
 
-        def st_ss_bank(hw, bk):
-            if bk == 0 and hw in DIAG:
-                sil[hw] = outp.tile([P, TT, HS], F32, name="sbg", tag="sbg", bufs=1)
-            elif bk == 0:
-                sil[hw] = outp.tile([P, TT, HS], F32, name="s", tag="s")
-            nc.scalar.activation(out=sil[hw][:, bk * 4:(bk + 1) * 4, :], in_=cvs[hw][bk][:], func=ACT.Silu)
-            grp, r = divmod(hw, 6)
-            if r == 5 and TAIL >= 2 and hw == NHEADS - 1:
-                nc.sync.dma_start(out=v_view[:, bk * 4:(bk + 1) * 4, grp, :], in_=sil[hw][:, bk * 4:(bk + 1) * 4, :])
-            elif r == 5 and bk == 1:
-                nc.sync.dma_start(out=v_view[:, :, grp, :], in_=sil[hw][:])
-
-        def halves(t):
-            return t[:].rearrange("p t (h i) -> p t h i", h=2)
-
-        def both_halves(table):
+        def for_both_halves(table):
             return table.unsqueeze(2).to_broadcast([P, TT, 2, HALF])
 
-        def st_rope_products(hw, between):
-            s = sil[hw]
-            o = outp.tile([P, TT, HS], F32, name="o", tag="o")
-            rot = outp.tile([P, TT, HS], F32, name="rot", tag="rot")
-            ropes[hw] = (o, rot)
-            if TAIL >= 4 and hw >= V_ADD_FROM:
-                grp = hw // 6
-                fin = outp.tile([P, TT, HS], F32, name="fin", tag="fin")
-                for b in range(2):
-                    tsl = slice(b * 4, (b + 1) * 4)
-                    for dst, k in ((o, 0), (rot, 1)):
-                        nc.vector.tensor_tensor(
-                            out=halves(dst)[:, tsl, :, :], in0=halves(s)[:, tsl, :, :], in1=tab[:, k, tsl, :].unsqueeze(2).to_broadcast([P, 4, 2, HALF]), op=ALU.mult
-                        )
-                    nc.vector.tensor_tensor(out=fin[:, tsl, 0:HALF], in0=o[:, tsl, 0:HALF], in1=rot[:, tsl, HALF:HS], op=ALU.subtract)
-                    nc.vector.tensor_tensor(out=fin[:, tsl, HALF:HS], in0=o[:, tsl, HALF:HS], in1=rot[:, tsl, 0:HALF], op=ALU.add)
-                    nc.sync.dma_start(out=k_view[:, tsl, grp, :], in_=fin[:, tsl, :])
-                between()
-                return
-            if hw in POOL_O:
-                nc.gpsimd.tensor_tensor(out=halves(o), in0=halves(s), in1=both_halves(tabs[:, 0, :, :]), op=ALU.mult)
-                nc.vector.tensor_tensor(out=halves(rot), in0=halves(s), in1=both_halves(tab[:, 1, :, :]), op=ALU.mult)
-                between()
-            else:
-                nc.vector.tensor_tensor(out=halves(o), in0=halves(s), in1=both_halves(tab[:, 0, :, :]), op=ALU.mult)
-                between()
-                if RA1:
-                    nc.vector.tensor_tensor(out=halves(rot), in0=halves(s)[:, :, ::-1, :], in1=sgn[:], op=ALU.mult)
-                else:
-                    nc.vector.tensor_tensor(out=halves(rot), in0=halves(s), in1=both_halves(tab[:, 1, :, :]), op=ALU.mult)
+        def rope_products(hw, between):
+            by_cos = outp.tile([P, TT, HS], F32, name="o", tag="o")
+            by_sin = outp.tile([P, TT, HS], F32, name="rot", tag="rot")
+            rope_terms[hw] = (by_cos, by_sin)
+            nc.vector.tensor_tensor(out=by_halves(by_cos), in0=by_halves(silu_out[hw]), in1=for_both_halves(tables[:, 0, :, :]), op=ALU.mult)
+            between()
+            nc.vector.tensor_tensor(out=by_halves(by_sin), in0=by_halves(silu_out[hw]), in1=for_both_halves(tables[:, 1, :, :]), op=ALU.mult)
 
-        def st_rope_add(hw):
-            grp, r = divmod(hw, 6)
-            if r == 5:
+        def rope_sum(hw):
+            grp, r = divmod(hw, GROUP)
+            if r == GROUP - 1:
                 return
-            if TAIL >= 4 and hw >= V_ADD_FROM:
-                return
-            o, rot = ropes[hw]
+            by_cos, by_sin = rope_terms[hw]
             fin = outp.tile([P, TT, HS], F32, name="fin", tag="fin")
-            eng = nc.vector if hw >= V_ADD_FROM else nc.gpsimd
-            if TAIL >= 3 and hw >= V_ADD_FROM:
-                for b in range(2):
-                    tsl = slice(b * 4, (b + 1) * 4)
-                    eng.tensor_tensor(out=fin[:, tsl, 0:HALF], in0=o[:, tsl, 0:HALF], in1=rot[:, tsl, HALF:HS], op=ALU.subtract)
-                    eng.tensor_tensor(out=fin[:, tsl, HALF:HS], in0=o[:, tsl, HALF:HS], in1=rot[:, tsl, 0:HALF], op=ALU.add)
-                    nc.sync.dma_start(out=k_view[:, tsl, grp, :], in_=fin[:, tsl, :])
-                return
-            if RA1:
-                eng.tensor_tensor(out=fin[:], in0=o[:], in1=rot[:], op=ALU.add)
-            else:
-                eng.tensor_tensor(out=fin[:, :, 0:HALF], in0=o[:, :, 0:HALF], in1=rot[:, :, HALF:HS], op=ALU.subtract)
-                eng.tensor_tensor(out=fin[:, :, HALF:HS], in0=o[:, :, HALF:HS], in1=rot[:, :, 0:HALF], op=ALU.add)
-            if r == 4:
+            eng = nc.vector if hw >= LAST_ROPE_HEAD else nc.gpsimd
+            eng.tensor_tensor(out=fin[:, :, 0:HALF], in0=by_cos[:, :, 0:HALF], in1=by_sin[:, :, HALF:HS], op=ALU.subtract)
+            eng.tensor_tensor(out=fin[:, :, HALF:HS], in0=by_cos[:, :, HALF:HS], in1=by_sin[:, :, 0:HALF], op=ALU.add)
+            if r == QUERIES:
                 nc.sync.dma_start(out=k_view[:, :, grp, :], in_=fin[:])
             else:
-                nc.sync.dma_start(out=q_view[:, :, grp * 4 + r, :], in_=fin[:])
+                nc.sync.dma_start(out=q_view[:, :, grp * QUERIES + r, :], in_=fin[:])
+
+        w_widen(0)
+        w_widen(1)
+        x_turn(0, "VVVV")
+        w_interleave(0)
+        w_interleave(1)
+        x_quantize(0)
+        w_quantize(1)
+        w_widen(2)
+        w_widen(3)
+        x_turn(1, "SVSV")
+        w_widen(4)
+        w_interleave(2)
+        w_interleave(3)
+        x_quantize(1)
+        w_quantize(3)
+        next_piece = {"widen": 5, "interleave": 4, "quantize": 4}
+
+        def advance(stage, work, upto):
+            for piece in range(next_piece[stage], upto + 1):
+                work(piece)
+            next_piece[stage] = max(next_piece[stage], upto + 1)
 
         def nothing():
             return None
 
-        if HEAD == 0:
-            w_widen(0)
-            w_widen(1)
-            x_turn(0, "VVVV")
-            w_interleave(0)
-            x_quant(0)
-            w_quant(0)
-            w_interleave(1)
-            for k in range(2, LEAD_W - 1):
-                w_widen(k)
-            x_turn(1, "SVSV")
-            w_quant(1)
-            x_quant(1)
-            for k in range(2, LEAD_I - 1):
-                w_interleave(k)
-                if k < LEAD_Q - 1:
-                    w_quant(k)
-            tables_gpsimd()
-        elif HEAD == 2:
-            w_widen(0)
-            w_widen(1)
-            x_turn(0, "VVVV")
-            w_interleave(0)
-            w_interleave(1)
-            x_quant(0)
-            if not WQ0_LATE:
-                w_quant(0)
-                w_quant(1)
-            for k in range(2, HW_A):
-                w_widen(k)
-            x_turn(1, X1ENG)
-            for k in range(HW_A, LEAD_W - 1):
-                w_widen(k)
-            if WIDE2:
-                w_widen_block(None)
-            if WQ0_LATE:
-                x_quant(1)
-                w_quant(0)
-                w_quant(1)
-            w_interleave(2)
-            w_interleave(3)
-            if not WQ0_LATE:
-                x_quant(1)
-            w_quant(2)
-            w_quant(3)
-            for k in range(4, LEAD_I - 1):
-                w_interleave(k)
-            for k in range(4, LEAD_Q - 1):
-                w_quant(k)
-            tables_gpsimd()
-        else:
-            w_widen(0)
-            w_widen(1)
-            x_turn(0, "VVVV")
-            w_interleave(0)
-            w_interleave(1)
-            x_quant(0)
-            w_quant(0)
-            w_quant(1)
-            for k in range(2, HW_A):
-                w_widen(k)
-            x_turn(1, X1ENG, X1A)
-            st_mx(0, (0,))
-            st_mx(1, (0,))
-            x_turn(1, X1ENG, X1B)
-            st_s_taps(0, (0,))
-            st_s_taps(1, (0,))
-            for k in range(HW_A, LEAD_W - 1):
-                w_widen(k)
-            w_interleave(2)
-            w_interleave(3)
-            if XQ_FIRST:
-                x_quant(1)
-            st_v_taps(0, nothing, (0,))
-            st_v_taps(1, nothing, (0,))
-            if not XQ_FIRST:
-                x_quant(1)
-            w_quant(2)
-            w_quant(3)
-            for k in range(4, LEAD_I - 1):
-                w_interleave(k)
-            for k in range(4, LEAD_Q - 1):
-                w_quant(k)
-            tables_gpsimd()
-
-        for i in range(NHEADS + max(LR, LA) + 1):
-            if i < NHEADS and HEAD == 1 and i < 2:
-                st_mx(i, (1,))
-                st_s_taps(i, (1,))
-            elif i < NHEADS:
-                st_mx(i)
-                st_s_taps(i)
-            if not BG_LATE:
-                for n, hw in enumerate(DIAG):
-                    for tt in range(TT):
-                        if i == BG_START[n] + (BG_NUM * tt) // BG_DEN:
-                            st_diag_tile(hw, tt)
+        for i in range(NHEADS + 1):
+            if i < NHEADS:
+                project(i)
+                taps_on_scalar(i)
             if i == 2:
-                tables_tensor()
-                if RA1:
-                    tables_tensor2()
-            def widen_now():
-                if i == 0:
-                    w_widen(LEAD_W - 1)
-                w_widen(i + LEAD_W)
-                if WIDE2:
-                    w_widen_block(i)
-
-            if not WW_LAST:
-                widen_now()
+                tables_to_psum()
+            advance("widen", w_widen, i + WIDEN_AHEAD)
 
             def w_step():
-                w_quant(i - 1 + LEAD_Q)
-                w_interleave(i - 1 + LEAD_I)
+                advance("quantize", w_quantize, i + QUANTIZE_AHEAD)
+                advance("interleave", w_interleave, i + INTERLEAVE_AHEAD)
 
-            if 0 <= i - LR < NHEADS and (i - LR) % 6 != 5:
-                st_rope_products(i - LR, w_step)
+            roped = i - 2
+            if 0 <= roped and roped % GROUP != GROUP - 1:
+                rope_products(roped, w_step)
                 if i < NHEADS:
-                    st_v_taps(i, nothing)
-            elif i < NHEADS and HEAD == 1 and i < 2:
-                w_step()
-                st_v_taps(i, nothing, (1,))
-            elif i < NHEADS:
-                st_v_taps(i, w_step)
-            if i in P2:
-                st_g_taps(i)
-            if i + 2 in DIAG and not DIAG_ON_V:
-                diag_matrices(i + 2)
-            late_add = TAIL >= 1 and i >= NHEADS
-            if 0 <= i - LA < NHEADS and not late_add:
-                st_rope_add(i - LA)
-            if 0 <= i - 1 < NHEADS and i - 1 not in DIAG:
-                st_tr(i - 1)
-                st_ss_bank(i - 1, 0)
-                st_ss_bank(i - 1, 1)
-            if 0 <= i - LA < NHEADS and late_add:
-                st_rope_add(i - LA)
-            if WW_LAST:
-                widen_now()
-            if BG_LATE:
-                for n, hw in enumerate(DIAG):
-                    for tt in range(TT):
-                        if i == BG_START[n] + (BG_NUM * tt) // BG_DEN:
-                            st_diag_tile(hw, tt)
-            for n, hw in enumerate(DIAG):
-                if i == BG_START[n] + (BG_NUM * 3) // BG_DEN + BG_SS:
-                    st_ss_bank(hw, 0)
-                if i == BG_START[n] + (BG_NUM * 7) // BG_DEN + BG_SS:
-                    st_ss_bank(hw, 1)
+                    taps_on_vector(i, nothing)
+            else:
+                taps_on_vector(i, w_step)
+            draining = i == NHEADS
+            if 0 <= roped and not draining:
+                rope_sum(roped)
+            if 1 <= i:
+                turn_and_add(i - 1)
+                silu(i - 1, 0)
+                silu(i - 1, 1)
+            if draining:
+                rope_sum(roped)

@@ -38,9 +38,24 @@ NPIECES = (NCOL // PIECE) * PASSES
 WIDEN_AHEAD = 6
 INTERLEAVE_AHEAD = 4
 QUANTIZE_AHEAD = 3
+LEAD = 8
 TAP_SETS = 3
-VECTOR_HEAVY = (0, 1)
-SCALAR_HEAVY = (21, 22, 23)
+VHEAVY = (0, 1, 5, 11, 17)
+SHEAVY = (22, 23)
+PB = 4
+CB = 3
+XT0 = "VVVV"
+XT1 = 'SSSS'
+XQ = 2
+PEORD = 1
+SORD = 1
+VO = 1
+RSPREAD = 3
+PREQ = 0
+W512 = 0
+OB = 4
+TBL = 1
+WPB = 4
 LAST_ROPE_HEAD = 22
 
 
@@ -49,10 +64,10 @@ def tile_gpt_pa_kernel(tc, x, Wqkv_bytes, Wqkv_scale, q_conv_w, k_conv_w, v_conv
     with ExitStack() as ctx:
         keep = ctx.enter_context(tc.tile_pool(name="keep", bufs=1))
         wstage = ctx.enter_context(tc.tile_pool(name="wstage", bufs=3))
-        outp = ctx.enter_context(tc.tile_pool(name="outp", bufs=3))
+        outp = ctx.enter_context(tc.tile_pool(name="outp", bufs=OB))
         psum_t = ctx.enter_context(tc.psum_pool(name="psum_t", bufs=1))
-        psum_p = ctx.enter_context(tc.psum_pool(name="psum_p", bufs=4))
-        psum_c = ctx.enter_context(tc.psum_pool(name="psum_c", bufs=3))
+        psum_p = ctx.enter_context(tc.psum_pool(name="psum_p", bufs=PB))
+        psum_c = ctx.enter_context(tc.psum_pool(name="psum_c", bufs=CB))
         ctx.enter_context(tc.manual_schedule())
 
         wbytes = []
@@ -67,14 +82,16 @@ def tile_gpt_pa_kernel(tc, x, Wqkv_bytes, Wqkv_scale, q_conv_w, k_conv_w, v_conv
         ident = keep.tile([P, P], F32, name="ident", tag="ident")
         identb = keep.tile([P, P], BF16, name="identb", tag="identb")
         warm = keep.tile([P, 1], F32, name="warm", tag="warm")
-        sum_a = []
-        sum_b = []
+        even_part = []
+        odd_part = []
+        both_part = []
+        more_part = []
         for st in range(TAP_SETS):
-            sum_a.append(keep.tile([P, T], F32, name="sum_a%d" % st, tag="sum_a%d" % st))
-            sum_b.append(keep.tile([P, T], F32, name="sum_b%d" % st, tag="sum_b%d" % st))
-        sum_c = []
-        for st in range(TAP_SETS):
-            sum_c.append(keep.tile([P, T], F32, name="sum_c%d" % st, tag="sum_c%d" % st))
+            even_part.append(keep.tile([P, BANK], F32, name="even%d" % st, tag="even%d" % st))
+            odd_part.append(keep.tile([P, LEAD + BANK], F32, name="odd%d" % st, tag="odd%d" % st))
+            both_part.append(keep.tile([P, BANK], F32, name="both%d" % st, tag="both%d" % st))
+            more_part.append(keep.tile([P, BANK], F32, name="more%d" % st, tag="more%d" % st))
+        both_w = keep.tile([P, NHEADS, 2], F32, name="both_w", tag="both_w")
         x_grouped = []
         x_codes = []
         x_scales = []
@@ -92,7 +109,7 @@ def tile_gpt_pa_kernel(tc, x, Wqkv_bytes, Wqkv_scale, q_conv_w, k_conv_w, v_conv
         conv_by_tap = keep.tile([P, TAPS, HS], BF16, name="conv_by_tap", tag="conv_by_tap")
 
         w_view = Wqkv_bytes.rearrange("(g p t) n -> g p t n", p=P, t=PACK)
-        x_view = x.rearrange("b (tt p) k -> (b tt) p k", p=P)
+        x_view = x.rearrange("b (tq p two) k -> two (b tq) p k", p=P, two=2)
 
         def load_w(li):
             c0, width = W_LOADS[li]
@@ -108,14 +125,16 @@ def tile_gpt_pa_kernel(tc, x, Wqkv_bytes, Wqkv_scale, q_conv_w, k_conv_w, v_conv
         nc.vector.memset(conv_rows[64:128, :], 0.0)
         nc.sync.dma_start(out=wscale[:], in_=Wqkv_scale.rearrange("(g p t) o -> p g (t o)", p=P, t=PACK))
         load_w(0)
-        for tt in range(TILES):
-            nc.sync.dma_start(out=xraw[tt][:], in_=x_view[tt])
+        for tq in range(TILES):
+            nc.sync.dma_start(out=xraw[tq][:], in_=x_view[0][tq])
         load_w(1)
-        for tt in range(TILES, TT):
-            nc.sync.dma_start(out=xraw[tt][:], in_=x_view[tt])
+        for tq in range(TILES):
+            nc.sync.dma_start(out=xraw[TILES + tq][:], in_=x_view[1][tq])
         load_w(2)
-        nc.sync.dma_start(out=tables_sb[:, 0, :, :], in_=cos.rearrange("(tt p) i -> p tt i", p=P))
-        nc.sync.dma_start(out=tables_sb[:, 1, :, :], in_=sin.rearrange("(tt p) i -> p tt i", p=P))
+        for n, table in enumerate((cos, sin)):
+            rows = table.rearrange("(tq p two) i -> two p tq i", p=P, two=2)
+            for hf in range(HALVES):
+                nc.sync.dma_start(out=tables_sb[:, n, hf * TILES:(hf + 1) * TILES, :], in_=rows[hf])
         for li in range(3, len(W_LOADS)):
             load_w(li)
 
@@ -124,8 +143,8 @@ def tile_gpt_pa_kernel(tc, x, Wqkv_bytes, Wqkv_scale, q_conv_w, k_conv_w, v_conv
         make_identity(nc, identb[:])
         make_identity(nc, ident[:])
         for st in range(TAP_SETS):
-            nc.gpsimd.memset(sum_a[st][:, 0:8], 0.0)
-            nc.gpsimd.memset(sum_c[st][:, 0:8], 0.0)
+            nc.gpsimd.memset(odd_part[st][:, 0:LEAD], 0.0)
+            nc.gpsimd.memset(more_part[st][:, 0:8], 0.0)
         nc.vector.tensor_copy(out=conv_by_tap[:], in_=conv_rows[:].rearrange("p (d j) -> p j d", j=TAPS))
         conv_t = psum_c.tile([P, TAPS, HS], BF16, name="conv_t", tag="cbank")
         for j in range(TAPS):
@@ -134,6 +153,8 @@ def tile_gpt_pa_kernel(tc, x, Wqkv_bytes, Wqkv_scale, q_conv_w, k_conv_w, v_conv
         nc.vector.tensor_copy(out=conv_w_groups[:, :, 0:QUERIES, :], in_=conv_t[:, :, 0:16].rearrange("p j (grp r) -> p grp r j", r=QUERIES))
         nc.vector.tensor_copy(out=conv_w_groups[:, :, QUERIES, :], in_=conv_t[:, :, 16:20].rearrange("p j grp -> p grp j"))
         nc.vector.tensor_copy(out=conv_w_groups[:, :, QUERIES + 1, :], in_=conv_t[:, :, 20:24].rearrange("p j grp -> p grp j"))
+
+        nc.vector.scalar_tensor_tensor(out=both_w[:], in0=conv_w[:, :, 0:TAPS:2], scalar=-1.0, in1=conv_w[:, :, 1:TAPS:2], op0=ALU.mult, op1=ALU.subtract)
 
         def tables_to_psum():
             for table in range(2):
@@ -161,12 +182,14 @@ def tile_gpt_pa_kernel(tc, x, Wqkv_bytes, Wqkv_scale, q_conv_w, k_conv_w, v_conv
                     nc.scalar.copy(out=dst, in_=src)
 
         def x_quantize(hf):
-            for g in range(PASSES):
-                nc.vector.quantize_mx(
-                    out=x_codes[hf][:, g, :].bitcast(FP8X4),
-                    scales=x_scales[hf][:, g, :],
-                    in_=x_grouped[hf][:, g, :, :].rearrange("p c t -> p (c t)"),
-                )
+            w = BANK // XQ
+            for q in range(XQ):
+                for g in range(PASSES):
+                    nc.vector.quantize_mx(
+                        out=x_codes[hf][:, g, q * w:(q + 1) * w].bitcast(FP8X4),
+                        scales=x_scales[hf][:, g, q * w:(q + 1) * w],
+                        in_=x_grouped[hf][:, g, q * w:(q + 1) * w, :].rearrange("p c t -> p (c t)"),
+                    )
 
         w_planes = {}
         w_grouped = {}
@@ -178,7 +201,7 @@ def tile_gpt_pa_kernel(tc, x, Wqkv_bytes, Wqkv_scale, q_conv_w, k_conv_w, v_conv
             c0 = pair * PIECE
             li = max(i for i in range(len(W_LOADS)) if W_LOADS[i][0] <= c0)
             off = c0 - W_LOADS[li][0]
-            w_planes[piece] = wstage.tile([P, PACK, PIECE], BF16, name="wp", tag="wp")
+            w_planes[piece] = wstage.tile([P, PACK, PIECE], BF16, name="wp", tag="wp", bufs=WPB)
             for t in range(PACK):
                 nc.scalar.activation(
                     out=w_planes[piece][:, t, :],
@@ -207,101 +230,100 @@ def tile_gpt_pa_kernel(tc, x, Wqkv_bytes, Wqkv_scale, q_conv_w, k_conv_w, v_conv
                 in_=w_grouped[pair][:].rearrange("p g n t -> p (g n t)"),
             )
 
-        q_view = out_0.rearrange("b (tt p) h d -> p (b tt) h d", p=P)
-        k_view = out_1.rearrange("b (tt p) h d -> p (b tt) h d", p=P)
-        v_view = out_2.rearrange("b (tt p) h d -> p (b tt) h d", p=P)
+        q_view = out_0.rearrange("b (tq p two) h d -> two p (b tq) h d", p=P, two=2)
+        k_view = out_1.rearrange("b (tq p two) h d -> two p (b tq) h d", p=P, two=2)
+        v_view = out_2.rearrange("b (tq p two) h d -> two p (b tq) h d", p=P, two=2)
         proj = {}
         conv_sum = {}
         silu_out = {}
         rope_terms = {}
 
         def project(hw):
+            for hf in range(HALVES):
+                proj[(hw, hf)] = psum_p.tile([P, BANK], F32, name="acc", tag="pbank")
+                multiply(hw, proj[(hw, hf)], (hf,))
+
+        def multiply(hw, acc, halves):
             pair = (hw * HS) // PIECE
             off = hw * HS - pair * PIECE
             cols = slice(off, off + HS)
-            for hf in range(HALVES):
-                acc = psum_p.tile([P, BANK], F32, name="acc", tag="pbank")
-                proj[(hw, hf)] = acc
-                for g in range(PASSES):
-                    nc.tensor.matmul_mx(
-                        out=acc[:],
-                        lhsT=w_codes[pair][:, g, cols].bitcast(FP8X4),
-                        lhsT_scale=w_scales[pair][:, g, cols],
-                        rhs=x_codes[hf][:, g, :].bitcast(FP8X4),
-                        rhs_scale=x_scales[hf][:, g, :],
-                        start=(g == 0),
-                        stop=(g == PASSES - 1),
-                    )
+            passes = [(hf, g) for hf in halves for g in range(PASSES)]
+            for n, (hf, g) in enumerate(passes):
+                nc.tensor.matmul_mx(
+                    out=acc[:],
+                    lhsT=w_codes[pair][:, g, cols].bitcast(FP8X4),
+                    lhsT_scale=w_scales[pair][:, g, cols],
+                    rhs=x_codes[hf][:, g, :].bitcast(FP8X4),
+                    rhs_scale=x_scales[hf][:, g, :],
+                    start=(n == 0),
+                    stop=(n == len(passes) - 1),
+                )
 
-        def shifted(hf, j):
-            lo = TAPS - 1 - j + hf * BANK
-            return lo, min(lo + BANK, T)
+        def project_sum(hw):
+            proj[(hw, 2)] = psum_p.tile([P, BANK], F32, name="acc", tag="pbank")
+            multiply(hw, proj[(hw, 2)], (0, 1))
 
-        def scalar_product(hw, hf, dst, j):
-            lo, hi = shifted(hf, j)
-            nc.scalar.activation(out=dst[:, lo:hi], in_=proj[(hw, hf)][:, 0:hi - lo], func=ACT.Copy, scale=conv_w[:, hw, j:j + 1])
+        def scalar_product(out, in_, weight):
+            nc.scalar.activation(out=out, in_=in_, func=ACT.Copy, scale=weight)
 
-        def vector_multiply_add(hw, hf, dst, j):
-            lo, hi = shifted(hf, j)
-            nc.vector.scalar_tensor_tensor(
-                out=dst[:, lo:hi], in0=proj[(hw, hf)][:, 0:hi - lo], scalar=conv_w[:, hw, j:j + 1], in1=dst[:, lo:hi], op0=ALU.mult, op1=ALU.add
-            )
+        def vector_multiply_add(out, in0, weight, in1):
+            nc.vector.scalar_tensor_tensor(out=out, in0=in0, scalar=weight, in1=in1, op0=ALU.mult, op1=ALU.add)
+
+        def parts_of(hw):
+            st = hw % TAP_SETS
+            return even_part[st], odd_part[st], both_part[st], more_part[st]
 
         def taps_on_scalar(hw):
-            st = hw % TAP_SETS
-            for hf in range(HALVES):
-                if hw in VECTOR_HEAVY:
-                    scalar_product(hw, hf, sum_b[st], 3)
-                else:
-                    scalar_product(hw, hf, sum_a[st], 1)
-                    scalar_product(hw, hf, sum_b[st], 3)
-                    if hw in SCALAR_HEAVY:
-                        scalar_product(hw, hf, sum_c[st], 2)
+            even, odd, both, more = parts_of(hw)
+            scalar_product(even[:], proj[(hw, 0)][:], conv_w[:, hw, 3:4])
+            scalar_product(odd[:, LEAD:LEAD + BANK], proj[(hw, 1)][:], conv_w[:, hw, 2:3])
 
-        def taps_on_vector(hw, between):
-            st = hw % TAP_SETS
-            if hw in VECTOR_HEAVY:
-                for j in (2, 1, 0):
-                    for hf in range(HALVES):
-                        vector_multiply_add(hw, hf, sum_b[st], j)
-                    if j == 2:
-                        between()
-            else:
-                for hf in range(HALVES):
-                    vector_multiply_add(hw, hf, sum_a[st], 0)
-                    if hw not in SCALAR_HEAVY:
-                        vector_multiply_add(hw, hf, sum_b[st], 2)
-                    if hf == 0:
-                        between()
+        def sum_taps_on_scalar(hw):
+            even, odd, both, more = parts_of(hw)
+            if hw not in VHEAVY:
+                scalar_product(both[:], proj[(hw, 2)][:], both_w[:, hw, 1:2])
+            if hw in SHEAVY:
+                scalar_product(more[:, 1:BANK], proj[(hw, 2)][:, 0:BANK - 1], both_w[:, hw, 0:1])
+
+        def taps_on_vector(hw):
+            even, odd, both, more = parts_of(hw)
+            vector_multiply_add(even[:, 1:BANK], proj[(hw, 0)][:, 0:BANK - 1], conv_w[:, hw, 1:2], even[:, 1:BANK])
+            vector_multiply_add(odd[:, LEAD + 1:LEAD + BANK], proj[(hw, 1)][:, 0:BANK - 1], conv_w[:, hw, 0:1], odd[:, LEAD + 1:LEAD + BANK])
+
+        def sum_taps_on_vector(hw):
+            even, odd, both, more = parts_of(hw)
+            if hw in VHEAVY:
+                vector_multiply_add(both[:], proj[(hw, 2)][:], both_w[:, hw, 1:2], even[:])
+            if hw not in SHEAVY:
+                vector_multiply_add(both[:, 1:BANK], proj[(hw, 2)][:, 0:BANK - 1], both_w[:, hw, 0:1], both[:, 1:BANK])
 
         def turn_and_add(hw):
-            st = hw % TAP_SETS
-            parts = [sum_b[st]]
-            if hw not in VECTOR_HEAVY:
-                parts = [sum_a[st]] + ([sum_c[st]] if hw in SCALAR_HEAVY else []) + parts
+            even, odd, both, more = parts_of(hw)
             conv_sum[hw] = []
             for hf in range(HALVES):
                 cv = psum_c.tile([P, TILES, HS], F32, name="cv", tag="cbank")
                 conv_sum[hw].append(cv)
                 for tq in range(TILES):
-                    tt = hf * TILES + tq
+                    c0 = tq * P
+                    if hf == 0:
+                        parts = [even[:, c0:c0 + P], odd[:, LEAD - 1 + c0:LEAD - 1 + c0 + P]]
+                    else:
+                        parts = [odd[:, LEAD + c0:LEAD + c0 + P], both[:, c0:c0 + P]]
+                        if hw not in VHEAVY:
+                            parts = [even[:, c0:c0 + P]] + parts
+                        if hw in SHEAVY:
+                            parts = parts + [more[:, c0:c0 + P]]
                     for n, part in enumerate(parts):
-                        nc.tensor.matmul(
-                            out=cv[:, tq, :], lhsT=part[:, tt * P:(tt + 1) * P], rhs=ident[:], is_transpose=True, start=(n == 0), stop=(n == len(parts) - 1)
-                        )
+                        nc.tensor.matmul(out=cv[:, tq, :], lhsT=part, rhs=ident[:], is_transpose=True, start=(n == 0), stop=(n == len(parts) - 1))
 
         def silu(hw, hf):
             if hf == 0:
                 silu_out[hw] = outp.tile([P, TT, HS], F32, name="s", tag="s")
             tiles = slice(hf * TILES, (hf + 1) * TILES)
-            nc.scalar.activation(out=silu_out[hw][:, tiles, :], in_=conv_sum[hw][hf][:], func=ACT.Silu)
+            nc.scalar.activation(out=silu_out[hw][:, tiles, :], in_=conv_sum[hw][hf][:], func=ACT.Silu, scale=1.0 if hf == 0 else -1.0)
             grp, r = divmod(hw, GROUP)
-            if r != GROUP - 1:
-                return
-            if hw == NHEADS - 1:
-                nc.sync.dma_start(out=v_view[:, tiles, grp, :], in_=silu_out[hw][:, tiles, :])
-            elif hf == HALVES - 1:
-                nc.sync.dma_start(out=v_view[:, :, grp, :], in_=silu_out[hw][:])
+            if r == GROUP - 1:
+                nc.sync.dma_start(out=v_view[hf][:, :, grp, :], in_=silu_out[hw][:, tiles, :])
 
         def by_halves(tile):
             return tile[:].rearrange("p tt (h i) -> p tt h i", h=2)
@@ -309,13 +331,11 @@ def tile_gpt_pa_kernel(tc, x, Wqkv_bytes, Wqkv_scale, q_conv_w, k_conv_w, v_conv
         def for_both_halves(table):
             return table.unsqueeze(2).to_broadcast([P, TT, 2, HALF])
 
-        def rope_products(hw, between):
-            by_cos = outp.tile([P, TT, HS], F32, name="o", tag="o")
-            by_sin = outp.tile([P, TT, HS], F32, name="rot", tag="rot")
-            rope_terms[hw] = (by_cos, by_sin)
-            nc.vector.tensor_tensor(out=by_halves(by_cos), in0=by_halves(silu_out[hw]), in1=for_both_halves(tables[:, 0, :, :]), op=ALU.mult)
-            between()
-            nc.vector.tensor_tensor(out=by_halves(by_sin), in0=by_halves(silu_out[hw]), in1=for_both_halves(tables[:, 1, :, :]), op=ALU.mult)
+        def rope_product(hw, which):
+            name = "rot" if which else "o"
+            term = outp.tile([P, TT, HS], F32, name=name, tag=name)
+            rope_terms.setdefault(hw, []).append(term)
+            nc.vector.tensor_tensor(out=by_halves(term), in0=by_halves(silu_out[hw]), in1=for_both_halves(tables[:, which, :, :]), op=ALU.mult)
 
         def rope_sum(hw):
             grp, r = divmod(hw, GROUP)
@@ -326,27 +346,30 @@ def tile_gpt_pa_kernel(tc, x, Wqkv_bytes, Wqkv_scale, q_conv_w, k_conv_w, v_conv
             eng = nc.vector if hw >= LAST_ROPE_HEAD else nc.gpsimd
             eng.tensor_tensor(out=fin[:, :, 0:HALF], in0=by_cos[:, :, 0:HALF], in1=by_sin[:, :, HALF:HS], op=ALU.subtract)
             eng.tensor_tensor(out=fin[:, :, HALF:HS], in0=by_cos[:, :, HALF:HS], in1=by_sin[:, :, 0:HALF], op=ALU.add)
-            if r == QUERIES:
-                nc.sync.dma_start(out=k_view[:, :, grp, :], in_=fin[:])
-            else:
-                nc.sync.dma_start(out=q_view[:, :, grp * QUERIES + r, :], in_=fin[:])
+            for hf in range(HALVES):
+                tiles = slice(hf * TILES, (hf + 1) * TILES)
+                if r == QUERIES:
+                    nc.sync.dma_start(out=k_view[hf][:, :, grp, :], in_=fin[:, tiles, :])
+                else:
+                    nc.sync.dma_start(out=q_view[hf][:, :, grp * QUERIES + r, :], in_=fin[:, tiles, :])
 
         w_widen(0)
         w_widen(1)
-        x_turn(0, "VVVV")
+        x_turn(0, XT0)
         w_interleave(0)
         w_interleave(1)
         x_quantize(0)
         w_quantize(1)
         w_widen(2)
         w_widen(3)
-        x_turn(1, "SVSV")
+        x_turn(1, XT1)
         w_widen(4)
         w_interleave(2)
         w_interleave(3)
         x_quantize(1)
-        w_quantize(3)
-        next_piece = {"widen": 5, "interleave": 4, "quantize": 4}
+        if PREQ:
+            w_quantize(3)
+        next_piece = {"widen": 5, "interleave": 4, "quantize": 4 if PREQ else 2}
 
         def advance(stage, work, upto):
             for piece in range(next_piece[stage], upto + 1):
@@ -356,31 +379,58 @@ def tile_gpt_pa_kernel(tc, x, Wqkv_bytes, Wqkv_scale, q_conv_w, k_conv_w, v_conv
         def nothing():
             return None
 
+        ropes = {}
+        counts = [(2, 2, 2, 2, 2, 0), (2, 1, 2, 2, 1, 2), (2, 2, 1, 2, 1, 2), (1, 2, 2, 1, 2, 2)][RSPREAD]
+        todo = []
+        for i in range(NHEADS + 2):
+            if 0 <= i - 2 < NHEADS and (i - 2) % GROUP != GROUP - 1:
+                todo += [(i - 2, 0), (i - 2, 1)]
+            n = counts[(i - 2) % GROUP] if i < NHEADS - 2 else len(todo)
+            ropes[i] = todo[:n]
+            todo = todo[n:]
         for i in range(NHEADS + 1):
-            if i < NHEADS:
-                project(i)
-                taps_on_scalar(i)
-            if i == 2:
-                tables_to_psum()
-            advance("widen", w_widen, i + WIDEN_AHEAD)
+            live = i < NHEADS
+            draining = i == NHEADS
 
             def w_step():
                 advance("quantize", w_quantize, i + QUANTIZE_AHEAD)
                 advance("interleave", w_interleave, i + INTERLEAVE_AHEAD)
 
-            roped = i - 2
-            if 0 <= roped and roped % GROUP != GROUP - 1:
-                rope_products(roped, w_step)
-                if i < NHEADS:
-                    taps_on_vector(i, nothing)
-            else:
-                taps_on_vector(i, w_step)
-            draining = i == NHEADS
-            if 0 <= roped and not draining:
-                rope_sum(roped)
-            if 1 <= i:
+            if live:
+                project(i)
+                if PEORD == 2:
+                    project_sum(i)
+                taps_on_scalar(i)
+                if VO < 10:
+                    taps_on_vector(i)
+            if PEORD == 0 and 1 <= i:
                 turn_and_add(i - 1)
+            if live and PEORD != 2:
+                project_sum(i)
+            if PEORD >= 1 and 1 <= i:
+                turn_and_add(i - 1)
+            if i == TBL:
+                tables_to_psum()
+            if SORD == 2 and live:
+                sum_taps_on_scalar(i)
+            advance("widen", w_widen, i + WIDEN_AHEAD)
+            if SORD == 1 and live:
+                sum_taps_on_scalar(i)
+            if 1 <= i:
                 silu(i - 1, 0)
                 silu(i - 1, 1)
-            if draining:
-                rope_sum(roped)
+            if SORD == 0 and live:
+                sum_taps_on_scalar(i)
+            if VO % 10 == 0 or not ropes[i]:
+                w_step()
+            for n, (h, which) in enumerate(ropes[i]):
+                rope_product(h, which)
+                if n == 0 and VO % 10 == 1:
+                    w_step()
+            if live and VO >= 10:
+                taps_on_vector(i)
+            if live:
+                sum_taps_on_vector(i)
+            for h, which in ropes[i]:
+                if which:
+                    rope_sum(h)

@@ -38,24 +38,43 @@ NPIECES = (NCOL // PIECE) * PASSES
 WIDEN_AHEAD = 6
 INTERLEAVE_AHEAD = 4
 QUANTIZE_AHEAD = 3
-LEAD = 8
-TAP_SETS = 3
-VHEAVY = (0, 1, 5, 11, 17)
-SHEAVY = (22, 23)
+LEAD = 9
+TAP_SETS = 4
+
+
 PB = 4
 CB = 3
 XT0 = "VVVV"
-XT1 = 'SSSS'
+XT1 = "SSSS"
 XQ = 2
-PEORD = 1
 SORD = 1
 VO = 1
-RSPREAD = 3
+RSPREAD = 2
+MODES = 'VVF5FVF5FVF5FVF5FV555555'
+CONVLATE = 0
+PRE = "01XiIqw23Y4jJQ"
+SO = 'EOWMWst'
+VOR = 'rreowm'
+PO = 'EOS01'
+VOD = 'rrweom'
+SOD = 'EOMstWW'
+POD = 'EOS01'
+DORD = 0
+DIRECT = tuple(h for h in range(24) if MODES[h] in "D56")
+PLANES = 1
+VHEAVY = tuple(h for h in range(24) if MODES[h] == "V")
+SHEAVY = tuple(h for h in range(24) if MODES[h] == "S")
+WEXTRA = 0
+ODDM = 1
+SINT = ()
+GONE = 0
+GMERGE = 0
+DS = 0
 PREQ = 0
 W512 = 0
-OB = 4
+OB = 5
 TBL = 1
-WPB = 4
+WPB = 5
 LAST_ROPE_HEAD = 22
 
 
@@ -86,10 +105,12 @@ def tile_gpt_pa_kernel(tc, x, Wqkv_bytes, Wqkv_scale, q_conv_w, k_conv_w, v_conv
         odd_part = []
         both_part = []
         more_part = []
+        extra_part = []
         for st in range(TAP_SETS):
             even_part.append(keep.tile([P, BANK], F32, name="even%d" % st, tag="even%d" % st))
             odd_part.append(keep.tile([P, LEAD + BANK], F32, name="odd%d" % st, tag="odd%d" % st))
             both_part.append(keep.tile([P, BANK], F32, name="both%d" % st, tag="both%d" % st))
+            extra_part.append(keep.tile([P, BANK], F32, name="extra%d" % st, tag="extra%d" % st))
             more_part.append(keep.tile([P, BANK], F32, name="more%d" % st, tag="more%d" % st))
         both_w = keep.tile([P, NHEADS, 2], F32, name="both_w", tag="both_w")
         x_grouped = []
@@ -124,13 +145,14 @@ def tile_gpt_pa_kernel(tc, x, Wqkv_bytes, Wqkv_scale, q_conv_w, k_conv_w, v_conv
         nc.vector.memset(conv_rows[32:64, :], 0.0)
         nc.vector.memset(conv_rows[64:128, :], 0.0)
         nc.sync.dma_start(out=wscale[:], in_=Wqkv_scale.rearrange("(g p t) o -> p g (t o)", p=P, t=PACK))
-        load_w(0)
-        for tq in range(TILES):
-            nc.sync.dma_start(out=xraw[tq][:], in_=x_view[0][tq])
-        load_w(1)
-        for tq in range(TILES):
-            nc.sync.dma_start(out=xraw[TILES + tq][:], in_=x_view[1][tq])
-        load_w(2)
+        def load_x(tt):
+            nc.sync.dma_start(out=xraw[tt][:], in_=x_view[tt // TILES][tt % TILES])
+
+        for what in (("w0", "x0", "x1", "x2", "x3", "w1", "x4", "x5", "x6", "x7", "w2"), ("x0", "w0", "x1", "x2", "x3", "w1", "x4", "x5", "x6", "x7", "w2"), ("x0", "x1", "w0", "x2", "x3", "w1", "x4", "x5", "x6", "x7", "w2"), ("x0", "x1", "x2", "x3", "w0", "w1", "x4", "x5", "x6", "x7", "w2"), ("w0", "x0", "x1", "x2", "x3", "x4", "x5", "x6", "x7", "w1", "w2"))[DORD]:
+            if what[0] == "x":
+                load_x(int(what[1:]))
+            else:
+                load_w(int(what[1:]))
         for n, table in enumerate((cos, sin)):
             rows = table.rearrange("(tq p two) i -> two p tq i", p=P, two=2)
             for hf in range(HALVES):
@@ -145,16 +167,21 @@ def tile_gpt_pa_kernel(tc, x, Wqkv_bytes, Wqkv_scale, q_conv_w, k_conv_w, v_conv
         for st in range(TAP_SETS):
             nc.gpsimd.memset(odd_part[st][:, 0:LEAD], 0.0)
             nc.gpsimd.memset(more_part[st][:, 0:8], 0.0)
-        nc.vector.tensor_copy(out=conv_by_tap[:], in_=conv_rows[:].rearrange("p (d j) -> p j d", j=TAPS))
-        conv_t = psum_c.tile([P, TAPS, HS], BF16, name="conv_t", tag="cbank")
-        for j in range(TAPS):
-            nc.tensor.transpose(conv_t[:, j, :], conv_by_tap[:, j, :], identb[:])
-        conv_w_groups = conv_w[:].rearrange("p (grp r) j -> p grp r j", r=GROUP)
-        nc.vector.tensor_copy(out=conv_w_groups[:, :, 0:QUERIES, :], in_=conv_t[:, :, 0:16].rearrange("p j (grp r) -> p grp r j", r=QUERIES))
-        nc.vector.tensor_copy(out=conv_w_groups[:, :, QUERIES, :], in_=conv_t[:, :, 16:20].rearrange("p j grp -> p grp j"))
-        nc.vector.tensor_copy(out=conv_w_groups[:, :, QUERIES + 1, :], in_=conv_t[:, :, 20:24].rearrange("p j grp -> p grp j"))
+            nc.gpsimd.memset(extra_part[st][:, 0:8], 0.0)
+        def prepare_conv():
+            nc.vector.tensor_copy(out=conv_by_tap[:], in_=conv_rows[:].rearrange("p (d j) -> p j d", j=TAPS))
+            conv_t = psum_c.tile([P, TAPS, HS], BF16, name="conv_t", tag="cbank")
+            for j in range(TAPS):
+                nc.tensor.transpose(conv_t[:, j, :], conv_by_tap[:, j, :], identb[:])
+            conv_w_groups = conv_w[:].rearrange("p (grp r) j -> p grp r j", r=GROUP)
+            nc.vector.tensor_copy(out=conv_w_groups[:, :, 0:QUERIES, :], in_=conv_t[:, :, 0:16].rearrange("p j (grp r) -> p grp r j", r=QUERIES))
+            nc.vector.tensor_copy(out=conv_w_groups[:, :, QUERIES, :], in_=conv_t[:, :, 16:20].rearrange("p j grp -> p grp j"))
+            nc.vector.tensor_copy(out=conv_w_groups[:, :, QUERIES + 1, :], in_=conv_t[:, :, 20:24].rearrange("p j grp -> p grp j"))
 
-        nc.vector.scalar_tensor_tensor(out=both_w[:], in0=conv_w[:, :, 0:TAPS:2], scalar=-1.0, in1=conv_w[:, :, 1:TAPS:2], op0=ALU.mult, op1=ALU.subtract)
+            nc.vector.scalar_tensor_tensor(out=both_w[:], in0=conv_w[:, :, 0:TAPS:2], scalar=-1.0, in1=conv_w[:, :, 1:TAPS:2], op0=ALU.mult, op1=ALU.subtract)
+
+        if CONVLATE == 0:
+            prepare_conv()
 
         def tables_to_psum():
             for table in range(2):
@@ -194,15 +221,16 @@ def tile_gpt_pa_kernel(tc, x, Wqkv_bytes, Wqkv_scale, q_conv_w, k_conv_w, v_conv
         w_planes = {}
         w_grouped = {}
 
-        def w_widen(piece):
+        def w_widen(piece, plane=None):
             if not 0 <= piece < NPIECES:
                 return
             pair, g = divmod(piece, PASSES)
             c0 = pair * PIECE
             li = max(i for i in range(len(W_LOADS)) if W_LOADS[i][0] <= c0)
             off = c0 - W_LOADS[li][0]
-            w_planes[piece] = wstage.tile([P, PACK, PIECE], BF16, name="wp", tag="wp", bufs=WPB)
-            for t in range(PACK):
+            if plane in (None, 0):
+                w_planes[piece] = wstage.tile([P, PACK, PIECE], BF16, name="wp", tag="wp", bufs=WPB)
+            for t in range(PACK) if plane is None else (plane,):
                 nc.scalar.activation(
                     out=w_planes[piece][:, t, :],
                     in_=wbytes[li][:, g, t, off:off + PIECE].bitcast(FP8),
@@ -216,9 +244,12 @@ def tile_gpt_pa_kernel(tc, x, Wqkv_bytes, Wqkv_scale, q_conv_w, k_conv_w, v_conv
             pair, g = divmod(piece, PASSES)
             if g == 0:
                 w_grouped[pair] = wstage.tile([P, PASSES, PIECE, PACK], BF16, name="wg", tag="wg", bufs=1, align_bytes=64)
-            nc.gpsimd.tensor_scalar(
-                out=w_grouped[pair][:, g, :, :], in0=w_planes[piece][:].rearrange("p t n -> p n t"), scalar1=1.0, scalar2=0.0, op0=ALU.mult, op1=ALU.add
-            )
+            if piece in SINT:
+                nc.scalar.copy(out=w_grouped[pair][:, g, :, :], in_=w_planes[piece][:].rearrange("p t n -> p n t"))
+            else:
+                nc.gpsimd.tensor_scalar(
+                    out=w_grouped[pair][:, g, :, :], in0=w_planes[piece][:].rearrange("p t n -> p n t"), scalar1=1.0, scalar2=0.0, op0=ALU.mult, op1=ALU.add
+                )
 
         def w_quantize(piece):
             if not 0 <= piece < NPIECES or piece % PASSES != PASSES - 1:
@@ -237,6 +268,10 @@ def tile_gpt_pa_kernel(tc, x, Wqkv_bytes, Wqkv_scale, q_conv_w, k_conv_w, v_conv
         conv_sum = {}
         silu_out = {}
         rope_terms = {}
+
+        def project_one(hw, hf):
+            proj[(hw, hf)] = psum_p.tile([P, BANK], F32, name="acc", tag="pbank")
+            multiply(hw, proj[(hw, hf)], (hf,))
 
         def project(hw):
             for hf in range(HALVES):
@@ -273,6 +308,20 @@ def tile_gpt_pa_kernel(tc, x, Wqkv_bytes, Wqkv_scale, q_conv_w, k_conv_w, v_conv
             st = hw % TAP_SETS
             return even_part[st], odd_part[st], both_part[st], more_part[st]
 
+        def tap_on_scalar(hw, which):
+            even, odd, both, more = parts_of(hw)
+            if which == 0:
+                scalar_product(even[:], proj[(hw, 0)][:], conv_w[:, hw, 3:4])
+            else:
+                scalar_product(odd[:, LEAD:LEAD + BANK], proj[(hw, 1)][:], conv_w[:, hw, 2:3])
+
+        def tap_on_vector(hw, which):
+            even, odd, both, more = parts_of(hw)
+            if which == 0:
+                vector_multiply_add(even[:, 1:BANK], proj[(hw, 0)][:, 0:BANK - 1], conv_w[:, hw, 1:2], even[:, 1:BANK])
+            else:
+                vector_multiply_add(odd[:, LEAD + 1:LEAD + BANK], proj[(hw, 1)][:, 0:BANK - 1], conv_w[:, hw, 0:1], odd[:, LEAD + 1:LEAD + BANK])
+
         def taps_on_scalar(hw):
             even, odd, both, more = parts_of(hw)
             scalar_product(even[:], proj[(hw, 0)][:], conv_w[:, hw, 3:4])
@@ -280,6 +329,12 @@ def tile_gpt_pa_kernel(tc, x, Wqkv_bytes, Wqkv_scale, q_conv_w, k_conv_w, v_conv
 
         def sum_taps_on_scalar(hw):
             even, odd, both, more = parts_of(hw)
+            if hw in DIRECT:
+                scalar_product(both[:], proj[(hw, 1)][:], conv_w[:, hw, 3:4])
+                scalar_product(more[:], proj[(hw, 0)][:], conv_w[:, hw, 2:3])
+                if MODES[hw] == "5":
+                    scalar_product(extra_part[hw % TAP_SETS][:, 1:BANK], proj[(hw, 0)][:, 0:BANK - 1], conv_w[:, hw, 0:1])
+                return
             if hw not in VHEAVY:
                 scalar_product(both[:], proj[(hw, 2)][:], both_w[:, hw, 1:2])
             if hw in SHEAVY:
@@ -292,27 +347,40 @@ def tile_gpt_pa_kernel(tc, x, Wqkv_bytes, Wqkv_scale, q_conv_w, k_conv_w, v_conv
 
         def sum_taps_on_vector(hw):
             even, odd, both, more = parts_of(hw)
+            if hw in DIRECT:
+                vector_multiply_add(both[:, 1:BANK], proj[(hw, 1)][:, 0:BANK - 1], conv_w[:, hw, 1:2], both[:, 1:BANK])
+                if MODES[hw] != "5":
+                    vector_multiply_add(more[:, 1:BANK], proj[(hw, 0)][:, 0:BANK - 1], conv_w[:, hw, 0:1], more[:, 1:BANK])
+                return
             if hw in VHEAVY:
-                vector_multiply_add(both[:], proj[(hw, 2)][:], both_w[:, hw, 1:2], even[:])
+                vector_multiply_add(both[:], proj[(hw, 2)][:], both_w[:, hw, 1:2], odd[:, LEAD:LEAD + BANK] if ODDM else even[:])
             if hw not in SHEAVY:
                 vector_multiply_add(both[:, 1:BANK], proj[(hw, 2)][:, 0:BANK - 1], both_w[:, hw, 0:1], both[:, 1:BANK])
 
-        def turn_and_add(hw):
+        def turn_and_add(hw, only=None):
             even, odd, both, more = parts_of(hw)
-            conv_sum[hw] = []
-            for hf in range(HALVES):
+            if only in (None, 0):
+                conv_sum[hw] = []
+            for hf in range(HALVES) if only is None else (only,):
                 cv = psum_c.tile([P, TILES, HS], F32, name="cv", tag="cbank")
                 conv_sum[hw].append(cv)
                 for tq in range(TILES):
                     c0 = tq * P
+                    here = slice(c0, c0 + P)
+                    odd_now = odd[:, LEAD + c0:LEAD + c0 + P]
+                    odd_before = odd[:, LEAD - 1 + c0:LEAD - 1 + c0 + P]
                     if hf == 0:
-                        parts = [even[:, c0:c0 + P], odd[:, LEAD - 1 + c0:LEAD - 1 + c0 + P]]
+                        parts = [even[:, here], odd_before]
+                    elif hw in DIRECT:
+                        parts = [both[:, here], more[:, here]]
+                        if MODES[hw] == "5":
+                            parts.append(extra_part[hw % TAP_SETS][:, here])
+                    elif hw in VHEAVY:
+                        parts = [even[:, here], both[:, here]] if ODDM else [odd_now, both[:, here]]
                     else:
-                        parts = [odd[:, LEAD + c0:LEAD + c0 + P], both[:, c0:c0 + P]]
-                        if hw not in VHEAVY:
-                            parts = [even[:, c0:c0 + P]] + parts
+                        parts = [even[:, here], odd_now, both[:, here]]
                         if hw in SHEAVY:
-                            parts = parts + [more[:, c0:c0 + P]]
+                            parts.append(more[:, here])
                     for n, part in enumerate(parts):
                         nc.tensor.matmul(out=cv[:, tq, :], lhsT=part, rhs=ident[:], is_transpose=True, start=(n == 0), stop=(n == len(parts) - 1))
 
@@ -320,7 +388,7 @@ def tile_gpt_pa_kernel(tc, x, Wqkv_bytes, Wqkv_scale, q_conv_w, k_conv_w, v_conv
             if hf == 0:
                 silu_out[hw] = outp.tile([P, TT, HS], F32, name="s", tag="s")
             tiles = slice(hf * TILES, (hf + 1) * TILES)
-            nc.scalar.activation(out=silu_out[hw][:, tiles, :], in_=conv_sum[hw][hf][:], func=ACT.Silu, scale=1.0 if hf == 0 else -1.0)
+            nc.scalar.activation(out=silu_out[hw][:, tiles, :], in_=conv_sum[hw][hf][:], func=ACT.Silu, scale=1.0 if hf == 0 or hw in DIRECT else -1.0)
             grp, r = divmod(hw, GROUP)
             if r == GROUP - 1:
                 nc.sync.dma_start(out=v_view[hf][:, :, grp, :], in_=silu_out[hw][:, tiles, :])
@@ -335,7 +403,12 @@ def tile_gpt_pa_kernel(tc, x, Wqkv_bytes, Wqkv_scale, q_conv_w, k_conv_w, v_conv
             name = "rot" if which else "o"
             term = outp.tile([P, TT, HS], F32, name=name, tag=name)
             rope_terms.setdefault(hw, []).append(term)
-            nc.vector.tensor_tensor(out=by_halves(term), in0=by_halves(silu_out[hw]), in1=for_both_halves(tables[:, which, :, :]), op=ALU.mult)
+            if which and GONE:
+                s_t = silu_out[hw]
+                nc.vector.scalar_tensor_tensor(out=term[:, :, 0:HALF], in0=s_t[:, :, HALF:HS], scalar=-1.0, in1=tables[:, 1, :, :], op0=ALU.mult, op1=ALU.mult)
+                nc.vector.tensor_tensor(out=term[:, :, HALF:HS], in0=s_t[:, :, 0:HALF], in1=tables[:, 1, :, :], op=ALU.mult)
+            else:
+                nc.vector.tensor_tensor(out=by_halves(term), in0=by_halves(silu_out[hw]), in1=for_both_halves(tables[:, which, :, :]), op=ALU.mult)
 
         def rope_sum(hw):
             grp, r = divmod(hw, GROUP)
@@ -344,8 +417,11 @@ def tile_gpt_pa_kernel(tc, x, Wqkv_bytes, Wqkv_scale, q_conv_w, k_conv_w, v_conv
             by_cos, by_sin = rope_terms[hw]
             fin = outp.tile([P, TT, HS], F32, name="fin", tag="fin")
             eng = nc.vector if hw >= LAST_ROPE_HEAD else nc.gpsimd
-            eng.tensor_tensor(out=fin[:, :, 0:HALF], in0=by_cos[:, :, 0:HALF], in1=by_sin[:, :, HALF:HS], op=ALU.subtract)
-            eng.tensor_tensor(out=fin[:, :, HALF:HS], in0=by_cos[:, :, HALF:HS], in1=by_sin[:, :, 0:HALF], op=ALU.add)
+            if GONE:
+                eng.tensor_tensor(out=fin[:], in0=by_cos[:], in1=by_sin[:], op=ALU.add)
+            else:
+                eng.tensor_tensor(out=fin[:, :, 0:HALF], in0=by_cos[:, :, 0:HALF], in1=by_sin[:, :, HALF:HS], op=ALU.subtract)
+                eng.tensor_tensor(out=fin[:, :, HALF:HS], in0=by_cos[:, :, HALF:HS], in1=by_sin[:, :, 0:HALF], op=ALU.add)
             for hf in range(HALVES):
                 tiles = slice(hf * TILES, (hf + 1) * TILES)
                 if r == QUERIES:
@@ -353,22 +429,13 @@ def tile_gpt_pa_kernel(tc, x, Wqkv_bytes, Wqkv_scale, q_conv_w, k_conv_w, v_conv
                 else:
                     nc.sync.dma_start(out=q_view[hf][:, :, grp * QUERIES + r, :], in_=fin[:, tiles, :])
 
-        w_widen(0)
-        w_widen(1)
-        x_turn(0, XT0)
-        w_interleave(0)
-        w_interleave(1)
-        x_quantize(0)
-        w_quantize(1)
-        w_widen(2)
-        w_widen(3)
-        x_turn(1, XT1)
-        w_widen(4)
-        w_interleave(2)
-        w_interleave(3)
-        x_quantize(1)
-        if PREQ:
-            w_quantize(3)
+        steps = {
+            "0": lambda: w_widen(0), "1": lambda: w_widen(1), "2": lambda: w_widen(2), "3": lambda: w_widen(3), "4": lambda: w_widen(4),
+            "X": lambda: x_turn(0, XT0), "Y": lambda: x_turn(1, XT1), "i": lambda: w_interleave(0), "I": lambda: w_interleave(1), "j": lambda: w_interleave(2), "J": lambda: w_interleave(3),
+            "q": lambda: x_quantize(0), "Q": lambda: x_quantize(1), "w": lambda: w_quantize(1),
+        }
+        for c in PRE:
+            steps[c]()
         next_piece = {"widen": 5, "interleave": 4, "quantize": 4 if PREQ else 2}
 
         def advance(stage, work, upto):
@@ -379,58 +446,82 @@ def tile_gpt_pa_kernel(tc, x, Wqkv_bytes, Wqkv_scale, q_conv_w, k_conv_w, v_conv
         def nothing():
             return None
 
+        next_plane = [5 * PACK]
         ropes = {}
         counts = [(2, 2, 2, 2, 2, 0), (2, 1, 2, 2, 1, 2), (2, 2, 1, 2, 1, 2), (1, 2, 2, 1, 2, 2)][RSPREAD]
         todo = []
-        for i in range(NHEADS + 2):
-            if 0 <= i - 2 < NHEADS and (i - 2) % GROUP != GROUP - 1:
-                todo += [(i - 2, 0), (i - 2, 1)]
-            n = counts[(i - 2) % GROUP] if i < NHEADS - 2 else len(todo)
+        last = NHEADS + DS
+        for i in range(last + 1):
+            h = i - 2 - DS
+            if 0 <= h < NHEADS and h % GROUP != GROUP - 1:
+                todo += [(h, 0), (h, 1)]
+            n = counts[h % GROUP] if i < NHEADS - 2 + DS else len(todo)
             ropes[i] = todo[:n]
             todo = todo[n:]
-        for i in range(NHEADS + 1):
+        for i in range(last + 1):
             live = i < NHEADS
-            draining = i == NHEADS
+            turned = i - 1 - DS
 
             def w_step():
                 advance("quantize", w_quantize, i + QUANTIZE_AHEAD)
                 advance("interleave", w_interleave, i + INTERLEAVE_AHEAD)
 
-            if live:
-                project(i)
-                if PEORD == 2:
+            special = live and MODES[i] in "D56"
+            for c in (POD if special and POD else PO):
+                if c in "EO" and live:
+                    project_one(i, "EO".index(c))
+                elif c == "S" and live and i not in DIRECT:
                     project_sum(i)
-                taps_on_scalar(i)
-                if VO < 10:
-                    taps_on_vector(i)
-            if PEORD == 0 and 1 <= i:
-                turn_and_add(i - 1)
-            if live and PEORD != 2:
-                project_sum(i)
-            if PEORD >= 1 and 1 <= i:
-                turn_and_add(i - 1)
+                elif c in "01" and 0 <= turned:
+                    turn_and_add(turned, int(c))
             if i == TBL:
                 tables_to_psum()
-            if SORD == 2 and live:
-                sum_taps_on_scalar(i)
-            advance("widen", w_widen, i + WIDEN_AHEAD)
-            if SORD == 1 and live:
-                sum_taps_on_scalar(i)
-            if 1 <= i:
-                silu(i - 1, 0)
-                silu(i - 1, 1)
-            if SORD == 0 and live:
-                sum_taps_on_scalar(i)
-            if VO % 10 == 0 or not ropes[i]:
-                w_step()
-            for n, (h, which) in enumerate(ropes[i]):
-                rope_product(h, which)
-                if n == 0 and VO % 10 == 1:
+
+            def planes(k):
+                if not live:
+                    return
+                n0 = next_plane[0]
+                for n in range(n0, n0 + k):
+                    w_widen(n // PACK, n % PACK)
+                next_plane[0] = n0 + k
+
+            so = SOD if special and SOD else SO
+            total = max({"F": 4, "V": 6, "D": 2, "5": 2, "S": 2}[MODES[i]], PACK * (i + INTERLEAVE_AHEAD + 1) - next_plane[0]) if live else 0
+            nw = so.count("W")
+            done = 0
+            seen = 0
+            for c in so:
+                if c in "EO" and live:
+                    tap_on_scalar(i, "EO".index(c))
+                elif c == "M" and live:
+                    sum_taps_on_scalar(i)
+                elif c == "W":
+                    seen += 1
+                    k = total * seen // nw - done
+                    planes(k)
+                    done += k
+                elif c in "st" and 0 <= turned:
+                    silu(turned, "st".index(c))
+            todo_r = list(ropes[i])
+            wdone = False
+            vo = VOD if special and VOD else VOR
+            for c in vo:
+                if c == "r" and todo_r:
+                    h, which = todo_r.pop(0)
+                    rope_product(h, which)
+                elif c == "R":
+                    while todo_r:
+                        h, which = todo_r.pop(0)
+                        rope_product(h, which)
+                elif c == "w":
                     w_step()
-            if live and VO >= 10:
-                taps_on_vector(i)
-            if live:
-                sum_taps_on_vector(i)
+                elif c in "eo" and live:
+                    tap_on_vector(i, "eo".index(c))
+                elif c == "m" and live:
+                    sum_taps_on_vector(i)
+            while todo_r:
+                h, which = todo_r.pop(0)
+                rope_product(h, which)
             for h, which in ropes[i]:
                 if which:
                     rope_sum(h)

from contextlib import ExitStack

import concourse.mybir as mybir
from concourse.masks import make_identity

F32 = mybir.dt.float32
BF16 = mybir.dt.bfloat16
U32 = mybir.dt.uint32
U8 = mybir.dt.uint8
FP8 = mybir.dt.float8_e4m3fn
FP8X4 = mybir.dt.float8_e4m3fn_x4
ACT = mybir.ActivationFunctionType
ALU = mybir.AluOpType

P = 128
T = 1024
C = 1024
NCOL = 3072
HS = 128
HALF = HS // 2
TAPS = 4
PACK = 4
NHEADS = NCOL // HS
GROUP = 6
QUERIES = 4
PASSES = C // (P * PACK)
WORDS = P * PACK // 2
BANK = 512
HALVES = T // BANK
TT = T // P
TILES = TT // HALVES

FLOPS = 2 * T * C * NCOL

W_LOADS = [(0, 256), (256, 256), (512, 512), (1024, 512), (1536, 512), (2048, 512), (2560, 512)]
PIECE = 256
NPIECES = (NCOL // PIECE) * PASSES
WIDEN_AHEAD = 6
INTERLEAVE_AHEAD = 4
QUANTIZE_AHEAD = 3
LEAD = 9
TAP_SETS = 4


PB = 4
CB = 3
XT0 = "VVVV"
XT1 = "SSSS"
XQ = 2
SORD = 1
VO = 1
RSPREAD = 2
MODES = 'VVF5FVF5FVF5FVF5FV555555'
CONVLATE = 0
PRE = "01XiIqw23Y4jJQ"
SO = 'EOWMWst'
VOR = 'rreowm'
PO = 'EOS01'
VOD = 'rrweom'
SOD = 'EOMstWW'
POD = 'EOS01'
DORD = 0
DIRECT = tuple(h for h in range(24) if MODES[h] in "D56")
PLANES = 1
VHEAVY = tuple(h for h in range(24) if MODES[h] == "V")
SHEAVY = tuple(h for h in range(24) if MODES[h] == "S")
WEXTRA = 0
ODDM = 1
SINT = ()
GONE = 0
GMERGE = 0
DS = 0
PREQ = 0
W512 = 0
OB = 5
TBL = 1
WPB = 5
LAST_ROPE_HEAD = 22


def tile_gpt_pa_kernel(tc, x, Wqkv_bytes, Wqkv_scale, q_conv_w, k_conv_w, v_conv_w, cos, sin, out_0, out_1, out_2):
    nc = tc.nc
    with ExitStack() as ctx:
        keep = ctx.enter_context(tc.tile_pool(name="keep", bufs=1))
        wstage = ctx.enter_context(tc.tile_pool(name="wstage", bufs=3))
        outp = ctx.enter_context(tc.tile_pool(name="outp", bufs=OB))
        psum_t = ctx.enter_context(tc.psum_pool(name="psum_t", bufs=1))
        psum_p = ctx.enter_context(tc.psum_pool(name="psum_p", bufs=PB))
        psum_c = ctx.enter_context(tc.psum_pool(name="psum_c", bufs=CB))
        ctx.enter_context(tc.manual_schedule())

        wbytes = []
        for li, (c0, width) in enumerate(W_LOADS):
            wbytes.append(keep.tile([P, PASSES, PACK, width], U8, name="wbytes%d" % li, tag="wbytes%d" % li))
        xraw = []
        for tt in range(TT):
            xraw.append(keep.tile([P, C], BF16, name="xraw%d" % tt, tag="xraw%d" % tt))
        wscale = keep.tile([P, PASSES, PACK], F32, name="wscale", tag="wscale")
        conv_w = keep.tile([P, NHEADS, TAPS], F32, name="conv_w", tag="conv_w")
        tables_sb = keep.tile([P, 2, TT, HALF], BF16, name="tables_sb", tag="tables_sb")
        ident = keep.tile([P, P], F32, name="ident", tag="ident")
        identb = keep.tile([P, P], BF16, name="identb", tag="identb")
        warm = keep.tile([P, 1], F32, name="warm", tag="warm")
        even_part = []
        odd_part = []
        both_part = []
        more_part = []
        extra_part = []
        for st in range(TAP_SETS):
            even_part.append(keep.tile([P, BANK], F32, name="even%d" % st, tag="even%d" % st))
            odd_part.append(keep.tile([P, LEAD + BANK], F32, name="odd%d" % st, tag="odd%d" % st))
            both_part.append(keep.tile([P, BANK], F32, name="both%d" % st, tag="both%d" % st))
            extra_part.append(keep.tile([P, BANK], F32, name="extra%d" % st, tag="extra%d" % st))
            more_part.append(keep.tile([P, BANK], F32, name="more%d" % st, tag="more%d" % st))
        both_w = keep.tile([P, NHEADS, 2], F32, name="both_w", tag="both_w")
        x_grouped = []
        x_codes = []
        x_scales = []
        for hf in range(HALVES):
            x_grouped.append(keep.tile([P, PASSES, BANK, PACK], BF16, name="x_grouped%d" % hf, tag="x_grouped%d" % hf, align_bytes=64))
            x_codes.append(keep.tile([P, PASSES, BANK], U32, name="x_codes%d" % hf, tag="x_codes%d" % hf, align_bytes=64))
            x_scales.append(keep.tile([P, PASSES, BANK], U8, name="x_scales%d" % hf, tag="x_scales%d" % hf, align_bytes=64))
        w_codes = []
        w_scales = []
        for pair in range(NPIECES // PASSES):
            w_codes.append(keep.tile([P, PASSES, PIECE], U32, name="w_codes%d" % pair, tag="w_codes%d" % pair, align_bytes=64))
            w_scales.append(keep.tile([P, PASSES, PIECE], U8, name="w_scales%d" % pair, tag="w_scales%d" % pair, align_bytes=64))
        tables = psum_t.tile([P, 2, TT, HALF], BF16, name="tables", tag="tables")
        conv_rows = keep.tile([P, HS * TAPS], BF16, name="conv_rows", tag="conv_rows")
        conv_by_tap = keep.tile([P, TAPS, HS], BF16, name="conv_by_tap", tag="conv_by_tap")

        w_view = Wqkv_bytes.rearrange("(g p t) n -> g p t n", p=P, t=PACK)
        x_view = x.rearrange("b (tq p two) k -> two (b tq) p k", p=P, two=2)

        def load_w(li):
            c0, width = W_LOADS[li]
            for g in range(PASSES):
                nc.sync.dma_start(out=wbytes[li][:, g, :, :], in_=w_view[g][:, :, c0:c0 + width])

        q_rows = q_conv_w.rearrange("(h d) j -> h (d j)", d=P)
        nc.scalar.dma_start(out=conv_rows[0:16, :], in_=q_rows)
        nc.scalar.dma_start(out=conv_rows[16:20, :], in_=k_conv_w.rearrange("(h d) j -> h (d j)", d=P))
        nc.scalar.dma_start(out=conv_rows[20:24, :], in_=v_conv_w.rearrange("(h d) j -> h (d j)", d=P))
        nc.scalar.dma_start(out=conv_rows[24:32, :], in_=q_rows[0:8, :])
        nc.vector.memset(conv_rows[32:64, :], 0.0)
        nc.vector.memset(conv_rows[64:128, :], 0.0)
        nc.sync.dma_start(out=wscale[:], in_=Wqkv_scale.rearrange("(g p t) o -> p g (t o)", p=P, t=PACK))
        def load_x(tt):
            nc.sync.dma_start(out=xraw[tt][:], in_=x_view[tt // TILES][tt % TILES])

        for what in (("w0", "x0", "x1", "x2", "x3", "w1", "x4", "x5", "x6", "x7", "w2"), ("x0", "w0", "x1", "x2", "x3", "w1", "x4", "x5", "x6", "x7", "w2"), ("x0", "x1", "w0", "x2", "x3", "w1", "x4", "x5", "x6", "x7", "w2"), ("x0", "x1", "x2", "x3", "w0", "w1", "x4", "x5", "x6", "x7", "w2"), ("w0", "x0", "x1", "x2", "x3", "x4", "x5", "x6", "x7", "w1", "w2"))[DORD]:
            if what[0] == "x":
                load_x(int(what[1:]))
            else:
                load_w(int(what[1:]))
        for n, table in enumerate((cos, sin)):
            rows = table.rearrange("(tq p two) i -> two p tq i", p=P, two=2)
            for hf in range(HALVES):
                nc.sync.dma_start(out=tables_sb[:, n, hf * TILES:(hf + 1) * TILES, :], in_=rows[hf])
        for li in range(3, len(W_LOADS)):
            load_w(li)

        nc.vector.memset(warm[:], 0.0)
        nc.scalar.activation(out=warm[:], in_=warm[:], func=ACT.Silu)
        make_identity(nc, identb[:])
        make_identity(nc, ident[:])
        for st in range(TAP_SETS):
            nc.gpsimd.memset(odd_part[st][:, 0:LEAD], 0.0)
            nc.gpsimd.memset(more_part[st][:, 0:8], 0.0)
            nc.gpsimd.memset(extra_part[st][:, 0:8], 0.0)
        def prepare_conv():
            nc.vector.tensor_copy(out=conv_by_tap[:], in_=conv_rows[:].rearrange("p (d j) -> p j d", j=TAPS))
            conv_t = psum_c.tile([P, TAPS, HS], BF16, name="conv_t", tag="cbank")
            for j in range(TAPS):
                nc.tensor.transpose(conv_t[:, j, :], conv_by_tap[:, j, :], identb[:])
            conv_w_groups = conv_w[:].rearrange("p (grp r) j -> p grp r j", r=GROUP)
            nc.vector.tensor_copy(out=conv_w_groups[:, :, 0:QUERIES, :], in_=conv_t[:, :, 0:16].rearrange("p j (grp r) -> p grp r j", r=QUERIES))
            nc.vector.tensor_copy(out=conv_w_groups[:, :, QUERIES, :], in_=conv_t[:, :, 16:20].rearrange("p j grp -> p grp j"))
            nc.vector.tensor_copy(out=conv_w_groups[:, :, QUERIES + 1, :], in_=conv_t[:, :, 20:24].rearrange("p j grp -> p grp j"))

            nc.vector.scalar_tensor_tensor(out=both_w[:], in0=conv_w[:, :, 0:TAPS:2], scalar=-1.0, in1=conv_w[:, :, 1:TAPS:2], op0=ALU.mult, op1=ALU.subtract)

        if CONVLATE == 0:
            prepare_conv()

        def tables_to_psum():
            for table in range(2):
                nc.tensor.matmul(
                    out=tables[:, table, :, :].rearrange("p tt i -> p (tt i)"),
                    lhsT=identb[:],
                    rhs=tables_sb[:, table, :, :].rearrange("p tt i -> p (tt i)"),
                    start=True,
                    stop=True,
                )

        def x_turn(hf, engines):
            words_out = x_grouped[hf][:].rearrange("p g c t -> p (g c t)").bitcast(F32).rearrange("p (g c w) -> p g c w", g=PASSES, w=2)
            for tq in range(TILES):
                words = xraw[hf * TILES + tq][:].bitcast(F32)
                xt = psum_c.tile([P, PASSES, 2, P], F32, name="xt", tag="cbank")
                for g in range(PASSES):
                    for w in range(2):
                        nc.tensor.transpose(xt[:, g, w, :], words[:, WORDS * g + w:WORDS * (g + 1):2], ident[:])
                dst = words_out[:, :, tq * P:(tq + 1) * P, :]
                src = xt[:].rearrange("p g w c -> p g c w")
                if engines[tq] == "V":
                    nc.vector.tensor_copy(out=dst, in_=src)
                else:
                    nc.scalar.copy(out=dst, in_=src)

        def x_quantize(hf):
            w = BANK // XQ
            for q in range(XQ):
                for g in range(PASSES):
                    nc.vector.quantize_mx(
                        out=x_codes[hf][:, g, q * w:(q + 1) * w].bitcast(FP8X4),
                        scales=x_scales[hf][:, g, q * w:(q + 1) * w],
                        in_=x_grouped[hf][:, g, q * w:(q + 1) * w, :].rearrange("p c t -> p (c t)"),
                    )

        w_planes = {}
        w_grouped = {}

        def w_widen(piece, plane=None):
            if not 0 <= piece < NPIECES:
                return
            pair, g = divmod(piece, PASSES)
            c0 = pair * PIECE
            li = max(i for i in range(len(W_LOADS)) if W_LOADS[i][0] <= c0)
            off = c0 - W_LOADS[li][0]
            if plane in (None, 0):
                w_planes[piece] = wstage.tile([P, PACK, PIECE], BF16, name="wp", tag="wp", bufs=WPB)
            for t in range(PACK) if plane is None else (plane,):
                nc.scalar.activation(
                    out=w_planes[piece][:, t, :],
                    in_=wbytes[li][:, g, t, off:off + PIECE].bitcast(FP8),
                    func=ACT.Copy,
                    scale=wscale[:, g, t:t + 1],
                )

        def w_interleave(piece):
            if not 0 <= piece < NPIECES:
                return
            pair, g = divmod(piece, PASSES)
            if g == 0:
                w_grouped[pair] = wstage.tile([P, PASSES, PIECE, PACK], BF16, name="wg", tag="wg", bufs=1, align_bytes=64)
            if piece in SINT:
                nc.scalar.copy(out=w_grouped[pair][:, g, :, :], in_=w_planes[piece][:].rearrange("p t n -> p n t"))
            else:
                nc.gpsimd.tensor_scalar(
                    out=w_grouped[pair][:, g, :, :], in0=w_planes[piece][:].rearrange("p t n -> p n t"), scalar1=1.0, scalar2=0.0, op0=ALU.mult, op1=ALU.add
                )

        def w_quantize(piece):
            if not 0 <= piece < NPIECES or piece % PASSES != PASSES - 1:
                return
            pair = piece // PASSES
            nc.vector.quantize_mx(
                out=w_codes[pair][:].rearrange("p g n -> p (g n)").bitcast(FP8X4),
                scales=w_scales[pair][:].rearrange("p g n -> p (g n)"),
                in_=w_grouped[pair][:].rearrange("p g n t -> p (g n t)"),
            )

        q_view = out_0.rearrange("b (tq p two) h d -> two p (b tq) h d", p=P, two=2)
        k_view = out_1.rearrange("b (tq p two) h d -> two p (b tq) h d", p=P, two=2)
        v_view = out_2.rearrange("b (tq p two) h d -> two p (b tq) h d", p=P, two=2)
        proj = {}
        conv_sum = {}
        silu_out = {}
        rope_terms = {}

        def project_one(hw, hf):
            proj[(hw, hf)] = psum_p.tile([P, BANK], F32, name="acc", tag="pbank")
            multiply(hw, proj[(hw, hf)], (hf,))

        def project(hw):
            for hf in range(HALVES):
                proj[(hw, hf)] = psum_p.tile([P, BANK], F32, name="acc", tag="pbank")
                multiply(hw, proj[(hw, hf)], (hf,))

        def multiply(hw, acc, halves):
            pair = (hw * HS) // PIECE
            off = hw * HS - pair * PIECE
            cols = slice(off, off + HS)
            passes = [(hf, g) for hf in halves for g in range(PASSES)]
            for n, (hf, g) in enumerate(passes):
                nc.tensor.matmul_mx(
                    out=acc[:],
                    lhsT=w_codes[pair][:, g, cols].bitcast(FP8X4),
                    lhsT_scale=w_scales[pair][:, g, cols],
                    rhs=x_codes[hf][:, g, :].bitcast(FP8X4),
                    rhs_scale=x_scales[hf][:, g, :],
                    start=(n == 0),
                    stop=(n == len(passes) - 1),
                )

        def project_sum(hw):
            proj[(hw, 2)] = psum_p.tile([P, BANK], F32, name="acc", tag="pbank")
            multiply(hw, proj[(hw, 2)], (0, 1))

        def scalar_product(out, in_, weight):
            nc.scalar.activation(out=out, in_=in_, func=ACT.Copy, scale=weight)

        def vector_multiply_add(out, in0, weight, in1):
            nc.vector.scalar_tensor_tensor(out=out, in0=in0, scalar=weight, in1=in1, op0=ALU.mult, op1=ALU.add)

        def parts_of(hw):
            st = hw % TAP_SETS
            return even_part[st], odd_part[st], both_part[st], more_part[st]

        def tap_on_scalar(hw, which):
            even, odd, both, more = parts_of(hw)
            if which == 0:
                scalar_product(even[:], proj[(hw, 0)][:], conv_w[:, hw, 3:4])
            else:
                scalar_product(odd[:, LEAD:LEAD + BANK], proj[(hw, 1)][:], conv_w[:, hw, 2:3])

        def tap_on_vector(hw, which):
            even, odd, both, more = parts_of(hw)
            if which == 0:
                vector_multiply_add(even[:, 1:BANK], proj[(hw, 0)][:, 0:BANK - 1], conv_w[:, hw, 1:2], even[:, 1:BANK])
            else:
                vector_multiply_add(odd[:, LEAD + 1:LEAD + BANK], proj[(hw, 1)][:, 0:BANK - 1], conv_w[:, hw, 0:1], odd[:, LEAD + 1:LEAD + BANK])

        def taps_on_scalar(hw):
            even, odd, both, more = parts_of(hw)
            scalar_product(even[:], proj[(hw, 0)][:], conv_w[:, hw, 3:4])
            scalar_product(odd[:, LEAD:LEAD + BANK], proj[(hw, 1)][:], conv_w[:, hw, 2:3])

        def sum_taps_on_scalar(hw):
            even, odd, both, more = parts_of(hw)
            if hw in DIRECT:
                scalar_product(both[:], proj[(hw, 1)][:], conv_w[:, hw, 3:4])
                scalar_product(more[:], proj[(hw, 0)][:], conv_w[:, hw, 2:3])
                if MODES[hw] == "5":
                    scalar_product(extra_part[hw % TAP_SETS][:, 1:BANK], proj[(hw, 0)][:, 0:BANK - 1], conv_w[:, hw, 0:1])
                return
            if hw not in VHEAVY:
                scalar_product(both[:], proj[(hw, 2)][:], both_w[:, hw, 1:2])
            if hw in SHEAVY:
                scalar_product(more[:, 1:BANK], proj[(hw, 2)][:, 0:BANK - 1], both_w[:, hw, 0:1])

        def taps_on_vector(hw):
            even, odd, both, more = parts_of(hw)
            vector_multiply_add(even[:, 1:BANK], proj[(hw, 0)][:, 0:BANK - 1], conv_w[:, hw, 1:2], even[:, 1:BANK])
            vector_multiply_add(odd[:, LEAD + 1:LEAD + BANK], proj[(hw, 1)][:, 0:BANK - 1], conv_w[:, hw, 0:1], odd[:, LEAD + 1:LEAD + BANK])

        def sum_taps_on_vector(hw):
            even, odd, both, more = parts_of(hw)
            if hw in DIRECT:
                vector_multiply_add(both[:, 1:BANK], proj[(hw, 1)][:, 0:BANK - 1], conv_w[:, hw, 1:2], both[:, 1:BANK])
                if MODES[hw] != "5":
                    vector_multiply_add(more[:, 1:BANK], proj[(hw, 0)][:, 0:BANK - 1], conv_w[:, hw, 0:1], more[:, 1:BANK])
                return
            if hw in VHEAVY:
                vector_multiply_add(both[:], proj[(hw, 2)][:], both_w[:, hw, 1:2], odd[:, LEAD:LEAD + BANK] if ODDM else even[:])
            if hw not in SHEAVY:
                vector_multiply_add(both[:, 1:BANK], proj[(hw, 2)][:, 0:BANK - 1], both_w[:, hw, 0:1], both[:, 1:BANK])

        def turn_and_add(hw, only=None):
            even, odd, both, more = parts_of(hw)
            if only in (None, 0):
                conv_sum[hw] = []
            for hf in range(HALVES) if only is None else (only,):
                cv = psum_c.tile([P, TILES, HS], F32, name="cv", tag="cbank")
                conv_sum[hw].append(cv)
                for tq in range(TILES):
                    c0 = tq * P
                    here = slice(c0, c0 + P)
                    odd_now = odd[:, LEAD + c0:LEAD + c0 + P]
                    odd_before = odd[:, LEAD - 1 + c0:LEAD - 1 + c0 + P]
                    if hf == 0:
                        parts = [even[:, here], odd_before]
                    elif hw in DIRECT:
                        parts = [both[:, here], more[:, here]]
                        if MODES[hw] == "5":
                            parts.append(extra_part[hw % TAP_SETS][:, here])
                    elif hw in VHEAVY:
                        parts = [even[:, here], both[:, here]] if ODDM else [odd_now, both[:, here]]
                    else:
                        parts = [even[:, here], odd_now, both[:, here]]
                        if hw in SHEAVY:
                            parts.append(more[:, here])
                    for n, part in enumerate(parts):
                        nc.tensor.matmul(out=cv[:, tq, :], lhsT=part, rhs=ident[:], is_transpose=True, start=(n == 0), stop=(n == len(parts) - 1))

        def silu(hw, hf):
            if hf == 0:
                silu_out[hw] = outp.tile([P, TT, HS], F32, name="s", tag="s")
            tiles = slice(hf * TILES, (hf + 1) * TILES)
            nc.scalar.activation(out=silu_out[hw][:, tiles, :], in_=conv_sum[hw][hf][:], func=ACT.Silu, scale=1.0 if hf == 0 or hw in DIRECT else -1.0)
            grp, r = divmod(hw, GROUP)
            if r == GROUP - 1:
                nc.sync.dma_start(out=v_view[hf][:, :, grp, :], in_=silu_out[hw][:, tiles, :])

        def by_halves(tile):
            return tile[:].rearrange("p tt (h i) -> p tt h i", h=2)

        def for_both_halves(table):
            return table.unsqueeze(2).to_broadcast([P, TT, 2, HALF])

        def rope_product(hw, which):
            name = "rot" if which else "o"
            term = outp.tile([P, TT, HS], F32, name=name, tag=name)
            rope_terms.setdefault(hw, []).append(term)
            if which and GONE:
                s_t = silu_out[hw]
                nc.vector.scalar_tensor_tensor(out=term[:, :, 0:HALF], in0=s_t[:, :, HALF:HS], scalar=-1.0, in1=tables[:, 1, :, :], op0=ALU.mult, op1=ALU.mult)
                nc.vector.tensor_tensor(out=term[:, :, HALF:HS], in0=s_t[:, :, 0:HALF], in1=tables[:, 1, :, :], op=ALU.mult)
            else:
                nc.vector.tensor_tensor(out=by_halves(term), in0=by_halves(silu_out[hw]), in1=for_both_halves(tables[:, which, :, :]), op=ALU.mult)

        def rope_sum(hw):
            grp, r = divmod(hw, GROUP)
            if r == GROUP - 1:
                return
            by_cos, by_sin = rope_terms[hw]
            fin = outp.tile([P, TT, HS], F32, name="fin", tag="fin")
            eng = nc.vector if hw >= LAST_ROPE_HEAD else nc.gpsimd
            if GONE:
                eng.tensor_tensor(out=fin[:], in0=by_cos[:], in1=by_sin[:], op=ALU.add)
            else:
                eng.tensor_tensor(out=fin[:, :, 0:HALF], in0=by_cos[:, :, 0:HALF], in1=by_sin[:, :, HALF:HS], op=ALU.subtract)
                eng.tensor_tensor(out=fin[:, :, HALF:HS], in0=by_cos[:, :, HALF:HS], in1=by_sin[:, :, 0:HALF], op=ALU.add)
            for hf in range(HALVES):
                tiles = slice(hf * TILES, (hf + 1) * TILES)
                if r == QUERIES:
                    nc.sync.dma_start(out=k_view[hf][:, :, grp, :], in_=fin[:, tiles, :])
                else:
                    nc.sync.dma_start(out=q_view[hf][:, :, grp * QUERIES + r, :], in_=fin[:, tiles, :])

        steps = {
            "0": lambda: w_widen(0), "1": lambda: w_widen(1), "2": lambda: w_widen(2), "3": lambda: w_widen(3), "4": lambda: w_widen(4),
            "X": lambda: x_turn(0, XT0), "Y": lambda: x_turn(1, XT1), "i": lambda: w_interleave(0), "I": lambda: w_interleave(1), "j": lambda: w_interleave(2), "J": lambda: w_interleave(3),
            "q": lambda: x_quantize(0), "Q": lambda: x_quantize(1), "w": lambda: w_quantize(1),
        }
        for c in PRE:
            steps[c]()
        next_piece = {"widen": 5, "interleave": 4, "quantize": 4 if PREQ else 2}

        def advance(stage, work, upto):
            for piece in range(next_piece[stage], upto + 1):
                work(piece)
            next_piece[stage] = max(next_piece[stage], upto + 1)

        def nothing():
            return None

        next_plane = [5 * PACK]
        ropes = {}
        counts = [(2, 2, 2, 2, 2, 0), (2, 1, 2, 2, 1, 2), (2, 2, 1, 2, 1, 2), (1, 2, 2, 1, 2, 2)][RSPREAD]
        todo = []
        last = NHEADS + DS
        for i in range(last + 1):
            h = i - 2 - DS
            if 0 <= h < NHEADS and h % GROUP != GROUP - 1:
                todo += [(h, 0), (h, 1)]
            n = counts[h % GROUP] if i < NHEADS - 2 + DS else len(todo)
            ropes[i] = todo[:n]
            todo = todo[n:]
        for i in range(last + 1):
            live = i < NHEADS
            turned = i - 1 - DS

            def w_step():
                advance("quantize", w_quantize, i + QUANTIZE_AHEAD)
                advance("interleave", w_interleave, i + INTERLEAVE_AHEAD)

            special = live and MODES[i] in "D56"
            for c in (POD if special and POD else PO):
                if c in "EO" and live:
                    project_one(i, "EO".index(c))
                elif c == "S" and live and i not in DIRECT:
                    project_sum(i)
                elif c in "01" and 0 <= turned:
                    turn_and_add(turned, int(c))
            if i == TBL:
                tables_to_psum()

            def planes(k):
                if not live:
                    return
                n0 = next_plane[0]
                for n in range(n0, n0 + k):
                    w_widen(n // PACK, n % PACK)
                next_plane[0] = n0 + k

            so = SOD if special and SOD else SO
            total = max({"F": 4, "V": 6, "D": 2, "5": 2, "S": 2}[MODES[i]], PACK * (i + INTERLEAVE_AHEAD + 1) - next_plane[0]) if live else 0
            nw = so.count("W")
            done = 0
            seen = 0
            for c in so:
                if c in "EO" and live:
                    tap_on_scalar(i, "EO".index(c))
                elif c == "M" and live:
                    sum_taps_on_scalar(i)
                elif c == "W":
                    seen += 1
                    k = total * seen // nw - done
                    planes(k)
                    done += k
                elif c in "st" and 0 <= turned:
                    silu(turned, "st".index(c))
            todo_r = list(ropes[i])
            wdone = False
            vo = VOD if special and VOD else VOR
            for c in vo:
                if c == "r" and todo_r:
                    h, which = todo_r.pop(0)
                    rope_product(h, which)
                elif c == "R":
                    while todo_r:
                        h, which = todo_r.pop(0)
                        rope_product(h, which)
                elif c == "w":
                    w_step()
                elif c in "eo" and live:
                    tap_on_vector(i, "eo".index(c))
                elif c == "m" and live:
                    sum_taps_on_vector(i)
            while todo_r:
                h, which = todo_r.pop(0)
                rope_product(h, which)
            for h, which in ropes[i]:
                if which:
                    rope_sum(h)
